import numpy as np
import ml_dtypes


def mxq(x, axis, fmt="e4m3"):
    dtype, down = {"e4m3": (ml_dtypes.float8_e4m3fn, 7), "e5m2": (ml_dtypes.float8_e5m2, 14)}[fmt]
    v = np.moveaxis(np.asarray(x, np.float32).astype(ml_dtypes.bfloat16).astype(np.float64), axis, -1)
    blocks = v.reshape(v.shape[:-1] + (-1, 32))
    amax = np.abs(blocks).max(-1, keepdims=True)
    byte = np.maximum(np.where(amax > 0, np.frexp(amax)[1] - 1 + 127, 0) - down, 1)
    scale = np.exp2(byte - 127.0)
    codes = (blocks / scale).astype(np.float32).astype(dtype).astype(np.float64)
    return np.moveaxis((codes * scale).reshape(v.shape), -1, axis)


WIDE = False


def mx_kscale(k):
    if not WIDE:
        return np.ones(k)
    levels = np.array([10, -10, 5, -5, 0])
    if k % 512:
        return np.exp2(np.random.permutation(np.resize(levels, k // 32))).repeat(32)
    a = np.empty((k // 512, 16))
    for p in range(k // 512):
        a[p, :8] = np.random.permutation(np.resize(levels, 8))
        for g in range(8):
            far = levels[np.abs(levels - a[p, g]) >= 10]
            a[p, g + 8] = far[np.random.randint(len(far))]
    return np.exp2(a.ravel()).repeat(32)


BF16 = ml_dtypes.bfloat16


def bf(x):
    return np.asarray(x, np.float32).astype(BF16)


def f64(x):
    return np.asarray(x).astype(np.float64)


B, H, HD = 512, 4, 512
W = H * HD


def sigmoid(v):
    return 1.0 / (1.0 + np.exp(-v))


def softplus(v):
    return np.log(1.0 + np.exp(v))


def block_diag_linear(xq, w, b):
    y = (xq.transpose(1, 0, 2) @ mxq(f64(w), 1, "e4m3")).transpose(1, 0, 2) + f64(b)
    return y.reshape(B, W)


def setup_inputs():
    s = mx_kscale(W)
    s = s / s.max()
    sw = s.reshape(H, HD, 1)
    return {"x": bf(np.random.standard_normal((B, W)) * s),
            "state": bf(np.random.standard_normal((B, W))),
            "w_in": bf(np.random.standard_normal((H, HD, HD)) / np.sqrt(HD) / sw),
            "b_in": bf(np.random.standard_normal((H, HD)) * 0.5),
            "w_a": bf(np.random.standard_normal((H, HD, HD)) / np.sqrt(HD) / sw),
            "b_a": bf(np.random.standard_normal((H, HD)) * 0.5),
            "a_param": bf(-2.0 + 0.5 * np.random.standard_normal(W))}


def core(x, state, w_in, b_in, w_a, b_a, a_param):
    xq = mxq(f64(x).reshape(B, H, HD), 2, "e4m3")
    gate_x = sigmoid(block_diag_linear(xq, w_in, b_in))
    gate_a = sigmoid(block_diag_linear(xq, w_a, b_a))
    log_a = -8.0 * gate_a * softplus(f64(a_param))
    a = np.exp(log_a)
    scale = np.sqrt(1.0 - np.exp(2.0 * log_a))
    return a * f64(state) + gate_x * f64(x) * scale


def e4m3fn_bytes(y):
    return np.clip(np.asarray(y, np.float64), -448.0, 448.0).astype(np.float32).astype(ml_dtypes.float8_e4m3fn).view(np.uint8)


Y_SCALE = 280.0


def reference(x, state, w_in, b_in, w_a, b_a, a_param):
    out = core(x, state, w_in, b_in, w_a, b_a, a_param)
    return out, e4m3fn_bytes(out * Y_SCALE)

@@ -1,0 +1,235 @@
+from contextlib import ExitStack
+
+import concourse.mybir as mybir
+from concourse.masks import make_identity
+
+B, H, HD = 512, 4, 512
+W = H * HD
+FLOPS = 2 * 2 * B * H * HD * HD
+
+F32 = mybir.dt.float32
+BF16 = mybir.dt.bfloat16
+U32 = mybir.dt.uint32
+U8 = mybir.dt.uint8
+FP8X4 = mybir.dt.float8_e4m3fn_x4
+FP8 = mybir.dt.float8_e4m3fn
+ACT = mybir.ActivationFunctionType
+ALU = mybir.AluOpType
+
+P = 128
+NT = 4
+NA = 4
+Y_SCALE = 280.0
+
+GROUPS = ((0, 1), (2, 3))
+XEVAC = ("V", "S", "S", "S")
+WINT = (("V", "V"), ("V", "V"), ("V", "V"), ("V", "V"))
+
+
+def tile_rglru_kernel(tc, x, state, w_in, b_in, w_a, b_a, a_param, out_0, out_1):
+    nc = tc.nc
+    w_dram = (w_in, w_a)
+
+    with ExitStack() as ctx:
+        const = ctx.enter_context(tc.tile_pool(name="const", bufs=1))
+        xin = ctx.enter_context(tc.tile_pool(name="xin", bufs=2))
+        win = ctx.enter_context(tc.tile_pool(name="win", bufs=4))
+        wgp = ctx.enter_context(tc.tile_pool(name="wgp", bufs=2))
+        keep = ctx.enter_context(tc.tile_pool(name="keep", bufs=1))
+        sqp = ctx.enter_context(tc.tile_pool(name="sqp", bufs=4))
+        f8p = ctx.enter_context(tc.tile_pool(name="f8p", bufs=4))
+        pmx = ctx.enter_context(tc.psum_pool(name="pmx", bufs=2))
+        ptr = ctx.enter_context(tc.psum_pool(name="ptr", bufs=4))
+        ctx.enter_context(tc.manual_schedule(engines={mybir.EngineType.Activation}))
+
+        warm = const.tile([P, 1], F32, name="warm")
+        nc.vector.memset(warm[:], 0.0)
+        one = const.tile([P, 1], F32, name="one")
+        nc.vector.memset(one[:], 1.0)
+        quarter = const.tile([P, 1], F32, name="quarter")
+        nc.vector.memset(quarter[:], 0.25)
+        warm2 = const.tile([P, 1], F32, name="warm2")
+        nc.scalar.activation(out=warm2[:], in_=warm[:], func=ACT.Exp)
+
+        vecs = const.tile([P, 3, H * NT], BF16, name="vecs")
+        with nc.allow_non_contiguous_dma(reason="three small per-channel vectors, 8-byte runs"):
+            nc.scalar.dma_start(
+                out=vecs[:, 2, :].rearrange("p (h t) -> p h t", t=NT),
+                in_=a_param.rearrange("(h p t) -> p h t", h=H, t=NT),
+            )
+            nc.scalar.dma_start(
+                out=vecs[:, 0, :].rearrange("p (h t) -> p h t", t=NT),
+                in_=b_in.rearrange("h (p t) -> p h t", t=NT),
+            )
+            nc.scalar.dma_start(
+                out=vecs[:, 1, :].rearrange("p (h t) -> p h t", t=NT),
+                in_=b_a.rearrange("h (p t) -> p h t", t=NT),
+            )
+
+        ident = const.tile([P, P], F32, name="ident")
+        make_identity(nc, ident[:])
+
+        xn = [None] * H
+        raw = [[None, None] for h in range(H)]
+        st = [None] * H
+
+        def load_x(h):
+            xn[h] = xin.tile([P, NA, HD], BF16, tag="xn", name="xn%d" % h)
+            src = x[:, h * HD:(h + 1) * HD].rearrange("(a p) c -> p a c", p=P)
+            if h == 0:
+                nc.sync.dma_start(out=xn[h][:, 0:2, :], in_=src[:, 0:2, :])
+                nc.sync.dma_start(out=xn[h][:, 2:4, :], in_=src[:, 2:4, :])
+            else:
+                nc.sync.dma_start(out=xn[h][:], in_=src)
+
+        def load_w(h, g):
+            raw[h][g] = win.tile([P, 4, HD], BF16, tag="raw", name="raw%d_%d" % (h, g))
+            nc.sync.dma_start(out=raw[h][g][:], in_=w_dram[g][h].rearrange("(p j) n -> p j n", j=4))
+
+        def load_st(h):
+            st[h] = keep.tile([P, NA, HD], BF16, name="st%d" % h)
+            nc.sync.dma_start(
+                out=st[h][:], in_=state[:, h * HD:(h + 1) * HD].rearrange("(a p) c -> p a c", p=P)
+            )
+
+        for h in range(H):
+            load_x(h)
+            load_w(h, 0)
+            load_w(h, 1)
+            if h >= 1:
+                load_st(h - 1)
+        load_st(H - 1)
+
+        v = vecs[:, 2, :]
+        av = const.tile([P, H * NT], F32, name="av")
+        nc.vector.scalar_tensor_tensor(out=av[:], in0=v, scalar=-1.0, in1=v, op0=ALU.mult, op1=ALU.max)
+        ex = const.tile([P, H * NT], F32, name="ex")
+        nc.scalar.activation(out=ex[:], in_=av[:], func=ACT.Exp, scale=-1.0)
+        ln = const.tile([P, H * NT], F32, name="ln")
+        nc.scalar.activation(out=ln[:], in_=ex[:], func=ACT.Ln, bias=one[:, 0:1], scale=1.0)
+        sp = const.tile([P, H * NT], F32, name="sp")
+        nc.vector.scalar_tensor_tensor(out=sp[:], in0=v, scalar=0.0, in1=ln[:], op0=ALU.max, op1=ALU.add)
+        ch = const.tile([P, H * NT], F32, name="ch")
+        nc.vector.tensor_scalar(out=ch[:], in0=sp[:], scalar1=-4.0, scalar2=None, op0=ALU.mult)
+        hb = const.tile([P, 2, H * NT], F32, name="hb")
+        nc.vector.tensor_scalar(out=hb[:], in0=vecs[:, 0:2, :], scalar1=0.5, scalar2=None, op0=ALU.mult)
+
+        xg = [keep.tile([P, 4 * B], BF16, name="xg%d" % h, align_bytes=64) for h in range(H)]
+        xc = [keep.tile([P, B], U32, name="xc%d" % h, align_bytes=64) for h in range(H)]
+        xs = [keep.tile([P, B], U8, name="xs%d" % h, align_bytes=64) for h in range(H)]
+        wc = [[keep.tile([P, HD], U32, name="wc%d_%d" % (h, g), align_bytes=64) for g in range(2)] for h in range(H)]
+        ws = [[keep.tile([P, HD], U8, name="ws%d_%d" % (h, g), align_bytes=64) for g in range(2)] for h in range(H)]
+        gx = [keep.tile([P, NT, B], F32, name="gx%d" % h) for h in range(H)]
+        ae = [keep.tile([P, NT, B], F32, name="ae%d" % h) for h in range(H)]
+        t1 = [[keep.tile([P, HD], F32, name="t1_%d_%d" % (h, a)) for a in range(NA)] for h in range(H)]
+
+        def prep(h):
+            xgw = xg[h][:].bitcast(F32).rearrange("p (a r u) -> p a r u", a=NA, u=2)
+            for half in range(2):
+                xt = ptr.tile([P, 2, 2, P], F32, tag="tr", name="xt%d_%d" % (h, half))
+                for a in range(2):
+                    words = xn[h][:, 2 * half + a, :].bitcast(F32)
+                    for u in range(2):
+                        nc.tensor.transpose(xt[:, a, u, :], words[:, u:HD // 2:2], ident[:])
+                dst = xgw[:, 2 * half:2 * half + 2, :, :]
+                src = xt[:].rearrange("p a u r -> p a r u")
+                if XEVAC[h] == "V":
+                    nc.vector.tensor_copy(out=dst, in_=src)
+                else:
+                    nc.scalar.copy(out=dst, in_=src)
+            wgs = []
+            for g in range(2):
+                wg = wgp.tile([P, 4 * HD], BF16, tag="wg", name="wg%d_%d" % (h, g), align_bytes=64)
+                dst = wg[:].rearrange("p (t m j) -> p t m j", t=NT, j=4)
+                src = raw[h][g][:].rearrange("p j (m t) -> p t m j", t=NT)
+                if WINT[h][g] == "V":
+                    nc.vector.tensor_copy(out=dst, in_=src)
+                elif WINT[h][g] == "S":
+                    nc.scalar.copy(out=dst, in_=src)
+                else:
+                    nc.gpsimd.tensor_scalar(out=dst, in0=src, scalar1=1.0, scalar2=0.0, op0=ALU.mult, op1=ALU.add)
+                wgs.append(wg)
+            nc.vector.quantize_mx(out=xc[h][:].bitcast(FP8X4), scales=xs[h][:], in_=xg[h][:])
+            for g in range(2):
+                nc.vector.quantize_mx(out=wc[h][g][:].bitcast(FP8X4), scales=ws[h][g][:], in_=wgs[g][:])
+
+        acc = {}
+
+        def issue_mx(c):
+            h, t = c // NT, c % NT
+            cols = slice(t * P, (t + 1) * P)
+            pair = []
+            for g in range(2):
+                ps = pmx.tile([P, B], F32, tag="ps%d" % g, name="ps%d_%d" % (g, c))
+                nc.tensor.matmul_mx(
+                    out=ps[:],
+                    lhsT=wc[h][g][:, cols].bitcast(FP8X4),
+                    lhsT_scale=ws[h][g][:, cols],
+                    rhs=xc[h][:].bitcast(FP8X4),
+                    rhs_scale=xs[h][:],
+                    start=True,
+                    stop=True,
+                )
+                pair.append(ps)
+            acc[c] = pair
+
+        def gates(c):
+            h, t = c // NT, c % NT
+            nc.scalar.activation(out=gx[h][:, t, :], in_=acc[c][0][:], func=ACT.Tanh, bias=hb[:, 0, c:c + 1], scale=0.5)
+            nc.scalar.activation(out=ae[h][:, t, :], in_=acc[c][1][:], func=ACT.Tanh, bias=hb[:, 1, c:c + 1], scale=0.5)
+            if c + 2 < H * NT:
+                issue_mx(c + 2)
+            nc.scalar.activation(out=ae[h][:, t, :], in_=ae[h][:, t, :], func=ACT.Exp, bias=ch[:, c:c + 1], scale=ch[:, c:c + 1])
+            nc.vector.scalar_tensor_tensor(
+                out=gx[h][:, t, :], in0=gx[h][:, t, :], scalar=1.0,
+                in1=xg[h][:].rearrange("p (r t) -> p t r", t=NT)[:, t, :],
+                op0=ALU.add, op1=ALU.mult,
+            )
+
+        def carry(h):
+            for a in range(NA):
+                tr = ptr.tile([P, NT, P], F32, tag="tr", name="at%d_%d" % (h, a))
+                for t in range(NT):
+                    nc.tensor.transpose(tr[:, t, :], ae[h][:, t, a * P:(a + 1) * P], ident[:])
+                nc.vector.tensor_tensor(
+                    out=t1[h][a][:].rearrange("p (m t) -> p m t", t=NT),
+                    in0=tr[:].rearrange("p t m -> p m t"),
+                    in1=st[h][:, a, :].rearrange("p (m t) -> p m t", t=NT),
+                    op=ALU.mult,
+                )
+
+        def finish(h, a):
+            blk = slice(a * P, (a + 1) * P)
+            sq = sqp.tile([P, NT, P], F32, tag="sq", name="sq%d_%d" % (h, a))
+            nc.scalar.activation(out=sq[:], in_=ae[h][:, :, blk], func=ACT.Square)
+            nc.scalar.activation(out=sq[:], in_=sq[:], func=ACT.Sqrt, bias=quarter[:, 0:1], scale=-0.25)
+            nc.vector.tensor_tensor(out=sq[:], in0=gx[h][:, :, blk], in1=sq[:], op=ALU.mult)
+            tr = ptr.tile([P, NT, P], F32, tag="tr", name="ot%d_%d" % (h, a))
+            for t in range(NT):
+                nc.tensor.transpose(tr[:, t, :], sq[:, t, :], ident[:])
+            nc.vector.tensor_tensor(
+                out=t1[h][a][:].rearrange("p (m t) -> p m t", t=NT),
+                in0=tr[:].rearrange("p t m -> p m t"),
+                in1=t1[h][a][:].rearrange("p (m t) -> p m t", t=NT),
+                op=ALU.add,
+            )
+            f8 = f8p.tile([P, HD], FP8, tag="f8", name="f8_%d_%d" % (h, a))
+            nc.vector.tensor_scalar(out=f8[:], in0=t1[h][a][:], scalar1=Y_SCALE, scalar2=None, op0=ALU.mult, saturate=False)
+            rows = slice(a * P, (a + 1) * P)
+            cols = slice(h * HD, (h + 1) * HD)
+            nc.sync.dma_start(out=out_0[rows, cols], in_=t1[h][a][:])
+            nc.sync.dma_start(out=out_1[rows, cols], in_=f8[:].bitcast(U8))
+
+        prep(0)
+        issue_mx(0)
+        issue_mx(1)
+        for group in GROUPS:
+            for h in group:
+                for t in range(NT):
+                    gates(h * NT + t)
+                    if t == 0 and h + 1 < H:
+                        prep(h + 1)
+                carry(h)
+            for h in group:
+                for a in range(NA):
+                    finish(h, a)

@@ -21,9 +21,9 @@ NT = 4
 NA = 4
 Y_SCALE = 280.0
 
-GROUPS = ((0, 1), (2, 3))
 XEVAC = ("V", "S", "S", "S")
-WINT = (("V", "V"), ("V", "V"), ("V", "V"), ("V", "V"))
+CAST_ON_ACT = ()
+CAST_LAG_ACT = 6
 
 
 def tile_rglru_kernel(tc, x, state, w_in, b_in, w_a, b_a, a_param, out_0, out_1):
@@ -32,15 +32,15 @@ def tile_rglru_kernel(tc, x, state, w_in, b_in, w_a, b_a, a_param, out_0, out_1)
 
     with ExitStack() as ctx:
         const = ctx.enter_context(tc.tile_pool(name="const", bufs=1))
-        xin = ctx.enter_context(tc.tile_pool(name="xin", bufs=2))
+        xin = ctx.enter_context(tc.tile_pool(name="xin", bufs=3))
         win = ctx.enter_context(tc.tile_pool(name="win", bufs=4))
-        wgp = ctx.enter_context(tc.tile_pool(name="wgp", bufs=2))
+        wgp = ctx.enter_context(tc.tile_pool(name="wgp", bufs=4))
         keep = ctx.enter_context(tc.tile_pool(name="keep", bufs=1))
-        sqp = ctx.enter_context(tc.tile_pool(name="sqp", bufs=4))
+        sqp = ctx.enter_context(tc.tile_pool(name="sqp", bufs=6))
         f8p = ctx.enter_context(tc.tile_pool(name="f8p", bufs=4))
         pmx = ctx.enter_context(tc.psum_pool(name="pmx", bufs=2))
         ptr = ctx.enter_context(tc.psum_pool(name="ptr", bufs=4))
-        ctx.enter_context(tc.manual_schedule(engines={mybir.EngineType.Activation}))
+        ctx.enter_context(tc.manual_schedule())
 
         warm = const.tile([P, 1], F32, name="warm")
         nc.vector.memset(warm[:], 0.0)
@@ -103,16 +103,18 @@ def tile_rglru_kernel(tc, x, state, w_in, b_in, w_a, b_a, a_param, out_0, out_1)
         v = vecs[:, 2, :]
         av = const.tile([P, H * NT], F32, name="av")
         nc.vector.scalar_tensor_tensor(out=av[:], in0=v, scalar=-1.0, in1=v, op0=ALU.mult, op1=ALU.max)
-        ex = const.tile([P, H * NT], F32, name="ex")
-        nc.scalar.activation(out=ex[:], in_=av[:], func=ACT.Exp, scale=-1.0)
+        ex_t = const.tile([P, H * NT], F32, name="ex_t")
+        nc.scalar.activation(out=ex_t[:], in_=av[:], func=ACT.Exp, scale=-1.0)
         ln = const.tile([P, H * NT], F32, name="ln")
-        nc.scalar.activation(out=ln[:], in_=ex[:], func=ACT.Ln, bias=one[:, 0:1], scale=1.0)
-        sp = const.tile([P, H * NT], F32, name="sp")
-        nc.vector.scalar_tensor_tensor(out=sp[:], in0=v, scalar=0.0, in1=ln[:], op0=ALU.max, op1=ALU.add)
-        ch = const.tile([P, H * NT], F32, name="ch")
-        nc.vector.tensor_scalar(out=ch[:], in0=sp[:], scalar1=-4.0, scalar2=None, op0=ALU.mult)
+        nc.scalar.activation(out=ln[:], in_=ex_t[:], func=ACT.Ln, bias=one[:, 0:1], scale=1.0)
         hb = const.tile([P, 2, H * NT], F32, name="hb")
         nc.vector.tensor_scalar(out=hb[:], in0=vecs[:, 0:2, :], scalar1=0.5, scalar2=None, op0=ALU.mult)
+        sp = const.tile([P, H * NT], F32, name="sp")
+        ch = const.tile([P, H * NT], F32, name="ch")
+
+        def softplus_tail():
+            nc.vector.scalar_tensor_tensor(out=sp[:], in0=v, scalar=0.0, in1=ln[:], op0=ALU.max, op1=ALU.add)
+            nc.vector.tensor_scalar(out=ch[:], in0=sp[:], scalar1=-4.0, scalar2=None, op0=ALU.mult)
 
         xg = [keep.tile([P, 4 * B], BF16, name="xg%d" % h, align_bytes=64) for h in range(H)]
         xc = [keep.tile([P, B], U32, name="xc%d" % h, align_bytes=64) for h in range(H)]
@@ -121,41 +123,62 @@ def tile_rglru_kernel(tc, x, state, w_in, b_in, w_a, b_a, a_param, out_0, out_1)
         ws = [[keep.tile([P, HD], U8, name="ws%d_%d" % (h, g), align_bytes=64) for g in range(2)] for h in range(H)]
         gx = [keep.tile([P, NT, B], F32, name="gx%d" % h) for h in range(H)]
         ae = [keep.tile([P, NT, B], F32, name="ae%d" % h) for h in range(H)]
-        t1 = [[keep.tile([P, HD], F32, name="t1_%d_%d" % (h, a)) for a in range(NA)] for h in range(H)]
+        t1t = [keep.tile([P, HD], F32, name="t1_%d" % u) for u in range(H * NA)]
 
-        def prep(h):
-            xgw = xg[h][:].bitcast(F32).rearrange("p (a r u) -> p a r u", a=NA, u=2)
-            for half in range(2):
-                xt = ptr.tile([P, 2, 2, P], F32, tag="tr", name="xt%d_%d" % (h, half))
-                for a in range(2):
-                    words = xn[h][:, 2 * half + a, :].bitcast(F32)
-                    for u in range(2):
-                        nc.tensor.transpose(xt[:, a, u, :], words[:, u:HD // 2:2], ident[:])
-                dst = xgw[:, 2 * half:2 * half + 2, :, :]
-                src = xt[:].rearrange("p a u r -> p a r u")
-                if XEVAC[h] == "V":
-                    nc.vector.tensor_copy(out=dst, in_=src)
-                else:
-                    nc.scalar.copy(out=dst, in_=src)
-            wgs = []
-            for g in range(2):
-                wg = wgp.tile([P, 4 * HD], BF16, tag="wg", name="wg%d_%d" % (h, g), align_bytes=64)
-                dst = wg[:].rearrange("p (t m j) -> p t m j", t=NT, j=4)
-                src = raw[h][g][:].rearrange("p j (m t) -> p t m j", t=NT)
-                if WINT[h][g] == "V":
-                    nc.vector.tensor_copy(out=dst, in_=src)
-                elif WINT[h][g] == "S":
-                    nc.scalar.copy(out=dst, in_=src)
-                else:
-                    nc.gpsimd.tensor_scalar(out=dst, in0=src, scalar1=1.0, scalar2=0.0, op0=ALU.mult, op1=ALU.add)
-                wgs.append(wg)
-            nc.vector.quantize_mx(out=xc[h][:].bitcast(FP8X4), scales=xs[h][:], in_=xg[h][:])
-            for g in range(2):
-                nc.vector.quantize_mx(out=wc[h][g][:].bitcast(FP8X4), scales=ws[h][g][:], in_=wgs[g][:])
-
+        xts = {}
+        wgs = {}
         acc = {}
+        ats = {}
+        sqs = {}
+        ots = {}
 
-        def issue_mx(c):
+        def x_t(h, half):
+            xt = ptr.tile([P, 2, 2, P], F32, tag="tr", name="xt%d_%d" % (h, half))
+            xts[(h, half)] = xt
+            for a in range(2):
+                words = xn[h][:, 2 * half + a, :].bitcast(F32)
+                for u in range(2):
+                    nc.tensor.transpose(xt[:, a, u, :], words[:, u:HD // 2:2], ident[:])
+
+        def xev(h, half):
+            xgw = xg[h][:].bitcast(F32).rearrange("p (a r u) -> p a r u", a=NA, u=2)
+            dst = xgw[:, 2 * half:2 * half + 2, :, :]
+            src = xts[(h, half)][:].rearrange("p a u r -> p a r u")
+            if XEVAC[h] == "V":
+                nc.vector.tensor_copy(out=dst, in_=src)
+            else:
+                nc.scalar.copy(out=dst, in_=src)
+
+        def xq(h):
+            nc.vector.quantize_mx(out=xc[h][:].bitcast(FP8X4), scales=xs[h][:], in_=xg[h][:])
+
+        def new_wg(h, g):
+            wgs[(h, g)] = wgp.tile([P, 4 * HD], BF16, tag="wg", name="wg%d_%d" % (h, g), align_bytes=64)
+
+        def wint(h, g):
+            new_wg(h, g)
+            dst = wgs[(h, g)][:].rearrange("p (t m j) -> p t m j", t=NT, j=4)
+            src = raw[h][g][:].rearrange("p j (m t) -> p t m j", t=NT)
+            nc.vector.tensor_copy(out=dst, in_=src)
+
+        def wq(h, g):
+            nc.vector.quantize_mx(out=wc[h][g][:].bitcast(FP8X4), scales=ws[h][g][:], in_=wgs[(h, g)][:])
+
+        def wintq(h, g, t):
+            if t == 0:
+                new_wg(h, g)
+            dst = wgs[(h, g)][:, t * HD:(t + 1) * HD].rearrange("p (m j) -> p m j", j=4)
+            src = raw[h][g][:].rearrange("p j (m t) -> p t m j", t=NT)[:, t, :, :]
+            nc.vector.tensor_copy(out=dst, in_=src)
+
+        def wqq(h, g, t):
+            cols = slice(t * P, (t + 1) * P)
+            nc.vector.quantize_mx(
+                out=wc[h][g][:, cols].bitcast(FP8X4), scales=ws[h][g][:, cols],
+                in_=wgs[(h, g)][:, t * HD:(t + 1) * HD],
+            )
+
+        def mx(c):
             h, t = c // NT, c % NT
             cols = slice(t * P, (t + 1) * P)
             pair = []
@@ -173,63 +196,181 @@ def tile_rglru_kernel(tc, x, state, w_in, b_in, w_a, b_a, a_param, out_0, out_1)
                 pair.append(ps)
             acc[c] = pair
 
-        def gates(c):
+        def thx(c):
             h, t = c // NT, c % NT
             nc.scalar.activation(out=gx[h][:, t, :], in_=acc[c][0][:], func=ACT.Tanh, bias=hb[:, 0, c:c + 1], scale=0.5)
+
+        def tha(c):
+            h, t = c // NT, c % NT
             nc.scalar.activation(out=ae[h][:, t, :], in_=acc[c][1][:], func=ACT.Tanh, bias=hb[:, 1, c:c + 1], scale=0.5)
-            if c + 2 < H * NT:
-                issue_mx(c + 2)
+
+        def ex(c):
+            h, t = c // NT, c % NT
             nc.scalar.activation(out=ae[h][:, t, :], in_=ae[h][:, t, :], func=ACT.Exp, bias=ch[:, c:c + 1], scale=ch[:, c:c + 1])
+
+        def gxx(c):
+            h, t = c // NT, c % NT
             nc.vector.scalar_tensor_tensor(
                 out=gx[h][:, t, :], in0=gx[h][:, t, :], scalar=1.0,
                 in1=xg[h][:].rearrange("p (r t) -> p t r", t=NT)[:, t, :],
                 op0=ALU.add, op1=ALU.mult,
             )
 
-        def carry(h):
-            for a in range(NA):
-                tr = ptr.tile([P, NT, P], F32, tag="tr", name="at%d_%d" % (h, a))
-                for t in range(NT):
-                    nc.tensor.transpose(tr[:, t, :], ae[h][:, t, a * P:(a + 1) * P], ident[:])
-                nc.vector.tensor_tensor(
-                    out=t1[h][a][:].rearrange("p (m t) -> p m t", t=NT),
-                    in0=tr[:].rearrange("p t m -> p m t"),
-                    in1=st[h][:, a, :].rearrange("p (m t) -> p m t", t=NT),
-                    op=ALU.mult,
-                )
-
-        def finish(h, a):
-            blk = slice(a * P, (a + 1) * P)
-            sq = sqp.tile([P, NT, P], F32, tag="sq", name="sq%d_%d" % (h, a))
-            nc.scalar.activation(out=sq[:], in_=ae[h][:, :, blk], func=ACT.Square)
-            nc.scalar.activation(out=sq[:], in_=sq[:], func=ACT.Sqrt, bias=quarter[:, 0:1], scale=-0.25)
-            nc.vector.tensor_tensor(out=sq[:], in0=gx[h][:, :, blk], in1=sq[:], op=ALU.mult)
-            tr = ptr.tile([P, NT, P], F32, tag="tr", name="ot%d_%d" % (h, a))
+        def a_t(u):
+            h, a = u // NA, u % NA
+            tr = ptr.tile([P, NT, P], F32, tag="tr", name="at%d" % u)
+            ats[u] = tr
             for t in range(NT):
-                nc.tensor.transpose(tr[:, t, :], sq[:, t, :], ident[:])
+                nc.tensor.transpose(tr[:, t, :], ae[h][:, t, a * P:(a + 1) * P], ident[:])
+
+        def t1(u):
+            h, a = u // NA, u % NA
             nc.vector.tensor_tensor(
-                out=t1[h][a][:].rearrange("p (m t) -> p m t", t=NT),
-                in0=tr[:].rearrange("p t m -> p m t"),
-                in1=t1[h][a][:].rearrange("p (m t) -> p m t", t=NT),
+                out=t1t[u][:].rearrange("p (m t) -> p m t", t=NT),
+                in0=ats[u][:].rearrange("p t m -> p m t"),
+                in1=st[h][:, a, :].rearrange("p (m t) -> p m t", t=NT),
+                op=ALU.mult,
+            )
+
+        def sqr(u):
+            h, a = u // NA, u % NA
+            sqs[u] = sqp.tile([P, NT, P], F32, tag="sq", name="sq%d" % u)
+            nc.scalar.activation(out=sqs[u][:], in_=ae[h][:, :, a * P:(a + 1) * P], func=ACT.Square)
+
+        def sqrt(u):
+            nc.scalar.activation(out=sqs[u][:], in_=sqs[u][:], func=ACT.Sqrt, bias=quarter[:, 0:1], scale=-0.25)
+
+        def t3c(u):
+            h, a = u // NA, u % NA
+            nc.vector.tensor_tensor(out=sqs[u][:], in0=gx[h][:, :, a * P:(a + 1) * P], in1=sqs[u][:], op=ALU.mult)
+
+        def o_t(u):
+            tr = ptr.tile([P, NT, P], F32, tag="tr", name="ot%d" % u)
+            ots[u] = tr
+            for t in range(NT):
+                nc.tensor.transpose(tr[:, t, :], sqs[u][:, t, :], ident[:])
+
+        def add(u):
+            h, a = u // NA, u % NA
+            nc.vector.tensor_tensor(
+                out=t1t[u][:].rearrange("p (m t) -> p m t", t=NT),
+                in0=ots[u][:].rearrange("p t m -> p m t"),
+                in1=t1t[u][:].rearrange("p (m t) -> p m t", t=NT),
                 op=ALU.add,
             )
-            f8 = f8p.tile([P, HD], FP8, tag="f8", name="f8_%d_%d" % (h, a))
-            nc.vector.tensor_scalar(out=f8[:], in0=t1[h][a][:], scalar1=Y_SCALE, scalar2=None, op0=ALU.mult, saturate=False)
-            rows = slice(a * P, (a + 1) * P)
-            cols = slice(h * HD, (h + 1) * HD)
-            nc.sync.dma_start(out=out_0[rows, cols], in_=t1[h][a][:])
-            nc.sync.dma_start(out=out_1[rows, cols], in_=f8[:].bitcast(U8))
+            nc.sync.dma_start(out=out_0[a * P:(a + 1) * P, h * HD:(h + 1) * HD], in_=t1t[u][:])
 
-        prep(0)
-        issue_mx(0)
-        issue_mx(1)
-        for group in GROUPS:
-            for h in group:
-                for t in range(NT):
-                    gates(h * NT + t)
-                    if t == 0 and h + 1 < H:
-                        prep(h + 1)
-                carry(h)
-            for h in group:
-                for a in range(NA):
-                    finish(h, a)
+        def cast(u):
+            h, a = u // NA, u % NA
+            f8 = f8p.tile([P, HD], FP8, tag="f8", name="f8_%d" % u)
+            if u in CAST_ON_ACT:
+                nc.scalar.activation(out=f8[:], in_=t1t[u][:], func=ACT.Copy, scale=Y_SCALE, saturate=False)
+            else:
+                nc.vector.tensor_scalar(out=f8[:], in0=t1t[u][:], scalar1=Y_SCALE, scalar2=None, op0=ALU.mult, saturate=False)
+            nc.sync.dma_start(out=out_1[a * P:(a + 1) * P, h * HD:(h + 1) * HD], in_=f8[:].bitcast(U8))
+
+        x_t(0, 0)
+        x_t(0, 1)
+        xev(0, 0)
+        xev(0, 1)
+        wintq(0, 0, 0)
+        xq(0)
+        wqq(0, 0, 0)
+        wintq(0, 1, 0)
+        wintq(0, 0, 1)
+        wqq(0, 1, 0)
+        softplus_tail()
+        wintq(0, 1, 1)
+        wqq(0, 0, 1)
+        wqq(0, 1, 1)
+        mx(0)
+        mx(1)
+        x_t(1, 0)
+        x_t(1, 1)
+
+        atq = []
+        t1q = []
+        gq = []
+        for c in range(H * NT):
+            h, t = c // NT, c % NT
+            hn = h + 1
+            tha(c)
+            thx(c)
+            ex(c)
+            if hn < H and t == 0 and XEVAC[hn] == "S":
+                xev(hn, 0)
+                xev(hn, 1)
+            if t1q:
+                t1(t1q.pop(0))
+            if hn < H and t == 0:
+                wint(hn, 0)
+                wint(hn, 1)
+            if h == 0 and t < 2:
+                wintq(0, 0, t + 2)
+                wintq(0, 1, t + 2)
+            if gq:
+                gxx(gq.pop(0))
+            gq.append(c)
+            if h == 0 and t < 2:
+                wqq(0, 0, t + 2)
+                wqq(0, 1, t + 2)
+            if hn < H and t == 0 and XEVAC[hn] == "V":
+                xev(hn, 0)
+                xev(hn, 1)
+            if hn < H and t == 1:
+                wq(hn, 0)
+                wq(hn, 1)
+                xq(hn)
+            if c + 2 < H * NT:
+                mx(c + 2)
+            if atq:
+                u = atq.pop(0)
+                a_t(u)
+                t1q.append(u)
+            if t == NT - 1 and h + 2 < H:
+                x_t(h + 2, 0)
+                x_t(h + 2, 1)
+            if t == NT - 1:
+                atq.extend([h * NA + a for a in range(NA)])
+
+        mq = []
+        oq = []
+        aq = []
+        kq = []
+        kaq = []
+        sqr(0)
+        s = 0
+        while s < H * NA or mq or oq or aq or kq or kaq:
+            if s + 1 < H * NA:
+                sqr(s + 1)
+            if s < H * NA:
+                sqrt(s)
+                mq.append(s)
+            if kaq and (kaq[0] <= s - CAST_LAG_ACT or s >= H * NA):
+                cast(kaq.pop(0))
+            if t1q:
+                t1(t1q.pop(0))
+            while gq:
+                gxx(gq.pop(0))
+            if aq and aq[0] <= s - 3:
+                u = aq.pop(0)
+                add(u)
+                if u in CAST_ON_ACT:
+                    kaq.append(u)
+                else:
+                    kq.append(u)
+            if mq and mq[0] <= s - 1:
+                u = mq.pop(0)
+                t3c(u)
+                oq.append(u)
+            if kq and kq[0] <= s - 4:
+                cast(kq.pop(0))
+            if atq:
+                u = atq.pop(0)
+                a_t(u)
+                t1q.append(u)
+            if oq and oq[0] <= s - 2:
+                u = oq.pop(0)
+                o_t(u)
+                aq.append(u)
+            s += 1

@@ -22,7 +22,8 @@ NA = 4
 Y_SCALE = 280.0
 
 XEVAC = ("V", "S", "S", "S")
-CAST_ON_ACT = ()
+UNITS = ((0, 0, 1), (0, 1, 1), (0, 2, 2), (1, 0, 2), (1, 2, 2), (2, 0, 2), (2, 2, 2), (3, 0, 2), (3, 2, 1), (3, 3, 1))
+CAST_ON_ACT = (1, 3, 5, 7, 9)
 CAST_LAG_ACT = 6
 
 
@@ -36,8 +37,8 @@ def tile_rglru_kernel(tc, x, state, w_in, b_in, w_a, b_a, a_param, out_0, out_1)
         win = ctx.enter_context(tc.tile_pool(name="win", bufs=4))
         wgp = ctx.enter_context(tc.tile_pool(name="wgp", bufs=4))
         keep = ctx.enter_context(tc.tile_pool(name="keep", bufs=1))
-        sqp = ctx.enter_context(tc.tile_pool(name="sqp", bufs=6))
-        f8p = ctx.enter_context(tc.tile_pool(name="f8p", bufs=4))
+        sqp = ctx.enter_context(tc.tile_pool(name="sqp", bufs=3))
+        f8p = ctx.enter_context(tc.tile_pool(name="f8p", bufs=3))
         pmx = ctx.enter_context(tc.psum_pool(name="pmx", bufs=2))
         ptr = ctx.enter_context(tc.psum_pool(name="ptr", bufs=4))
         ctx.enter_context(tc.manual_schedule())
@@ -48,9 +49,6 @@ def tile_rglru_kernel(tc, x, state, w_in, b_in, w_a, b_a, a_param, out_0, out_1)
         nc.vector.memset(one[:], 1.0)
         quarter = const.tile([P, 1], F32, name="quarter")
         nc.vector.memset(quarter[:], 0.25)
-        warm2 = const.tile([P, 1], F32, name="warm2")
-        nc.scalar.activation(out=warm2[:], in_=warm[:], func=ACT.Exp)
-
         vecs = const.tile([P, 3, H * NT], BF16, name="vecs")
         with nc.allow_non_contiguous_dma(reason="three small per-channel vectors, 8-byte runs"):
             nc.scalar.dma_start(
@@ -65,6 +63,9 @@ def tile_rglru_kernel(tc, x, state, w_in, b_in, w_a, b_a, a_param, out_0, out_1)
                 out=vecs[:, 1, :].rearrange("p (h t) -> p h t", t=NT),
                 in_=b_a.rearrange("h (p t) -> p h t", t=NT),
             )
+
+        warm2 = const.tile([P, 1], F32, name="warm2")
+        nc.scalar.activation(out=warm2[:], in_=warm[:], func=ACT.Exp)
 
         ident = const.tile([P, P], F32, name="ident")
         make_identity(nc, ident[:])
@@ -123,7 +124,11 @@ def tile_rglru_kernel(tc, x, state, w_in, b_in, w_a, b_a, a_param, out_0, out_1)
         ws = [[keep.tile([P, HD], U8, name="ws%d_%d" % (h, g), align_bytes=64) for g in range(2)] for h in range(H)]
         gx = [keep.tile([P, NT, B], F32, name="gx%d" % h) for h in range(H)]
         ae = [keep.tile([P, NT, B], F32, name="ae%d" % h) for h in range(H)]
-        t1t = [keep.tile([P, HD], F32, name="t1_%d" % u) for u in range(H * NA)]
+        t1u = [keep.tile([P, k, HD], F32, name="t1_%d" % j) for j, (h, a0, k) in enumerate(UNITS)]
+        unit_of = {}
+        for j, (h, a0, k) in enumerate(UNITS):
+            for i in range(k):
+                unit_of[h * NA + a0 + i] = (j, i)
 
         xts = {}
         wgs = {}
@@ -157,8 +162,8 @@ def tile_rglru_kernel(tc, x, state, w_in, b_in, w_a, b_a, a_param, out_0, out_1)
 
         def wint(h, g):
             new_wg(h, g)
-            dst = wgs[(h, g)][:].rearrange("p (t m j) -> p t m j", t=NT, j=4)
-            src = raw[h][g][:].rearrange("p j (m t) -> p t m j", t=NT)
+            dst = wgs[(h, g)][:].rearrange("p (t m j) -> p m j t", t=NT, j=4)
+            src = raw[h][g][:].rearrange("p j (m t) -> p m j t", t=NT)
             nc.vector.tensor_copy(out=dst, in_=src)
 
         def wq(h, g):
@@ -223,51 +228,64 @@ def tile_rglru_kernel(tc, x, state, w_in, b_in, w_a, b_a, a_param, out_0, out_1)
             for t in range(NT):
                 nc.tensor.transpose(tr[:, t, :], ae[h][:, t, a * P:(a + 1) * P], ident[:])
 
-        def t1(u):
-            h, a = u // NA, u % NA
+        def t1(v):
+            h, a = v // NA, v % NA
+            j, i = unit_of[v]
             nc.vector.tensor_tensor(
-                out=t1t[u][:].rearrange("p (m t) -> p m t", t=NT),
-                in0=ats[u][:].rearrange("p t m -> p m t"),
+                out=t1u[j][:, i, :].rearrange("p (m t) -> p m t", t=NT),
+                in0=ats[v][:].rearrange("p t m -> p m t"),
                 in1=st[h][:, a, :].rearrange("p (m t) -> p m t", t=NT),
                 op=ALU.mult,
             )
 
-        def sqr(u):
-            h, a = u // NA, u % NA
-            sqs[u] = sqp.tile([P, NT, P], F32, tag="sq", name="sq%d" % u)
-            nc.scalar.activation(out=sqs[u][:], in_=ae[h][:, :, a * P:(a + 1) * P], func=ACT.Square)
+        def sqr(j):
+            h, a0, k = UNITS[j]
+            sqs[j] = sqp.tile([P, NT, k * P], F32, tag="sq%d" % k, name="sq%d" % j)
+            nc.scalar.activation(out=sqs[j][:], in_=ae[h][:, :, a0 * P:(a0 + k) * P], func=ACT.Square)
 
-        def sqrt(u):
-            nc.scalar.activation(out=sqs[u][:], in_=sqs[u][:], func=ACT.Sqrt, bias=quarter[:, 0:1], scale=-0.25)
+        def sqrt(j):
+            nc.scalar.activation(out=sqs[j][:], in_=sqs[j][:], func=ACT.Sqrt, bias=quarter[:, 0:1], scale=-0.25)
 
-        def t3c(u):
-            h, a = u // NA, u % NA
-            nc.vector.tensor_tensor(out=sqs[u][:], in0=gx[h][:, :, a * P:(a + 1) * P], in1=sqs[u][:], op=ALU.mult)
+        def t3c(j):
+            h, a0, k = UNITS[j]
+            nc.vector.tensor_tensor(out=sqs[j][:], in0=gx[h][:, :, a0 * P:(a0 + k) * P], in1=sqs[j][:], op=ALU.mult)
 
-        def o_t(u):
-            tr = ptr.tile([P, NT, P], F32, tag="tr", name="ot%d" % u)
-            ots[u] = tr
+        def o_t(v):
+            j, i = unit_of[v]
+            tr = ptr.tile([P, NT, P], F32, tag="tr", name="ot%d" % v)
+            ots[v] = tr
             for t in range(NT):
-                nc.tensor.transpose(tr[:, t, :], sqs[u][:, t, :], ident[:])
+                nc.tensor.transpose(tr[:, t, :], sqs[j][:, t, i * P:(i + 1) * P], ident[:])
 
-        def add(u):
-            h, a = u // NA, u % NA
+        def add(v):
+            j, i = unit_of[v]
             nc.vector.tensor_tensor(
-                out=t1t[u][:].rearrange("p (m t) -> p m t", t=NT),
-                in0=ots[u][:].rearrange("p t m -> p m t"),
-                in1=t1t[u][:].rearrange("p (m t) -> p m t", t=NT),
+                out=t1u[j][:, i, :].rearrange("p (m t) -> p m t", t=NT),
+                in0=ots[v][:].rearrange("p t m -> p m t"),
+                in1=t1u[j][:, i, :].rearrange("p (m t) -> p m t", t=NT),
                 op=ALU.add,
             )
-            nc.sync.dma_start(out=out_0[a * P:(a + 1) * P, h * HD:(h + 1) * HD], in_=t1t[u][:])
 
-        def cast(u):
-            h, a = u // NA, u % NA
-            f8 = f8p.tile([P, HD], FP8, tag="f8", name="f8_%d" % u)
-            if u in CAST_ON_ACT:
-                nc.scalar.activation(out=f8[:], in_=t1t[u][:], func=ACT.Copy, scale=Y_SCALE, saturate=False)
+        def dram_view(out, j):
+            h, a0, k = UNITS[j]
+            return out[a0 * P:(a0 + k) * P, h * HD:(h + 1) * HD].rearrange("(i p) c -> p i c", p=P)
+
+        def st0(j):
+            nc.sync.dma_start(out=dram_view(out_0, j), in_=t1u[j][:])
+
+        def cast(j):
+            h, a0, k = UNITS[j]
+            f8 = f8p.tile([P, k * HD], FP8, tag="f8%d" % k, name="f8_%d" % j)
+            src = t1u[j][:].rearrange("p i c -> p (i c)")
+            if j in CAST_ON_ACT:
+                nc.scalar.activation(out=f8[:], in_=src, func=ACT.Copy, scale=Y_SCALE, saturate=False)
             else:
-                nc.vector.tensor_scalar(out=f8[:], in0=t1t[u][:], scalar1=Y_SCALE, scalar2=None, op0=ALU.mult, saturate=False)
-            nc.sync.dma_start(out=out_1[a * P:(a + 1) * P, h * HD:(h + 1) * HD], in_=f8[:].bitcast(U8))
+                nc.vector.tensor_scalar(out=f8[:], in0=src, scalar1=Y_SCALE, scalar2=None, op0=ALU.mult, saturate=False)
+            nc.sync.dma_start(out=dram_view(out_1, j), in_=f8[:].bitcast(U8).rearrange("p (i c) -> p i c", i=k))
+
+        def tiles(j):
+            h, a0, k = UNITS[j]
+            return [h * NA + a0 + i for i in range(k)]
 
         x_t(0, 0)
         x_t(0, 1)
@@ -333,44 +351,32 @@ def tile_rglru_kernel(tc, x, state, w_in, b_in, w_a, b_a, a_param, out_0, out_1)
             if t == NT - 1:
                 atq.extend([h * NA + a for a in range(NA)])
 
-        mq = []
-        oq = []
-        aq = []
-        kq = []
-        kaq = []
-        sqr(0)
-        s = 0
-        while s < H * NA or mq or oq or aq or kq or kaq:
-            if s + 1 < H * NA:
-                sqr(s + 1)
-            if s < H * NA:
-                sqrt(s)
-                mq.append(s)
-            if kaq and (kaq[0] <= s - CAST_LAG_ACT or s >= H * NA):
-                cast(kaq.pop(0))
+        n = len(UNITS)
+        for j in range(n + 4):
+            if j < n:
+                sqr(j)
+                sqrt(j)
+            if 0 <= j - CAST_LAG_ACT < n and (j - CAST_LAG_ACT) in CAST_ON_ACT:
+                cast(j - CAST_LAG_ACT)
             if t1q:
                 t1(t1q.pop(0))
             while gq:
                 gxx(gq.pop(0))
-            if aq and aq[0] <= s - 3:
-                u = aq.pop(0)
-                add(u)
-                if u in CAST_ON_ACT:
-                    kaq.append(u)
-                else:
-                    kq.append(u)
-            if mq and mq[0] <= s - 1:
-                u = mq.pop(0)
-                t3c(u)
-                oq.append(u)
-            if kq and kq[0] <= s - 4:
-                cast(kq.pop(0))
+            if 0 <= j - 3 < n:
+                for v in tiles(j - 3):
+                    add(v)
+                st0(j - 3)
+            if 0 <= j - 1 < n:
+                t3c(j - 1)
+            if 0 <= j - 4 < n and (j - 4) not in CAST_ON_ACT:
+                cast(j - 4)
             if atq:
                 u = atq.pop(0)
                 a_t(u)
                 t1q.append(u)
-            if oq and oq[0] <= s - 2:
-                u = oq.pop(0)
-                o_t(u)
-                aq.append(u)
-            s += 1
+            if 0 <= j - 2 < n:
+                for v in tiles(j - 2):
+                    o_t(v)
+        for j in range(max(0, n + 4 - CAST_LAG_ACT), n):
+            if j in CAST_ON_ACT:
+                cast(j)

@@ -21,9 +21,9 @@ NT = 4
 NA = 4
 Y_SCALE = 280.0
 
-XEVAC = ("V", "S", "S", "S")
+XEVAC = ("V", "S", "V", "S")
 UNITS = ((0, 0, 1), (0, 1, 1), (0, 2, 2), (1, 0, 2), (1, 2, 2), (2, 0, 2), (2, 2, 2), (3, 0, 2), (3, 2, 1), (3, 3, 1))
-CAST_ON_ACT = (1, 3, 5, 7, 9)
+CAST_ON_ACT = (0, 2, 4, 6, 8)
 CAST_LAG_ACT = 6
 
 
@@ -34,7 +34,7 @@ def tile_rglru_kernel(tc, x, state, w_in, b_in, w_a, b_a, a_param, out_0, out_1)
     with ExitStack() as ctx:
         const = ctx.enter_context(tc.tile_pool(name="const", bufs=1))
         xin = ctx.enter_context(tc.tile_pool(name="xin", bufs=3))
-        win = ctx.enter_context(tc.tile_pool(name="win", bufs=4))
+        win = ctx.enter_context(tc.tile_pool(name="win", bufs=5))
         wgp = ctx.enter_context(tc.tile_pool(name="wgp", bufs=4))
         keep = ctx.enter_context(tc.tile_pool(name="keep", bufs=1))
         sqp = ctx.enter_context(tc.tile_pool(name="sqp", bufs=3))
@@ -213,11 +213,10 @@ def tile_rglru_kernel(tc, x, state, w_in, b_in, w_a, b_a, a_param, out_0, out_1)
             h, t = c // NT, c % NT
             nc.scalar.activation(out=ae[h][:, t, :], in_=ae[h][:, t, :], func=ACT.Exp, bias=ch[:, c:c + 1], scale=ch[:, c:c + 1])
 
-        def gxx(c):
-            h, t = c // NT, c % NT
+        def gxx(h):
             nc.vector.scalar_tensor_tensor(
-                out=gx[h][:, t, :], in0=gx[h][:, t, :], scalar=1.0,
-                in1=xg[h][:].rearrange("p (r t) -> p t r", t=NT)[:, t, :],
+                out=gx[h][:], in0=gx[h][:], scalar=1.0,
+                in1=xg[h][:].rearrange("p (r t) -> p t r", t=NT),
                 op0=ALU.add, op1=ALU.mult,
             )
 
@@ -308,7 +307,6 @@ def tile_rglru_kernel(tc, x, state, w_in, b_in, w_a, b_a, a_param, out_0, out_1)
 
         atq = []
         t1q = []
-        gq = []
         for c in range(H * NT):
             h, t = c // NT, c % NT
             hn = h + 1
@@ -326,9 +324,6 @@ def tile_rglru_kernel(tc, x, state, w_in, b_in, w_a, b_a, a_param, out_0, out_1)
             if h == 0 and t < 2:
                 wintq(0, 0, t + 2)
                 wintq(0, 1, t + 2)
-            if gq:
-                gxx(gq.pop(0))
-            gq.append(c)
             if h == 0 and t < 2:
                 wqq(0, 0, t + 2)
                 wqq(0, 1, t + 2)
@@ -339,6 +334,8 @@ def tile_rglru_kernel(tc, x, state, w_in, b_in, w_a, b_a, a_param, out_0, out_1)
                 wq(hn, 0)
                 wq(hn, 1)
                 xq(hn)
+            if h > 0 and t == 1:
+                gxx(h - 1)
             if c + 2 < H * NT:
                 mx(c + 2)
             if atq:
@@ -360,8 +357,8 @@ def tile_rglru_kernel(tc, x, state, w_in, b_in, w_a, b_a, a_param, out_0, out_1)
                 cast(j - CAST_LAG_ACT)
             if t1q:
                 t1(t1q.pop(0))
-            while gq:
-                gxx(gq.pop(0))
+            if j == 0:
+                gxx(H - 1)
             if 0 <= j - 3 < n:
                 for v in tiles(j - 3):
                     add(v)

@@ -21,10 +21,16 @@ NT = 4
 NA = 4
 Y_SCALE = 280.0
 
-XEVAC = ("V", "S", "V", "S")
+XEVAC = ("V", "S", "V", "V")
 UNITS = ((0, 0, 1), (0, 1, 1), (0, 2, 2), (1, 0, 2), (1, 2, 2), (2, 0, 2), (2, 2, 2), (3, 0, 2), (3, 2, 1), (3, 3, 1))
-CAST_ON_ACT = (0, 2, 4, 6, 8)
-CAST_LAG_ACT = 6
+CAST_ON_ACT = (2, 3, 4, 5, 6, 7)
+T3C_ON_POOL = ()
+WINT_ON_POOL = ()
+T1_PER_STEP = 1
+LAG_T3C = 1
+LAG_OT = 2
+LAG_ADD = 3
+LAG_CAST = 4
 
 
 def tile_rglru_kernel(tc, x, state, w_in, b_in, w_a, b_a, a_param, out_0, out_1):
@@ -33,12 +39,11 @@ def tile_rglru_kernel(tc, x, state, w_in, b_in, w_a, b_a, a_param, out_0, out_1)
 
     with ExitStack() as ctx:
         const = ctx.enter_context(tc.tile_pool(name="const", bufs=1))
-        xin = ctx.enter_context(tc.tile_pool(name="xin", bufs=3))
-        win = ctx.enter_context(tc.tile_pool(name="win", bufs=5))
+        xin = ctx.enter_context(tc.tile_pool(name="xin", bufs=4))
+        win = ctx.enter_context(tc.tile_pool(name="win", bufs=8))
         wgp = ctx.enter_context(tc.tile_pool(name="wgp", bufs=4))
         keep = ctx.enter_context(tc.tile_pool(name="keep", bufs=1))
-        sqp = ctx.enter_context(tc.tile_pool(name="sqp", bufs=3))
-        f8p = ctx.enter_context(tc.tile_pool(name="f8p", bufs=3))
+        f8p = ctx.enter_context(tc.tile_pool(name="f8p", bufs=6))
         pmx = ctx.enter_context(tc.psum_pool(name="pmx", bufs=2))
         ptr = ctx.enter_context(tc.psum_pool(name="ptr", bufs=4))
         ctx.enter_context(tc.manual_schedule())
@@ -95,11 +100,10 @@ def tile_rglru_kernel(tc, x, state, w_in, b_in, w_a, b_a, a_param, out_0, out_1)
 
         for h in range(H):
             load_x(h)
-            load_w(h, 0)
             load_w(h, 1)
-            if h >= 1:
-                load_st(h - 1)
-        load_st(H - 1)
+            load_w(h, 0)
+        for h in range(H):
+            load_st(h)
 
         v = vecs[:, 2, :]
         av = const.tile([P, H * NT], F32, name="av")
@@ -162,9 +166,14 @@ def tile_rglru_kernel(tc, x, state, w_in, b_in, w_a, b_a, a_param, out_0, out_1)
 
         def wint(h, g):
             new_wg(h, g)
-            dst = wgs[(h, g)][:].rearrange("p (t m j) -> p m j t", t=NT, j=4)
-            src = raw[h][g][:].rearrange("p j (m t) -> p m j t", t=NT)
-            nc.vector.tensor_copy(out=dst, in_=src)
+            if (h, g) in WINT_ON_POOL:
+                dst = wgs[(h, g)][:].rearrange("p (t m j) -> p t m j", t=NT, j=4)
+                src = raw[h][g][:].rearrange("p j (m t) -> p t m j", t=NT)
+                nc.gpsimd.tensor_scalar(out=dst, in0=src, scalar1=1.0, scalar2=0.0, op0=ALU.mult, op1=ALU.add)
+            else:
+                dst = wgs[(h, g)][:].rearrange("p (t m j) -> p m j t", t=NT, j=4)
+                src = raw[h][g][:].rearrange("p j (m t) -> p m j t", t=NT)
+                nc.vector.tensor_copy(out=dst, in_=src)
 
         def wq(h, g):
             nc.vector.quantize_mx(out=wc[h][g][:].bitcast(FP8X4), scales=ws[h][g][:], in_=wgs[(h, g)][:])
@@ -186,8 +195,8 @@ def tile_rglru_kernel(tc, x, state, w_in, b_in, w_a, b_a, a_param, out_0, out_1)
         def mx(c):
             h, t = c // NT, c % NT
             cols = slice(t * P, (t + 1) * P)
-            pair = []
-            for g in range(2):
+            pair = [None, None]
+            for g in (1, 0):
                 ps = pmx.tile([P, B], F32, tag="ps%d" % g, name="ps%d_%d" % (g, c))
                 nc.tensor.matmul_mx(
                     out=ps[:],
@@ -198,7 +207,7 @@ def tile_rglru_kernel(tc, x, state, w_in, b_in, w_a, b_a, a_param, out_0, out_1)
                     start=True,
                     stop=True,
                 )
-                pair.append(ps)
+                pair[g] = ps
             acc[c] = pair
 
         def thx(c):
@@ -239,15 +248,17 @@ def tile_rglru_kernel(tc, x, state, w_in, b_in, w_a, b_a, a_param, out_0, out_1)
 
         def sqr(j):
             h, a0, k = UNITS[j]
-            sqs[j] = sqp.tile([P, NT, k * P], F32, tag="sq%d" % k, name="sq%d" % j)
-            nc.scalar.activation(out=sqs[j][:], in_=ae[h][:, :, a0 * P:(a0 + k) * P], func=ACT.Square)
+            assert all((h * NA + a0 + i) in ats for i in range(k))
+            sqs[j] = ae[h][:, :, a0 * P:(a0 + k) * P]
+            nc.scalar.activation(out=sqs[j], in_=sqs[j], func=ACT.Square)
 
         def sqrt(j):
-            nc.scalar.activation(out=sqs[j][:], in_=sqs[j][:], func=ACT.Sqrt, bias=quarter[:, 0:1], scale=-0.25)
+            nc.scalar.activation(out=sqs[j], in_=sqs[j], func=ACT.Sqrt, bias=quarter[:, 0:1], scale=-0.25)
 
         def t3c(j):
             h, a0, k = UNITS[j]
-            nc.vector.tensor_tensor(out=sqs[j][:], in0=gx[h][:, :, a0 * P:(a0 + k) * P], in1=sqs[j][:], op=ALU.mult)
+            eng = nc.gpsimd if j in T3C_ON_POOL else nc.vector
+            eng.tensor_tensor(out=sqs[j], in0=gx[h][:, :, a0 * P:(a0 + k) * P], in1=sqs[j], op=ALU.mult)
 
         def o_t(v):
             j, i = unit_of[v]
@@ -290,16 +301,16 @@ def tile_rglru_kernel(tc, x, state, w_in, b_in, w_a, b_a, a_param, out_0, out_1)
         x_t(0, 1)
         xev(0, 0)
         xev(0, 1)
-        wintq(0, 0, 0)
-        xq(0)
-        wqq(0, 0, 0)
         wintq(0, 1, 0)
-        wintq(0, 0, 1)
+        xq(0)
         wqq(0, 1, 0)
-        softplus_tail()
+        wintq(0, 0, 0)
         wintq(0, 1, 1)
-        wqq(0, 0, 1)
+        wqq(0, 0, 0)
+        softplus_tail()
+        wintq(0, 0, 1)
         wqq(0, 1, 1)
+        wqq(0, 0, 1)
         mx(0)
         mx(1)
         x_t(1, 0)
@@ -307,73 +318,81 @@ def tile_rglru_kernel(tc, x, state, w_in, b_in, w_a, b_a, a_param, out_0, out_1)
 
         atq = []
         t1q = []
+        gxq = []
         for c in range(H * NT):
             h, t = c // NT, c % NT
-            hn = h + 1
             tha(c)
             thx(c)
             ex(c)
-            if hn < H and t == 0 and XEVAC[hn] == "S":
-                xev(hn, 0)
-                xev(hn, 1)
-            if t1q:
-                t1(t1q.pop(0))
-            if hn < H and t == 0:
-                wint(hn, 0)
-                wint(hn, 1)
-            if h == 0 and t < 2:
-                wintq(0, 0, t + 2)
-                wintq(0, 1, t + 2)
-            if h == 0 and t < 2:
-                wqq(0, 0, t + 2)
-                wqq(0, 1, t + 2)
-            if hn < H and t == 0 and XEVAC[hn] == "V":
-                xev(hn, 0)
-                xev(hn, 1)
-            if hn < H and t == 1:
-                wq(hn, 0)
-                wq(hn, 1)
-                xq(hn)
-            if h > 0 and t == 1:
-                gxx(h - 1)
+            hp = c // 2 + 1
+            if hp < H and c % 2 == 0 and XEVAC[hp] == "S":
+                xev(hp, 0)
+                xev(hp, 1)
+            if c == 0:
+                for tt in (2, 3):
+                    wintq(0, 1, tt)
+                    wintq(0, 0, tt)
+                    wqq(0, 1, tt)
+                    wqq(0, 0, tt)
+            if hp < H and c % 2 == 0:
+                wint(hp, 1)
+                wint(hp, 0)
+                if XEVAC[hp] == "V":
+                    xev(hp, 0)
+                    xev(hp, 1)
+            if hp < H and c % 2 == 1:
+                wq(hp, 1)
+                wq(hp, 0)
+                xq(hp)
+            if hp >= H:
+                if gxq:
+                    gxx(gxq.pop(0))
+                for i in range(T1_PER_STEP):
+                    if t1q:
+                        t1(t1q.pop(0))
             if c + 2 < H * NT:
                 mx(c + 2)
-            if atq:
-                u = atq.pop(0)
-                a_t(u)
-                t1q.append(u)
-            if t == NT - 1 and h + 2 < H:
-                x_t(h + 2, 0)
-                x_t(h + 2, 1)
+            if hp + 1 < H and c % 2 == 1:
+                x_t(hp + 1, 0)
+                x_t(hp + 1, 1)
+            if hp >= H:
+                for i in range(T1_PER_STEP):
+                    if atq:
+                        u = atq.pop(0)
+                        a_t(u)
+                        t1q.append(u)
             if t == NT - 1:
                 atq.extend([h * NA + a for a in range(NA)])
+                gxq.append(h)
 
         n = len(UNITS)
-        for j in range(n + 4):
-            if j < n:
-                sqr(j)
-                sqrt(j)
-            if 0 <= j - CAST_LAG_ACT < n and (j - CAST_LAG_ACT) in CAST_ON_ACT:
-                cast(j - CAST_LAG_ACT)
+        sqr(0)
+        actq = list(CAST_ON_ACT)
+        for s in range(n + LAG_CAST + 1):
+            if s + 1 < n:
+                sqr(s + 1)
+            if s < n:
+                sqrt(s)
             if t1q:
                 t1(t1q.pop(0))
-            if j == 0:
-                gxx(H - 1)
-            if 0 <= j - 3 < n:
-                for v in tiles(j - 3):
+            if gxq:
+                gxx(gxq.pop(0))
+            if 0 <= s - LAG_T3C < n:
+                t3c(s - LAG_T3C)
+            if 0 <= s - LAG_ADD < n:
+                for v in tiles(s - LAG_ADD):
                     add(v)
-                st0(j - 3)
-            if 0 <= j - 1 < n:
-                t3c(j - 1)
-            if 0 <= j - 4 < n and (j - 4) not in CAST_ON_ACT:
-                cast(j - 4)
+                st0(s - LAG_ADD)
+            if 0 <= s - LAG_CAST < n and (s - LAG_CAST) not in CAST_ON_ACT:
+                cast(s - LAG_CAST)
+            if s >= n - 1:
+                for i in range(2):
+                    if actq and actq[0] <= s - LAG_ADD:
+                        cast(actq.pop(0))
             if atq:
                 u = atq.pop(0)
                 a_t(u)
                 t1q.append(u)
-            if 0 <= j - 2 < n:
-                for v in tiles(j - 2):
+            if 0 <= s - LAG_OT < n:
+                for v in tiles(s - LAG_OT):
                     o_t(v)
-        for j in range(max(0, n + 4 - CAST_LAG_ACT), n):
-            if j in CAST_ON_ACT:
-                cast(j)

@@ -23,10 +23,12 @@ Y_SCALE = 280.0
 
 XEVAC = ("V", "S", "V", "V")
 UNITS = ((0, 0, 1), (0, 1, 1), (0, 2, 2), (1, 0, 2), (1, 2, 2), (2, 0, 2), (2, 2, 2), (3, 0, 2), (3, 2, 1), (3, 3, 1))
-CAST_ON_ACT = (2, 3, 4, 5, 6, 7)
-T3C_ON_POOL = ()
+CAST_ON_ACT = (0, 1, 2, 3, 4, 5, 6, 7)
+T3C_ON_POOL = (0, 1, 2, 3, 4, 5, 6, 7, 8, 9)
 WINT_ON_POOL = ()
-T1_PER_STEP = 1
+SQ_ON_DVE = (0, 1, 2, 3, 4)
+T1_FROM = 16
+LAG_CA = 4
 LAG_T3C = 1
 LAG_OT = 2
 LAG_ADD = 3
@@ -248,9 +250,13 @@ def tile_rglru_kernel(tc, x, state, w_in, b_in, w_a, b_a, a_param, out_0, out_1)
 
         def sqr(j):
             h, a0, k = UNITS[j]
-            assert all((h * NA + a0 + i) in ats for i in range(k))
-            sqs[j] = ae[h][:, :, a0 * P:(a0 + k) * P]
-            nc.scalar.activation(out=sqs[j], in_=sqs[j], func=ACT.Square)
+            sq = win.tile([P, NT, k * P], F32, tag="raw", name="sq%d" % j)
+            sqs[j] = sq[:]
+            a = ae[h][:, :, a0 * P:(a0 + k) * P]
+            if j in SQ_ON_DVE:
+                nc.vector.tensor_tensor(out=sqs[j], in0=a, in1=a, op=ALU.mult)
+            else:
+                nc.scalar.activation(out=sqs[j], in_=a, func=ACT.Square)
 
         def sqrt(j):
             nc.scalar.activation(out=sqs[j], in_=sqs[j], func=ACT.Sqrt, bias=quarter[:, 0:1], scale=-0.25)
@@ -318,7 +324,6 @@ def tile_rglru_kernel(tc, x, state, w_in, b_in, w_a, b_a, a_param, out_0, out_1)
 
         atq = []
         t1q = []
-        gxq = []
         for c in range(H * NT):
             h, t = c // NT, c % NT
             tha(c)
@@ -344,39 +349,41 @@ def tile_rglru_kernel(tc, x, state, w_in, b_in, w_a, b_a, a_param, out_0, out_1)
                 wq(hp, 1)
                 wq(hp, 0)
                 xq(hp)
-            if hp >= H:
-                if gxq:
-                    gxx(gxq.pop(0))
-                for i in range(T1_PER_STEP):
-                    if t1q:
-                        t1(t1q.pop(0))
+            for hh in range(H - 1):
+                if c == max(6, NT * hh + NT):
+                    gxx(hh)
+                    for j in SQ_ON_DVE:
+                        if UNITS[j][0] == hh:
+                            sqr(j)
+            if c >= T1_FROM and t1q:
+                t1(t1q.pop(0))
             if c + 2 < H * NT:
                 mx(c + 2)
             if hp + 1 < H and c % 2 == 1:
                 x_t(hp + 1, 0)
                 x_t(hp + 1, 1)
-            if hp >= H:
-                for i in range(T1_PER_STEP):
-                    if atq:
-                        u = atq.pop(0)
-                        a_t(u)
-                        t1q.append(u)
+            if c + 1 >= T1_FROM and atq:
+                u = atq.pop(0)
+                a_t(u)
+                t1q.append(u)
             if t == NT - 1:
                 atq.extend([h * NA + a for a in range(NA)])
-                gxq.append(h)
 
         n = len(UNITS)
-        sqr(0)
+        act_sq = [j for j in range(n) if j not in SQ_ON_DVE]
         actq = list(CAST_ON_ACT)
-        for s in range(n + LAG_CAST + 1):
-            if s + 1 < n:
-                sqr(s + 1)
+        gxx(H - 1)
+        for s in range(n + LAG_CA + 1):
+            if s + 1 in act_sq or (s == 0 and 0 in act_sq):
+                if s == 0 and 0 in act_sq:
+                    sqr(0)
+                if s + 1 in act_sq:
+                    sqr(s + 1)
             if s < n:
                 sqrt(s)
-            if t1q:
-                t1(t1q.pop(0))
-            if gxq:
-                gxx(gxq.pop(0))
+            for i in range(2):
+                if t1q:
+                    t1(t1q.pop(0))
             if 0 <= s - LAG_T3C < n:
                 t3c(s - LAG_T3C)
             if 0 <= s - LAG_ADD < n:
@@ -385,14 +392,13 @@ def tile_rglru_kernel(tc, x, state, w_in, b_in, w_a, b_a, a_param, out_0, out_1)
                 st0(s - LAG_ADD)
             if 0 <= s - LAG_CAST < n and (s - LAG_CAST) not in CAST_ON_ACT:
                 cast(s - LAG_CAST)
-            if s >= n - 1:
-                for i in range(2):
-                    if actq and actq[0] <= s - LAG_ADD:
-                        cast(actq.pop(0))
-            if atq:
-                u = atq.pop(0)
-                a_t(u)
-                t1q.append(u)
+            if 0 <= s - LAG_CA < n and (s - LAG_CA) in CAST_ON_ACT:
+                cast(s - LAG_CA)
+            for i in range(2):
+                if atq:
+                    u = atq.pop(0)
+                    a_t(u)
+                    t1q.append(u)
             if 0 <= s - LAG_OT < n:
                 for v in tiles(s - LAG_OT):
                     o_t(v)

@@ -26,10 +26,12 @@ UNITS = ((0, 0, 1), (0, 1, 1), (0, 2, 2), (1, 0, 2), (1, 2, 2), (2, 0, 2), (2, 2
 CAST_ON_ACT = (0, 1, 2, 3, 4, 5, 6, 7)
 T3C_ON_POOL = (0, 1, 2, 3, 4, 5, 6, 7, 8, 9)
 WINT_ON_POOL = ()
-SQ_ON_DVE = (0, 1, 2, 3, 4)
-T1_FROM = 16
+SQ_ON_POOL = (0, 1, 2, 3, 4)
+R2_FROM = 10
+R2_RATE = 2
 LAG_CA = 4
 LAG_T3C = 1
+LAG_T3V = 1
 LAG_OT = 2
 LAG_ADD = 3
 LAG_CAST = 4
@@ -231,6 +233,20 @@ def tile_rglru_kernel(tc, x, state, w_in, b_in, w_a, b_a, a_param, out_0, out_1)
                 op0=ALU.add, op1=ALU.mult,
             )
 
+        xus = {}
+
+        def x_t2(h, u):
+            xu = ptr.tile([P, NA, P], F32, tag="tr", name="xu%d_%d" % (h, u))
+            xus[(h, u)] = xu
+            for a in range(NA):
+                words = xn[h][:, a, :].bitcast(F32)
+                nc.tensor.transpose(xu[:, a, :], words[:, u:HD // 2:2], ident[:])
+
+        def gxx2(h, u):
+            g = gx[h][:, 2 * u:2 * u + 2, :]
+            xv = xus[(h, u)][:].rearrange("p a r -> p (a r)").bitcast(BF16).rearrange("p (q e) -> p e q", e=2)
+            nc.vector.scalar_tensor_tensor(out=g, in0=g, scalar=1.0, in1=xv, op0=ALU.add, op1=ALU.mult)
+
         def a_t(u):
             h, a = u // NA, u % NA
             tr = ptr.tile([P, NT, P], F32, tag="tr", name="at%d" % u)
@@ -253,8 +269,8 @@ def tile_rglru_kernel(tc, x, state, w_in, b_in, w_a, b_a, a_param, out_0, out_1)
             sq = win.tile([P, NT, k * P], F32, tag="raw", name="sq%d" % j)
             sqs[j] = sq[:]
             a = ae[h][:, :, a0 * P:(a0 + k) * P]
-            if j in SQ_ON_DVE:
-                nc.vector.tensor_tensor(out=sqs[j], in0=a, in1=a, op=ALU.mult)
+            if j in SQ_ON_POOL:
+                nc.gpsimd.tensor_tensor(out=sqs[j], in0=a, in1=a, op=ALU.mult)
             else:
                 nc.scalar.activation(out=sqs[j], in_=a, func=ACT.Square)
 
@@ -268,7 +284,7 @@ def tile_rglru_kernel(tc, x, state, w_in, b_in, w_a, b_a, a_param, out_0, out_1)
 
         def o_t(v):
             j, i = unit_of[v]
-            tr = ptr.tile([P, NT, P], F32, tag="tr", name="ot%d" % v)
+            tr = pmx.tile([P, NT, P], F32, tag="ps%d" % (v % 2), name="ot%d" % v)
             ots[v] = tr
             for t in range(NT):
                 nc.tensor.transpose(tr[:, t, :], sqs[j][:, t, i * P:(i + 1) * P], ident[:])
@@ -322,17 +338,41 @@ def tile_rglru_kernel(tc, x, state, w_in, b_in, w_a, b_a, a_param, out_0, out_1)
         x_t(1, 0)
         x_t(1, 1)
 
-        atq = []
-        t1q = []
+        hold = const.tile([P, 1], U32, name="hold")
+        work = []
+        pend = []
+
+        def pe_part(task):
+            if task[0] == "g":
+                x_t2(task[1], task[2])
+            else:
+                a_t(task[1])
+
+        def dve_part(task):
+            if task[0] == "g":
+                gxx2(task[1], task[2])
+            else:
+                t1(task[1])
+
+        def regime2(rate):
+            for task in pend:
+                dve_part(task)
+            pend.clear()
+            for i in range(rate):
+                if work:
+                    task = work.pop(0)
+                    pe_part(task)
+                    pend.append(task)
+
         for c in range(H * NT):
             h, t = c // NT, c % NT
             tha(c)
             thx(c)
             ex(c)
             hp = c // 2 + 1
-            if hp < H and c % 2 == 0 and XEVAC[hp] == "S":
-                xev(hp, 0)
-                xev(hp, 1)
+            if c == 1:
+                xev(1, 0)
+                xev(1, 1)
             if c == 0:
                 for tt in (2, 3):
                     wintq(0, 1, tt)
@@ -349,43 +389,37 @@ def tile_rglru_kernel(tc, x, state, w_in, b_in, w_a, b_a, a_param, out_0, out_1)
                 wq(hp, 1)
                 wq(hp, 0)
                 xq(hp)
-            for hh in range(H - 1):
-                if c == max(6, NT * hh + NT):
-                    gxx(hh)
-                    for j in SQ_ON_DVE:
+            if c == 2 * (H - 1) - 1:
+                nc.gpsimd.tensor_copy(out=hold[:], in_=xc[H - 1][:, 0:1])
+            for hh in range(H):
+                if c == max(2 * (H - 1), NT * hh + NT):
+                    for j in SQ_ON_POOL:
                         if UNITS[j][0] == hh:
                             sqr(j)
-            if c >= T1_FROM and t1q:
-                t1(t1q.pop(0))
+            if c >= R2_FROM:
+                regime2(R2_RATE)
             if c + 2 < H * NT:
                 mx(c + 2)
             if hp + 1 < H and c % 2 == 1:
                 x_t(hp + 1, 0)
                 x_t(hp + 1, 1)
-            if c + 1 >= T1_FROM and atq:
-                u = atq.pop(0)
-                a_t(u)
-                t1q.append(u)
             if t == NT - 1:
-                atq.extend([h * NA + a for a in range(NA)])
+                work.extend([("g", h, 0), ("g", h, 1)] + [("t", h * NA + a) for a in range(NA)])
 
         n = len(UNITS)
-        act_sq = [j for j in range(n) if j not in SQ_ON_DVE]
-        actq = list(CAST_ON_ACT)
-        gxx(H - 1)
+        act_sq = [j for j in range(n) if j not in SQ_ON_POOL]
         for s in range(n + LAG_CA + 1):
-            if s + 1 in act_sq or (s == 0 and 0 in act_sq):
-                if s == 0 and 0 in act_sq:
-                    sqr(0)
-                if s + 1 in act_sq:
-                    sqr(s + 1)
+            if s == 0 and 0 in act_sq:
+                sqr(0)
+            if s + 1 in act_sq:
+                sqr(s + 1)
             if s < n:
                 sqrt(s)
-            for i in range(2):
-                if t1q:
-                    t1(t1q.pop(0))
-            if 0 <= s - LAG_T3C < n:
+            regime2(R2_RATE)
+            if 0 <= s - LAG_T3C < n and (s - LAG_T3C) in T3C_ON_POOL:
                 t3c(s - LAG_T3C)
+            if 0 <= s - LAG_T3V < n and (s - LAG_T3V) not in T3C_ON_POOL:
+                t3c(s - LAG_T3V)
             if 0 <= s - LAG_ADD < n:
                 for v in tiles(s - LAG_ADD):
                     add(v)
@@ -394,11 +428,6 @@ def tile_rglru_kernel(tc, x, state, w_in, b_in, w_a, b_a, a_param, out_0, out_1)
                 cast(s - LAG_CAST)
             if 0 <= s - LAG_CA < n and (s - LAG_CA) in CAST_ON_ACT:
                 cast(s - LAG_CA)
-            for i in range(2):
-                if atq:
-                    u = atq.pop(0)
-                    a_t(u)
-                    t1q.append(u)
             if 0 <= s - LAG_OT < n:
                 for v in tiles(s - LAG_OT):
                     o_t(v)

@@ -24,14 +24,14 @@ Y_SCALE = 280.0
 XEVAC = ("V", "S", "V", "V")
 UNITS = ((0, 0, 1), (0, 1, 1), (0, 2, 2), (1, 0, 2), (1, 2, 2), (2, 0, 2), (2, 2, 2), (3, 0, 2), (3, 2, 1), (3, 3, 1))
 CAST_ON_ACT = (0, 1, 2, 3, 4, 5, 6, 7)
-T3C_ON_POOL = (0, 1, 2, 3, 4, 5, 6, 7, 8, 9)
+T3C_ON_POOL = (0, 1, 2, 3, 4, 5, 7, 9)
 WINT_ON_POOL = ()
-SQ_ON_POOL = (0, 1, 2, 3, 4)
+SQ_ON_POOL = (0, 1, 2, 3, 4, 5)
 R2_FROM = 10
 R2_RATE = 2
 LAG_CA = 4
 LAG_T3C = 1
-LAG_T3V = 1
+LAG_T3V = 2
 LAG_OT = 2
 LAG_ADD = 3
 LAG_CAST = 4

@@ -338,7 +338,6 @@ def tile_rglru_kernel(tc, x, state, w_in, b_in, w_a, b_a, a_param, out_0, out_1)
         x_t(1, 0)
         x_t(1, 1)
 
-        hold = const.tile([P, 1], U32, name="hold")
         work = []
         pend = []
 
@@ -389,8 +388,6 @@ def tile_rglru_kernel(tc, x, state, w_in, b_in, w_a, b_a, a_param, out_0, out_1)
                 wq(hp, 1)
                 wq(hp, 0)
                 xq(hp)
-            if c == 2 * (H - 1) - 1:
-                nc.gpsimd.tensor_copy(out=hold[:], in_=xc[H - 1][:, 0:1])
             for hh in range(H):
                 if c == max(2 * (H - 1), NT * hh + NT):
                     for j in SQ_ON_POOL:

@@ -35,6 +35,9 @@ LAG_T3V = 2
 LAG_OT = 2
 LAG_ADD = 3
 LAG_CAST = 4
+WARM_HEAD = 1
+WARM_MID = 3
+WARM_GAP = 2
 
 
 def tile_rglru_kernel(tc, x, state, w_in, b_in, w_a, b_a, a_param, out_0, out_1):
@@ -52,6 +55,8 @@ def tile_rglru_kernel(tc, x, state, w_in, b_in, w_a, b_a, a_param, out_0, out_1)
         ptr = ctx.enter_context(tc.psum_pool(name="ptr", bufs=4))
         ctx.enter_context(tc.manual_schedule())
 
+        zeros = const.tile([P, 2 * P], F32, name="zeros")
+        nc.vector.memset(zeros[:], 0.0)
         warm = const.tile([P, 1], F32, name="warm")
         nc.vector.memset(warm[:], 0.0)
         one = const.tile([P, 1], F32, name="one")
@@ -289,6 +294,14 @@ def tile_rglru_kernel(tc, x, state, w_in, b_in, w_a, b_a, a_param, out_0, out_1)
             for t in range(NT):
                 nc.tensor.transpose(tr[:, t, :], sqs[j][:, t, i * P:(i + 1) * P], ident[:])
 
+        def keep_warm(k, n_cols, early):
+            for i in range(k):
+                if early:
+                    dummy = pmx.tile([P, n_cols], F32, tag="ps%d" % (i % 2), name="dummy")
+                else:
+                    dummy = ptr.tile([P, n_cols], F32, tag="tr", name="dummy")
+                nc.tensor.matmul(dummy[:], lhsT=zeros[:, 0:P], rhs=zeros[:, 0:n_cols], start=True, stop=True)
+
         def add(v):
             j, i = unit_of[v]
             nc.vector.tensor_tensor(
@@ -319,8 +332,10 @@ def tile_rglru_kernel(tc, x, state, w_in, b_in, w_a, b_a, a_param, out_0, out_1)
             h, a0, k = UNITS[j]
             return [h * NA + a0 + i for i in range(k)]
 
+        keep_warm(WARM_HEAD, 2 * P, True)
         x_t(0, 0)
         x_t(0, 1)
+        keep_warm(WARM_MID, 2 * P, True)
         xev(0, 0)
         xev(0, 1)
         wintq(0, 1, 0)
@@ -400,6 +415,8 @@ def tile_rglru_kernel(tc, x, state, w_in, b_in, w_a, b_a, a_param, out_0, out_1)
             if hp + 1 < H and c % 2 == 1:
                 x_t(hp + 1, 0)
                 x_t(hp + 1, 1)
+            if c == 1:
+                keep_warm(WARM_GAP, 2 * P, False)
             if t == NT - 1:
                 work.extend([("g", h, 0), ("g", h, 1)] + [("t", h * NA + a) for a in range(NA)])
 
@@ -428,3 +445,5 @@ def tile_rglru_kernel(tc, x, state, w_in, b_in, w_a, b_a, a_param, out_0, out_1)
             if 0 <= s - LAG_OT < n:
                 for v in tiles(s - LAG_OT):
                     o_t(v)
+            if s < n + LAG_OT:
+                keep_warm(1, 2 * P, False)

@@ -24,10 +24,10 @@ Y_SCALE = 280.0
 XEVAC = ("V", "S", "V", "V")
 UNITS = ((0, 0, 1), (0, 1, 1), (0, 2, 2), (1, 0, 2), (1, 2, 2), (2, 0, 2), (2, 2, 2), (3, 0, 2), (3, 2, 1), (3, 3, 1))
 CAST_ON_ACT = (0, 1, 2, 3, 4, 5, 6, 7)
-T3C_ON_POOL = (0, 1, 2, 3, 4, 5, 7, 9)
+T3C_ON_POOL = (0, 1, 2, 4, 5, 7)
 WINT_ON_POOL = ()
-SQ_ON_POOL = (0, 1, 2, 3, 4, 5)
-R2_FROM = 10
+SPLIT = 8
+R2_FROM = 9
 R2_RATE = 2
 LAG_CA = 4
 LAG_T3C = 1
@@ -148,6 +148,7 @@ def tile_rglru_kernel(tc, x, state, w_in, b_in, w_a, b_a, a_param, out_0, out_1)
         acc = {}
         ats = {}
         sqs = {}
+        sqt = {}
         ots = {}
 
         def x_t(h, half):
@@ -201,31 +202,28 @@ def tile_rglru_kernel(tc, x, state, w_in, b_in, w_a, b_a, a_param, out_0, out_1)
                 in_=wgs[(h, g)][:, t * HD:(t + 1) * HD],
             )
 
-        def mx(c):
+        def mx(c, g):
             h, t = c // NT, c % NT
             cols = slice(t * P, (t + 1) * P)
-            pair = [None, None]
-            for g in (1, 0):
-                ps = pmx.tile([P, B], F32, tag="ps%d" % g, name="ps%d_%d" % (g, c))
-                nc.tensor.matmul_mx(
-                    out=ps[:],
-                    lhsT=wc[h][g][:, cols].bitcast(FP8X4),
-                    lhsT_scale=ws[h][g][:, cols],
-                    rhs=xc[h][:].bitcast(FP8X4),
-                    rhs_scale=xs[h][:],
-                    start=True,
-                    stop=True,
-                )
-                pair[g] = ps
-            acc[c] = pair
+            ps = pmx.tile([P, B], F32, tag="ps%d" % (g if c < SPLIT else c % 2), name="ps%d_%d" % (g, c))
+            nc.tensor.matmul_mx(
+                out=ps[:],
+                lhsT=wc[h][g][:, cols].bitcast(FP8X4),
+                lhsT_scale=ws[h][g][:, cols],
+                rhs=xc[h][:].bitcast(FP8X4),
+                rhs_scale=xs[h][:],
+                start=True,
+                stop=True,
+            )
+            acc[(c, g)] = ps
 
         def thx(c):
             h, t = c // NT, c % NT
-            nc.scalar.activation(out=gx[h][:, t, :], in_=acc[c][0][:], func=ACT.Tanh, bias=hb[:, 0, c:c + 1], scale=0.5)
+            nc.scalar.activation(out=gx[h][:, t, :], in_=acc[(c, 0)][:], func=ACT.Tanh, bias=hb[:, 0, c:c + 1], scale=0.5)
 
         def tha(c):
             h, t = c // NT, c % NT
-            nc.scalar.activation(out=ae[h][:, t, :], in_=acc[c][1][:], func=ACT.Tanh, bias=hb[:, 1, c:c + 1], scale=0.5)
+            nc.scalar.activation(out=ae[h][:, t, :], in_=acc[(c, 1)][:], func=ACT.Tanh, bias=hb[:, 1, c:c + 1], scale=0.5)
 
         def ex(c):
             h, t = c // NT, c % NT
@@ -271,13 +269,11 @@ def tile_rglru_kernel(tc, x, state, w_in, b_in, w_a, b_a, a_param, out_0, out_1)
 
         def sqr(j):
             h, a0, k = UNITS[j]
-            sq = win.tile([P, NT, k * P], F32, tag="raw", name="sq%d" % j)
-            sqs[j] = sq[:]
+            if a0 % 2 == 0:
+                sqt[(h, a0 // 2)] = win.tile([P, NT, 2 * P], F32, tag="raw", name="sq%d" % j)
+            sqs[j] = sqt[(h, a0 // 2)][:, :, (a0 % 2) * P:(a0 % 2 + k) * P]
             a = ae[h][:, :, a0 * P:(a0 + k) * P]
-            if j in SQ_ON_POOL:
-                nc.gpsimd.tensor_tensor(out=sqs[j], in0=a, in1=a, op=ALU.mult)
-            else:
-                nc.scalar.activation(out=sqs[j], in_=a, func=ACT.Square)
+            nc.gpsimd.tensor_tensor(out=sqs[j], in0=a, in1=a, op=ALU.mult)
 
         def sqrt(j):
             nc.scalar.activation(out=sqs[j], in_=sqs[j], func=ACT.Sqrt, bias=quarter[:, 0:1], scale=-0.25)
@@ -348,13 +344,16 @@ def tile_rglru_kernel(tc, x, state, w_in, b_in, w_a, b_a, a_param, out_0, out_1)
         wintq(0, 0, 1)
         wqq(0, 1, 1)
         wqq(0, 0, 1)
-        mx(0)
-        mx(1)
+        mx(0, 1)
+        mx(0, 0)
+        mx(1, 1)
+        mx(1, 0)
         x_t(1, 0)
         x_t(1, 1)
 
         work = []
         pend = []
+        cost = {"g": 2, "t": 1}
 
         def pe_part(task):
             if task[0] == "g":
@@ -368,65 +367,86 @@ def tile_rglru_kernel(tc, x, state, w_in, b_in, w_a, b_a, a_param, out_0, out_1)
             else:
                 t1(task[1])
 
-        def regime2(rate):
+        def regime2_v():
             for task in pend:
                 dve_part(task)
             pend.clear()
+
+        def regime2_pe(budget):
+            while work and budget > 0:
+                task = work.pop(0)
+                budget -= cost[task[0]]
+                pe_part(task)
+                pend.append(task)
+
+        def regime2(rate):
+            regime2_v()
             for i in range(rate):
                 if work:
                     task = work.pop(0)
                     pe_part(task)
                     pend.append(task)
 
-        for c in range(H * NT):
-            h, t = c // NT, c % NT
-            tha(c)
-            thx(c)
-            ex(c)
-            hp = c // 2 + 1
-            if c == 1:
+        NC = H * NT
+        steps = []
+        for c in range(SPLIT):
+            steps.append(([(tha, c), (thx, c), (ex, c)], [(c + 2, 1), (c + 2, 0)] if c + 2 < SPLIT else [(c + 2, 1)], 3))
+        for c in range(SPLIT, NC):
+            steps.append(([(tha, c)] + ([(ex, c - 1)] if c > SPLIT else []), [(c + 2, 1)] if c + 2 < NC else [(SPLIT + c + 2 - NC, 0)], 2))
+        for c in range(SPLIT, NC, 2):
+            steps.append(([(thx, c)] + ([(ex, NC - 1)] if c == SPLIT else []) + [(thx, c + 1)], [(q, 0) for q in (c + 2, c + 3) if q < NC], 2))
+        ready = {}
+        for h in range(H):
+            first = NT * h < SPLIT
+            for u in range(2):
+                ready.setdefault(NT * h + NT - 1 if first else NC + (NT * h + 2 * u - SPLIT) // 2, []).append(("g", h, u))
+            ready.setdefault(NT * h + NT - 1 if first else NT * h + NT, []).extend([("t", h * NA + a) for a in range(NA)])
+        sq_step = {6: (0, 1, 2), 8: (3, 4), 13: (5, 6), 17: (7, 8, 9)}
+
+        for s, (aops, mxs, budget) in enumerate(steps):
+            for fn, c in aops:
+                fn(c)
+            hp = s // 2 + 1
+            if s == 1:
                 xev(1, 0)
                 xev(1, 1)
-            if c == 0:
+            if s == 0:
                 for tt in (2, 3):
                     wintq(0, 1, tt)
                     wintq(0, 0, tt)
                     wqq(0, 1, tt)
                     wqq(0, 0, tt)
-            if hp < H and c % 2 == 0:
+            if hp < H and s % 2 == 0:
                 wint(hp, 1)
                 wint(hp, 0)
                 if XEVAC[hp] == "V":
                     xev(hp, 0)
                     xev(hp, 1)
-            if hp < H and c % 2 == 1:
+            if hp < H and s % 2 == 1:
                 wq(hp, 1)
                 wq(hp, 0)
                 xq(hp)
-            for hh in range(H):
-                if c == max(2 * (H - 1), NT * hh + NT):
-                    for j in SQ_ON_POOL:
-                        if UNITS[j][0] == hh:
-                            sqr(j)
-            if c >= R2_FROM:
-                regime2(R2_RATE)
-            if c + 2 < H * NT:
-                mx(c + 2)
-            if hp + 1 < H and c % 2 == 1:
+            for j in sq_step.get(s, ()):
+                sqr(j)
+            work.extend(ready.get(s, []))
+            work[:] = [task for task in work if task[0] == "g"] + [task for task in work if task[0] != "g"]
+            if s >= R2_FROM:
+                regime2_v()
+                if s >= NC:
+                    for c, g in mxs:
+                        mx(c, g)
+                    mxs = []
+                regime2_pe(budget)
+            for c, g in mxs:
+                mx(c, g)
+            if hp + 1 < H and s % 2 == 1:
                 x_t(hp + 1, 0)
                 x_t(hp + 1, 1)
-            if c == 1:
+            if s == 1:
                 keep_warm(WARM_GAP, 2 * P, False)
-            if t == NT - 1:
-                work.extend([("g", h, 0), ("g", h, 1)] + [("t", h * NA + a) for a in range(NA)])
 
         n = len(UNITS)
-        act_sq = [j for j in range(n) if j not in SQ_ON_POOL]
         for s in range(n + LAG_CA + 1):
-            if s == 0 and 0 in act_sq:
-                sqr(0)
-            if s + 1 in act_sq:
-                sqr(s + 1)
             if s < n:
                 sqrt(s)
             regime2(R2_RATE)

@@ -24,10 +24,11 @@ Y_SCALE = 280.0
 XEVAC = ("V", "S", "V", "V")
 UNITS = ((0, 0, 1), (0, 1, 1), (0, 2, 2), (1, 0, 2), (1, 2, 2), (2, 0, 2), (2, 2, 2), (3, 0, 2), (3, 2, 1), (3, 3, 1))
 CAST_ON_ACT = (0, 1, 2, 3, 4, 5, 6, 7)
-T3C_ON_POOL = (0, 1, 2, 4, 5, 7)
+T3C_ON_POOL = (0, 1, 2, 3, 4, 5, 7, 8)
 WINT_ON_POOL = ()
-SPLIT = 8
-R2_FROM = 9
+T3C_FROM_PSUM = (6,)
+SQ_ON_POOL = (0, 1, 2, 3, 4, 5)
+R2_FROM = 10
 R2_RATE = 2
 LAG_CA = 4
 LAG_T3C = 1
@@ -38,6 +39,7 @@ LAG_CAST = 4
 WARM_HEAD = 1
 WARM_MID = 3
 WARM_GAP = 2
+GA, GB = 1.36, 0.71
 
 
 def tile_rglru_kernel(tc, x, state, w_in, b_in, w_a, b_a, a_param, out_0, out_1):
@@ -59,8 +61,6 @@ def tile_rglru_kernel(tc, x, state, w_in, b_in, w_a, b_a, a_param, out_0, out_1)
         nc.vector.memset(zeros[:], 0.0)
         warm = const.tile([P, 1], F32, name="warm")
         nc.vector.memset(warm[:], 0.0)
-        one = const.tile([P, 1], F32, name="one")
-        nc.vector.memset(one[:], 1.0)
         quarter = const.tile([P, 1], F32, name="quarter")
         nc.vector.memset(quarter[:], 0.25)
         vecs = const.tile([P, 3, H * NT], BF16, name="vecs")
@@ -92,8 +92,8 @@ def tile_rglru_kernel(tc, x, state, w_in, b_in, w_a, b_a, a_param, out_0, out_1)
             xn[h] = xin.tile([P, NA, HD], BF16, tag="xn", name="xn%d" % h)
             src = x[:, h * HD:(h + 1) * HD].rearrange("(a p) c -> p a c", p=P)
             if h == 0:
-                nc.sync.dma_start(out=xn[h][:, 0:2, :], in_=src[:, 0:2, :])
-                nc.sync.dma_start(out=xn[h][:, 2:4, :], in_=src[:, 2:4, :])
+                for a in range(NA):
+                    nc.sync.dma_start(out=xn[h][:, a, :], in_=src[:, a, :])
             else:
                 nc.sync.dma_start(out=xn[h][:], in_=src)
 
@@ -115,20 +115,36 @@ def tile_rglru_kernel(tc, x, state, w_in, b_in, w_a, b_a, a_param, out_0, out_1)
             load_st(h)
 
         v = vecs[:, 2, :]
-        av = const.tile([P, H * NT], F32, name="av")
-        nc.vector.scalar_tensor_tensor(out=av[:], in0=v, scalar=-1.0, in1=v, op0=ALU.mult, op1=ALU.max)
-        ex_t = const.tile([P, H * NT], F32, name="ex_t")
-        nc.scalar.activation(out=ex_t[:], in_=av[:], func=ACT.Exp, scale=-1.0)
-        ln = const.tile([P, H * NT], F32, name="ln")
-        nc.scalar.activation(out=ln[:], in_=ex_t[:], func=ACT.Ln, bias=one[:, 0:1], scale=1.0)
         hb = const.tile([P, 2, H * NT], F32, name="hb")
-        nc.vector.tensor_scalar(out=hb[:], in0=vecs[:, 0:2, :], scalar1=0.5, scalar2=None, op0=ALU.mult)
-        sp = const.tile([P, H * NT], F32, name="sp")
         ch = const.tile([P, H * NT], F32, name="ch")
+        sm = {}
+        for nm in ("av", "w", "t", "y0", "e1", "pa", "y1", "e2", "pb", "qa", "qb"):
+            sm[nm] = const.tile([P, H * NT], F32, name="sm_" + nm)
 
-        def softplus_tail():
-            nc.vector.scalar_tensor_tensor(out=sp[:], in0=v, scalar=0.0, in1=ln[:], op0=ALU.max, op1=ALU.add)
-            nc.vector.tensor_scalar(out=ch[:], in0=sp[:], scalar1=-4.0, scalar2=None, op0=ALU.mult)
+        def stt(out, in0, scalar, in1, op0, op1):
+            nc.vector.scalar_tensor_tensor(out=out, in0=in0, scalar=scalar, in1=in1, op0=op0, op1=op1)
+
+        def small_act(out, in_, func, scale):
+            nc.scalar.activation(out=sm[out][:], in_=in_, func=func, scale=scale)
+
+        small = {
+            "av": lambda: small_act("av", v, ACT.Abs, 1.0),
+            "w": lambda: small_act("w", sm["av"][:], ACT.Exp, -1.0),
+            "t": lambda: small_act("t", sm["w"][:], ACT.Exp, -GB),
+            "y0": lambda: nc.scalar.activation(out=sm["y0"][:], in_=sm["t"][:], func=ACT.Copy, scale=-GA, bias=GA),
+            "e1": lambda: small_act("e1", sm["y0"][:], ACT.Exp, -1.0),
+            "pa": lambda: stt(sm["pa"][:], sm["w"][:], 1.0, sm["e1"][:], ALU.add, ALU.mult),
+            "y1": lambda: stt(sm["y1"][:], sm["pa"][:], -1.0, sm["y0"][:], ALU.add, ALU.add),
+            "e2": lambda: small_act("e2", sm["y1"][:], ACT.Exp, -1.0),
+            "qa": lambda: stt(sm["qa"][:], v, 0.0, sm["y1"][:], ALU.max, ALU.add),
+            "qb": lambda: nc.vector.tensor_scalar(
+                out=sm["qb"][:], in0=sm["qa"][:], scalar1=-1.0, scalar2=-4.0, op0=ALU.add, op1=ALU.mult),
+            "pb": lambda: stt(sm["pb"][:], sm["w"][:], 1.0, sm["e2"][:], ALU.add, ALU.mult),
+            "ch": lambda: stt(ch[:], sm["pb"][:], -4.0, sm["qb"][:], ALU.mult, ALU.add),
+        }
+
+        def half_biases():
+            nc.scalar.activation(out=hb[:], in_=vecs[:, 0:2, :], func=ACT.Copy, scale=0.5)
 
         xg = [keep.tile([P, 4 * B], BF16, name="xg%d" % h, align_bytes=64) for h in range(H)]
         xc = [keep.tile([P, B], U32, name="xc%d" % h, align_bytes=64) for h in range(H)]
@@ -148,7 +164,6 @@ def tile_rglru_kernel(tc, x, state, w_in, b_in, w_a, b_a, a_param, out_0, out_1)
         acc = {}
         ats = {}
         sqs = {}
-        sqt = {}
         ots = {}
 
         def x_t(h, half):
@@ -159,14 +174,21 @@ def tile_rglru_kernel(tc, x, state, w_in, b_in, w_a, b_a, a_param, out_0, out_1)
                 for u in range(2):
                     nc.tensor.transpose(xt[:, a, u, :], words[:, u:HD // 2:2], ident[:])
 
-        def xev(h, half):
+        def xev(h, half, eng=None):
             xgw = xg[h][:].bitcast(F32).rearrange("p (a r u) -> p a r u", a=NA, u=2)
             dst = xgw[:, 2 * half:2 * half + 2, :, :]
             src = xts[(h, half)][:].rearrange("p a u r -> p a r u")
-            if XEVAC[h] == "V":
+            if (eng or XEVAC[h]) == "V":
                 nc.vector.tensor_copy(out=dst, in_=src)
             else:
                 nc.scalar.copy(out=dst, in_=src)
+
+        def xqh(h, half):
+            nc.vector.quantize_mx(
+                out=xc[h][:, half * (B // 2):(half + 1) * (B // 2)].bitcast(FP8X4),
+                scales=xs[h][:, half * (B // 2):(half + 1) * (B // 2)],
+                in_=xg[h][:, half * 2 * B:(half + 1) * 2 * B],
+            )
 
         def xq(h):
             nc.vector.quantize_mx(out=xc[h][:].bitcast(FP8X4), scales=xs[h][:], in_=xg[h][:])
@@ -188,12 +210,29 @@ def tile_rglru_kernel(tc, x, state, w_in, b_in, w_a, b_a, a_param, out_0, out_1)
         def wq(h, g):
             nc.vector.quantize_mx(out=wc[h][g][:].bitcast(FP8X4), scales=ws[h][g][:], in_=wgs[(h, g)][:])
 
-        def wintq(h, g, t):
+        def wintq(h, g, t, on_act=False):
             if t == 0:
                 new_wg(h, g)
             dst = wgs[(h, g)][:, t * HD:(t + 1) * HD].rearrange("p (m j) -> p m j", j=4)
             src = raw[h][g][:].rearrange("p j (m t) -> p t m j", t=NT)[:, t, :, :]
+            if on_act:
+                nc.scalar.copy(out=dst, in_=src)
+            else:
+                nc.vector.tensor_copy(out=dst, in_=src)
+
+        def winth(h, g, half):
+            if (h, g) not in wgs:
+                new_wg(h, g)
+            dst = wgs[(h, g)][:, half * 2 * HD:(half + 1) * 2 * HD].rearrange("p (t m j) -> p m j t", t=2, j=4)
+            src = raw[h][g][:].rearrange("p j (m t) -> p m j t", t=NT)[:, :, :, 2 * half:2 * half + 2]
             nc.vector.tensor_copy(out=dst, in_=src)
+
+        def wqh(h, g, half):
+            cols = slice(half * 2 * P, (half + 1) * 2 * P)
+            nc.vector.quantize_mx(
+                out=wc[h][g][:, cols].bitcast(FP8X4), scales=ws[h][g][:, cols],
+                in_=wgs[(h, g)][:, half * 2 * HD:(half + 1) * 2 * HD],
+            )
 
         def wqq(h, g, t):
             cols = slice(t * P, (t + 1) * P)
@@ -202,28 +241,31 @@ def tile_rglru_kernel(tc, x, state, w_in, b_in, w_a, b_a, a_param, out_0, out_1)
                 in_=wgs[(h, g)][:, t * HD:(t + 1) * HD],
             )
 
-        def mx(c, g):
+        def mx(c):
             h, t = c // NT, c % NT
             cols = slice(t * P, (t + 1) * P)
-            ps = pmx.tile([P, B], F32, tag="ps%d" % (g if c < SPLIT else c % 2), name="ps%d_%d" % (g, c))
-            nc.tensor.matmul_mx(
-                out=ps[:],
-                lhsT=wc[h][g][:, cols].bitcast(FP8X4),
-                lhsT_scale=ws[h][g][:, cols],
-                rhs=xc[h][:].bitcast(FP8X4),
-                rhs_scale=xs[h][:],
-                start=True,
-                stop=True,
-            )
-            acc[(c, g)] = ps
+            pair = [None, None]
+            for g in (1, 0):
+                ps = pmx.tile([P, B], F32, tag="ps%d" % g, name="ps%d_%d" % (g, c))
+                nc.tensor.matmul_mx(
+                    out=ps[:],
+                    lhsT=wc[h][g][:, cols].bitcast(FP8X4),
+                    lhsT_scale=ws[h][g][:, cols],
+                    rhs=xc[h][:].bitcast(FP8X4),
+                    rhs_scale=xs[h][:],
+                    start=True,
+                    stop=True,
+                )
+                pair[g] = ps
+            acc[c] = pair
 
         def thx(c):
             h, t = c // NT, c % NT
-            nc.scalar.activation(out=gx[h][:, t, :], in_=acc[(c, 0)][:], func=ACT.Tanh, bias=hb[:, 0, c:c + 1], scale=0.5)
+            nc.scalar.activation(out=gx[h][:, t, :], in_=acc[c][0][:], func=ACT.Tanh, bias=hb[:, 0, c:c + 1], scale=0.5)
 
         def tha(c):
             h, t = c // NT, c % NT
-            nc.scalar.activation(out=ae[h][:, t, :], in_=acc[(c, 1)][:], func=ACT.Tanh, bias=hb[:, 1, c:c + 1], scale=0.5)
+            nc.scalar.activation(out=ae[h][:, t, :], in_=acc[c][1][:], func=ACT.Tanh, bias=hb[:, 1, c:c + 1], scale=0.5)
 
         def ex(c):
             h, t = c // NT, c % NT
@@ -269,11 +311,13 @@ def tile_rglru_kernel(tc, x, state, w_in, b_in, w_a, b_a, a_param, out_0, out_1)
 
         def sqr(j):
             h, a0, k = UNITS[j]
-            if a0 % 2 == 0:
-                sqt[(h, a0 // 2)] = win.tile([P, NT, 2 * P], F32, tag="raw", name="sq%d" % j)
-            sqs[j] = sqt[(h, a0 // 2)][:, :, (a0 % 2) * P:(a0 % 2 + k) * P]
+            sq = win.tile([P, NT, k * P], F32, tag="raw", name="sq%d" % j)
+            sqs[j] = sq[:]
             a = ae[h][:, :, a0 * P:(a0 + k) * P]
-            nc.gpsimd.tensor_tensor(out=sqs[j], in0=a, in1=a, op=ALU.mult)
+            if j in SQ_ON_POOL:
+                nc.gpsimd.tensor_tensor(out=sqs[j], in0=a, in1=a, op=ALU.mult)
+            else:
+                nc.scalar.activation(out=sqs[j], in_=a, func=ACT.Square)
 
         def sqrt(j):
             nc.scalar.activation(out=sqs[j], in_=sqs[j], func=ACT.Sqrt, bias=quarter[:, 0:1], scale=-0.25)
@@ -282,6 +326,22 @@ def tile_rglru_kernel(tc, x, state, w_in, b_in, w_a, b_a, a_param, out_0, out_1)
             h, a0, k = UNITS[j]
             eng = nc.gpsimd if j in T3C_ON_POOL else nc.vector
             eng.tensor_tensor(out=sqs[j], in0=gx[h][:, :, a0 * P:(a0 + k) * P], in1=sqs[j], op=ALU.mult)
+
+        gps = {}
+
+        def g_copy(j, u):
+            h, a0, k = UNITS[j]
+            gp = ptr.tile([P, 2, k * P], F32, tag="tr", name="gp%d_%d" % (j, u))
+            gps[(j, u)] = gp
+            for e in range(2):
+                nc.tensor.matmul(
+                    gp[:, e, :], lhsT=ident[:], rhs=gx[h][:, 2 * u + e, a0 * P:(a0 + k) * P], start=True, stop=True
+                )
+
+        def t3c_psum(j):
+            for u in range(2):
+                r = sqs[j][:, 2 * u:2 * u + 2, :]
+                nc.vector.tensor_tensor(out=r, in0=gps[(j, u)][:], in1=r, op=ALU.mult)
 
         def o_t(v):
             j, i = unit_of[v]
@@ -332,28 +392,32 @@ def tile_rglru_kernel(tc, x, state, w_in, b_in, w_a, b_a, a_param, out_0, out_1)
         x_t(0, 0)
         x_t(0, 1)
         keep_warm(WARM_MID, 2 * P, True)
-        xev(0, 0)
-        xev(0, 1)
+        xev(0, 0, "V")
+        xev(0, 1, "S")
+        small["av"]()
         wintq(0, 1, 0)
-        xq(0)
+        xqh(0, 0)
+        xqh(0, 1)
+        wintq(0, 1, 1, True)
+        small["w"]()
         wqq(0, 1, 0)
         wintq(0, 0, 0)
-        wintq(0, 1, 1)
-        wqq(0, 0, 0)
-        softplus_tail()
-        wintq(0, 0, 1)
+        wintq(0, 0, 1, True)
+        small["t"]()
+        half_biases()
+        small["y0"]()
+        small["e1"]()
         wqq(0, 1, 1)
+        wqq(0, 0, 0)
         wqq(0, 0, 1)
-        mx(0, 1)
-        mx(0, 0)
-        mx(1, 1)
-        mx(1, 0)
+        winth(0, 1, 1)
+        mx(0)
+        mx(1)
         x_t(1, 0)
         x_t(1, 1)
 
         work = []
         pend = []
-        cost = {"g": 2, "t": 1}
 
         def pe_part(task):
             if task[0] == "g":
@@ -367,93 +431,96 @@ def tile_rglru_kernel(tc, x, state, w_in, b_in, w_a, b_a, a_param, out_0, out_1)
             else:
                 t1(task[1])
 
-        def regime2_v():
+        def regime2(rate):
             for task in pend:
                 dve_part(task)
             pend.clear()
-
-        def regime2_pe(budget):
-            while work and budget > 0:
-                task = work.pop(0)
-                budget -= cost[task[0]]
-                pe_part(task)
-                pend.append(task)
-
-        def regime2(rate):
-            regime2_v()
             for i in range(rate):
                 if work:
                     task = work.pop(0)
                     pe_part(task)
                     pend.append(task)
 
-        NC = H * NT
-        steps = []
-        for c in range(SPLIT):
-            steps.append(([(tha, c), (thx, c), (ex, c)], [(c + 2, 1), (c + 2, 0)] if c + 2 < SPLIT else [(c + 2, 1)], 3))
-        for c in range(SPLIT, NC):
-            steps.append(([(tha, c)] + ([(ex, c - 1)] if c > SPLIT else []), [(c + 2, 1)] if c + 2 < NC else [(SPLIT + c + 2 - NC, 0)], 2))
-        for c in range(SPLIT, NC, 2):
-            steps.append(([(thx, c)] + ([(ex, NC - 1)] if c == SPLIT else []) + [(thx, c + 1)], [(q, 0) for q in (c + 2, c + 3) if q < NC], 2))
-        ready = {}
-        for h in range(H):
-            first = NT * h < SPLIT
-            for u in range(2):
-                ready.setdefault(NT * h + NT - 1 if first else NC + (NT * h + 2 * u - SPLIT) // 2, []).append(("g", h, u))
-            ready.setdefault(NT * h + NT - 1 if first else NT * h + NT, []).extend([("t", h * NA + a) for a in range(NA)])
-        sq_step = {6: (0, 1, 2), 8: (3, 4), 13: (5, 6), 17: (7, 8, 9)}
-
-        for s, (aops, mxs, budget) in enumerate(steps):
-            for fn, c in aops:
-                fn(c)
-            hp = s // 2 + 1
-            if s == 1:
+        for c in range(H * NT):
+            h, t = c // NT, c % NT
+            tha(c)
+            thx(c)
+            if c == 3:
+                ex(0)
+                ex(1)
+                ex(2)
+            if c > 2:
+                ex(c)
+            hp = c // 2 + 1
+            if c == 1:
                 xev(1, 0)
                 xev(1, 1)
-            if s == 0:
-                for tt in (2, 3):
-                    wintq(0, 1, tt)
-                    wintq(0, 0, tt)
-                    wqq(0, 1, tt)
-                    wqq(0, 0, tt)
-            if hp < H and s % 2 == 0:
+                small["e2"]()
+            if c == 0:
+                winth(0, 0, 1)
+                wqh(0, 1, 1)
+                wqh(0, 0, 1)
+                small["pa"]()
+                winth(1, 1, 0)
+                small["y1"]()
+                winth(1, 0, 0)
+                small["qa"]()
+            if c == 1:
+                wqh(1, 1, 0)
+                small["qb"]()
+                wqh(1, 0, 0)
+                small["pb"]()
+                winth(1, 1, 1)
+                small["ch"]()
+                xq(1)
+                winth(1, 0, 1)
+            if c == 2:
+                wqh(1, 1, 1)
+                wqh(1, 0, 1)
+            if 1 < hp < H and c % 2 == 0:
                 wint(hp, 1)
                 wint(hp, 0)
                 if XEVAC[hp] == "V":
                     xev(hp, 0)
                     xev(hp, 1)
-            if hp < H and s % 2 == 1:
+            if 1 < hp < H and c % 2 == 1:
                 wq(hp, 1)
                 wq(hp, 0)
                 xq(hp)
-            for j in sq_step.get(s, ()):
-                sqr(j)
-            work.extend(ready.get(s, []))
-            work[:] = [task for task in work if task[0] == "g"] + [task for task in work if task[0] != "g"]
-            if s >= R2_FROM:
-                regime2_v()
-                if s >= NC:
-                    for c, g in mxs:
-                        mx(c, g)
-                    mxs = []
-                regime2_pe(budget)
-            for c, g in mxs:
-                mx(c, g)
-            if hp + 1 < H and s % 2 == 1:
+            for hh in range(H):
+                if c == max(2 * (H - 1), NT * hh + NT):
+                    for j in SQ_ON_POOL:
+                        if UNITS[j][0] == hh:
+                            sqr(j)
+            if c >= R2_FROM:
+                regime2(R2_RATE)
+            if c + 2 < H * NT:
+                mx(c + 2)
+            if hp + 1 < H and c % 2 == 1:
                 x_t(hp + 1, 0)
                 x_t(hp + 1, 1)
-            if s == 1:
+            if c == 1:
                 keep_warm(WARM_GAP, 2 * P, False)
+            if t == NT - 1:
+                work.extend([("g", h, 0), ("g", h, 1)] + [("t", h * NA + a) for a in range(NA)])
 
         n = len(UNITS)
+        act_sq = [j for j in range(n) if j not in SQ_ON_POOL]
         for s in range(n + LAG_CA + 1):
+            if s == 0 and 0 in act_sq:
+                sqr(0)
+            if s + 1 in act_sq:
+                sqr(s + 1)
             if s < n:
                 sqrt(s)
             regime2(R2_RATE)
             if 0 <= s - LAG_T3C < n and (s - LAG_T3C) in T3C_ON_POOL:
                 t3c(s - LAG_T3C)
             if 0 <= s - LAG_T3V < n and (s - LAG_T3V) not in T3C_ON_POOL:
-                t3c(s - LAG_T3V)
+                if s - LAG_T3V in T3C_FROM_PSUM:
+                    t3c_psum(s - LAG_T3V)
+                else:
+                    t3c(s - LAG_T3V)
             if 0 <= s - LAG_ADD < n:
                 for v in tiles(s - LAG_ADD):
                     add(v)
@@ -465,5 +532,11 @@ def tile_rglru_kernel(tc, x, state, w_in, b_in, w_a, b_a, a_param, out_0, out_1)
             if 0 <= s - LAG_OT < n:
                 for v in tiles(s - LAG_OT):
                     o_t(v)
-            if s < n + LAG_OT:
+            if s + 3 - LAG_T3V in T3C_FROM_PSUM:
+                g_copy(s + 3 - LAG_T3V, 0)
+            elif s + 2 - LAG_T3V in T3C_FROM_PSUM:
+                g_copy(s + 2 - LAG_T3V, 1)
+            elif s + 4 - LAG_T3V in T3C_FROM_PSUM or s + 1 - LAG_T3V in T3C_FROM_PSUM:
+                pass
+            elif s < n + LAG_OT:
                 keep_warm(1, 2 * P, False)

@@ -57,6 +57,8 @@ def tile_rglru_kernel(tc, x, state, w_in, b_in, w_a, b_a, a_param, out_0, out_1)
         ptr = ctx.enter_context(tc.psum_pool(name="ptr", bufs=4))
         ctx.enter_context(tc.manual_schedule())
 
+        vrow = const.tile([P, P], BF16, name="vrow")
+        nc.vector.memset(vrow[:], 0.0)
         zeros = const.tile([P, 2 * P], F32, name="zeros")
         nc.vector.memset(zeros[:], 0.0)
         warm = const.tile([P, 1], F32, name="warm")
@@ -64,25 +66,18 @@ def tile_rglru_kernel(tc, x, state, w_in, b_in, w_a, b_a, a_param, out_0, out_1)
         quarter = const.tile([P, 1], F32, name="quarter")
         nc.vector.memset(quarter[:], 0.25)
         vecs = const.tile([P, 3, H * NT], BF16, name="vecs")
-        with nc.allow_non_contiguous_dma(reason="three small per-channel vectors, 8-byte runs"):
-            nc.scalar.dma_start(
-                out=vecs[:, 2, :].rearrange("p (h t) -> p h t", t=NT),
-                in_=a_param.rearrange("(h p t) -> p h t", h=H, t=NT),
-            )
-            nc.scalar.dma_start(
-                out=vecs[:, 0, :].rearrange("p (h t) -> p h t", t=NT),
-                in_=b_in.rearrange("h (p t) -> p h t", t=NT),
-            )
-            nc.scalar.dma_start(
-                out=vecs[:, 1, :].rearrange("p (h t) -> p h t", t=NT),
-                in_=b_a.rearrange("h (p t) -> p h t", t=NT),
-            )
+        NC = H * NT
+        nc.scalar.dma_start(out=vrow[2 * NC:3 * NC, :], in_=a_param.rearrange("(c m) -> c m", m=P))
+        nc.scalar.dma_start(out=vrow[0:NC, :], in_=b_in.rearrange("h (t m) -> (h t) m", m=P))
+        nc.scalar.dma_start(out=vrow[NC:2 * NC, :], in_=b_a.rearrange("h (t m) -> (h t) m", m=P))
 
         warm2 = const.tile([P, 1], F32, name="warm2")
         nc.scalar.activation(out=warm2[:], in_=warm[:], func=ACT.Exp)
 
         ident = const.tile([P, P], F32, name="ident")
         make_identity(nc, ident[:])
+        ident_bf = const.tile([P, P], BF16, name="ident_bf")
+        make_identity(nc, ident_bf[:])
 
         xn = [None] * H
         raw = [[None, None] for h in range(H)]
@@ -203,8 +198,8 @@ def tile_rglru_kernel(tc, x, state, w_in, b_in, w_a, b_a, a_param, out_0, out_1)
                 src = raw[h][g][:].rearrange("p j (m t) -> p t m j", t=NT)
                 nc.gpsimd.tensor_scalar(out=dst, in0=src, scalar1=1.0, scalar2=0.0, op0=ALU.mult, op1=ALU.add)
             else:
-                dst = wgs[(h, g)][:].rearrange("p (t m j) -> p m j t", t=NT, j=4)
-                src = raw[h][g][:].rearrange("p j (m t) -> p m j t", t=NT)
+                dst = wgs[(h, g)][:].rearrange("p (c i j) -> p c j i", i=4, j=4)
+                src = raw[h][g][:].rearrange("p j (c i) -> p c j i", i=4)
                 nc.vector.tensor_copy(out=dst, in_=src)
 
         def wq(h, g):
@@ -213,8 +208,8 @@ def tile_rglru_kernel(tc, x, state, w_in, b_in, w_a, b_a, a_param, out_0, out_1)
         def wintq(h, g, t, on_act=False):
             if t == 0:
                 new_wg(h, g)
-            dst = wgs[(h, g)][:, t * HD:(t + 1) * HD].rearrange("p (m j) -> p m j", j=4)
-            src = raw[h][g][:].rearrange("p j (m t) -> p t m j", t=NT)[:, t, :, :]
+            dst = wgs[(h, g)][:, t * HD:(t + 1) * HD].rearrange("p (c i j) -> p c j i", i=4, j=4)
+            src = raw[h][g][:, :, t * P:(t + 1) * P].rearrange("p j (c i) -> p c j i", i=4)
             if on_act:
                 nc.scalar.copy(out=dst, in_=src)
             else:
@@ -223,8 +218,8 @@ def tile_rglru_kernel(tc, x, state, w_in, b_in, w_a, b_a, a_param, out_0, out_1)
         def winth(h, g, half):
             if (h, g) not in wgs:
                 new_wg(h, g)
-            dst = wgs[(h, g)][:, half * 2 * HD:(half + 1) * 2 * HD].rearrange("p (t m j) -> p m j t", t=2, j=4)
-            src = raw[h][g][:].rearrange("p j (m t) -> p m j t", t=NT)[:, :, :, 2 * half:2 * half + 2]
+            dst = wgs[(h, g)][:, half * 2 * HD:(half + 1) * 2 * HD].rearrange("p (c i j) -> p c j i", i=4, j=4)
+            src = raw[h][g][:, :, half * 2 * P:(half + 1) * 2 * P].rearrange("p j (c i) -> p c j i", i=4)
             nc.vector.tensor_copy(out=dst, in_=src)
 
         def wqh(h, g, half):
@@ -271,26 +266,19 @@ def tile_rglru_kernel(tc, x, state, w_in, b_in, w_a, b_a, a_param, out_0, out_1)
             h, t = c // NT, c % NT
             nc.scalar.activation(out=ae[h][:, t, :], in_=ae[h][:, t, :], func=ACT.Exp, bias=ch[:, c:c + 1], scale=ch[:, c:c + 1])
 
-        def gxx(h):
-            nc.vector.scalar_tensor_tensor(
-                out=gx[h][:], in0=gx[h][:], scalar=1.0,
-                in1=xg[h][:].rearrange("p (r t) -> p t r", t=NT),
-                op0=ALU.add, op1=ALU.mult,
-            )
-
         xus = {}
 
         def x_t2(h, u):
-            xu = ptr.tile([P, NA, P], F32, tag="tr", name="xu%d_%d" % (h, u))
+            xu = ptr.tile([P, 2, B], BF16, tag="tr", name="xu%d_%d" % (h, u))
             xus[(h, u)] = xu
-            for a in range(NA):
-                words = xn[h][:, a, :].bitcast(F32)
-                nc.tensor.transpose(xu[:, a, :], words[:, u:HD // 2:2], ident[:])
+            for e in range(2):
+                t = 2 * u + e
+                for a in range(NA):
+                    nc.tensor.transpose(xu[:, e, a * P:(a + 1) * P], xn[h][:, a, t * P:(t + 1) * P], ident_bf[:])
 
         def gxx2(h, u):
             g = gx[h][:, 2 * u:2 * u + 2, :]
-            xv = xus[(h, u)][:].rearrange("p a r -> p (a r)").bitcast(BF16).rearrange("p (q e) -> p e q", e=2)
-            nc.vector.scalar_tensor_tensor(out=g, in0=g, scalar=1.0, in1=xv, op0=ALU.add, op1=ALU.mult)
+            nc.vector.scalar_tensor_tensor(out=g, in0=g, scalar=1.0, in1=xus[(h, u)][:], op0=ALU.add, op1=ALU.mult)
 
         def a_t(u):
             h, a = u // NA, u % NA
@@ -303,9 +291,9 @@ def tile_rglru_kernel(tc, x, state, w_in, b_in, w_a, b_a, a_param, out_0, out_1)
             h, a = v // NA, v % NA
             j, i = unit_of[v]
             nc.vector.tensor_tensor(
-                out=t1u[j][:, i, :].rearrange("p (m t) -> p m t", t=NT),
-                in0=ats[v][:].rearrange("p t m -> p m t"),
-                in1=st[h][:, a, :].rearrange("p (m t) -> p m t", t=NT),
+                out=t1u[j][:, i, :],
+                in0=ats[v][:].rearrange("p t m -> p (t m)"),
+                in1=st[h][:, a, :],
                 op=ALU.mult,
             )
 
@@ -361,9 +349,9 @@ def tile_rglru_kernel(tc, x, state, w_in, b_in, w_a, b_a, a_param, out_0, out_1)
         def add(v):
             j, i = unit_of[v]
             nc.vector.tensor_tensor(
-                out=t1u[j][:, i, :].rearrange("p (m t) -> p m t", t=NT),
-                in0=ots[v][:].rearrange("p t m -> p m t"),
-                in1=t1u[j][:, i, :].rearrange("p (m t) -> p m t", t=NT),
+                out=t1u[j][:, i, :],
+                in0=ots[v][:].rearrange("p t m -> p (t m)"),
+                in1=t1u[j][:, i, :],
                 op=ALU.add,
             )
 
@@ -391,9 +379,12 @@ def tile_rglru_kernel(tc, x, state, w_in, b_in, w_a, b_a, a_param, out_0, out_1)
         keep_warm(WARM_HEAD, 2 * P, True)
         x_t(0, 0)
         x_t(0, 1)
+        vt = ptr.tile([P, P], BF16, tag="tr", name="vt")
+        nc.tensor.transpose(vt[:], vrow[:], ident_bf[:])
         keep_warm(WARM_MID, 2 * P, True)
         xev(0, 0, "V")
         xev(0, 1, "S")
+        nc.scalar.copy(out=vecs[:].rearrange("p i c -> p (i c)"), in_=vt[:, 0:3 * NC])
         small["av"]()
         wintq(0, 1, 0)
         xqh(0, 0)

@@ -58,7 +58,7 @@ def tile_rglru_kernel(tc, x, state, w_in, b_in, w_a, b_a, a_param, out_0, out_1)
         ctx.enter_context(tc.manual_schedule())
 
         vrow = const.tile([P, P], BF16, name="vrow")
-        nc.vector.memset(vrow[:], 0.0)
+        nc.gpsimd.memset(vrow[:], 0.0)
         zeros = const.tile([P, 2 * P], F32, name="zeros")
         nc.vector.memset(zeros[:], 0.0)
         warm = const.tile([P, 1], F32, name="warm")
@@ -492,6 +492,8 @@ def tile_rglru_kernel(tc, x, state, w_in, b_in, w_a, b_a, a_param, out_0, out_1)
                 x_t(hp + 1, 1)
             if c == 1:
                 keep_warm(WARM_GAP, 2 * P, False)
+            if c + 2 >= H * NT:
+                keep_warm(1, 2 * P, False)
             if t == NT - 1:
                 work.extend([("g", h, 0), ("g", h, 1)] + [("t", h * NA + a) for a in range(NA)])
 
@@ -527,7 +529,5 @@ def tile_rglru_kernel(tc, x, state, w_in, b_in, w_a, b_a, a_param, out_0, out_1)
                 g_copy(s + 3 - LAG_T3V, 0)
             elif s + 2 - LAG_T3V in T3C_FROM_PSUM:
                 g_copy(s + 2 - LAG_T3V, 1)
-            elif s + 4 - LAG_T3V in T3C_FROM_PSUM or s + 1 - LAG_T3V in T3C_FROM_PSUM:
-                pass
             elif s < n + LAG_OT:
                 keep_warm(1, 2 * P, False)

@@ -24,10 +24,10 @@ Y_SCALE = 280.0
 XEVAC = ("V", "S", "V", "V")
 UNITS = ((0, 0, 1), (0, 1, 1), (0, 2, 2), (1, 0, 2), (1, 2, 2), (2, 0, 2), (2, 2, 2), (3, 0, 2), (3, 2, 1), (3, 3, 1))
 CAST_ON_ACT = (0, 1, 2, 3, 4, 5, 6, 7)
-T3C_ON_POOL = (0, 1, 2, 3, 4, 5, 7, 8)
+T3C_ON_POOL = (0, 1, 2, 3, 4, 5, 7)
 WINT_ON_POOL = ()
 T3C_FROM_PSUM = (6,)
-SQ_ON_POOL = (0, 1, 2, 3, 4, 5)
+SQ_ON_POOL = (0, 1, 2, 3, 4, 5, 6)
 R2_FROM = 10
 R2_RATE = 2
 LAG_CA = 4

@@ -24,13 +24,13 @@ Y_SCALE = 280.0
 XEVAC = ("V", "S", "V", "V")
 UNITS = ((0, 0, 1), (0, 1, 1), (0, 2, 2), (1, 0, 2), (1, 2, 2), (2, 0, 2), (2, 2, 2), (3, 0, 2), (3, 2, 1), (3, 3, 1))
 CAST_ON_ACT = (0, 1, 2, 3, 4, 5, 6, 7)
-T3C_ON_POOL = (0, 1, 2, 3, 4, 5, 7)
+T3C_ON_POOL = (0, 1, 2, 4, 5, 7, 8)
 WINT_ON_POOL = ()
-T3C_FROM_PSUM = (6,)
+T3C_FROM_PSUM = (3, 6)
 SQ_ON_POOL = (0, 1, 2, 3, 4, 5, 6)
-R2_FROM = 10
+R2_FROM = 8
 R2_RATE = 2
-LAG_CA = 4
+LAG_CA = 5
 LAG_T3C = 1
 LAG_T3V = 2
 LAG_OT = 2

@@ -22,12 +22,12 @@ NA = 4
 Y_SCALE = 280.0
 
 XEVAC = ("V", "S", "V", "V")
-UNITS = ((0, 0, 1), (0, 1, 1), (0, 2, 2), (1, 0, 2), (1, 2, 2), (2, 0, 2), (2, 2, 2), (3, 0, 2), (3, 2, 1), (3, 3, 1))
+UNITS = ((0, 0, 1), (0, 1, 1), (1, 0, 2), (2, 0, 2), (3, 0, 2), (0, 2, 2), (1, 2, 2), (2, 2, 2), (3, 2, 1), (3, 3, 1))
 CAST_ON_ACT = (0, 1, 2, 3, 4, 5, 6, 7)
 T3C_ON_POOL = (0, 1, 2, 4, 5, 7, 8)
 WINT_ON_POOL = ()
 T3C_FROM_PSUM = (3, 6)
-SQ_ON_POOL = (0, 1, 2, 3, 4, 5, 6)
+POOL_HEADS = 3
 R2_FROM = 8
 R2_RATE = 2
 LAG_CA = 5
@@ -146,13 +146,20 @@ def tile_rglru_kernel(tc, x, state, w_in, b_in, w_a, b_a, a_param, out_0, out_1)
         xs = [keep.tile([P, B], U8, name="xs%d" % h, align_bytes=64) for h in range(H)]
         wc = [[keep.tile([P, HD], U32, name="wc%d_%d" % (h, g), align_bytes=64) for g in range(2)] for h in range(H)]
         ws = [[keep.tile([P, HD], U8, name="ws%d_%d" % (h, g), align_bytes=64) for g in range(2)] for h in range(H)]
-        gx = [keep.tile([P, NT, B], F32, name="gx%d" % h) for h in range(H)]
-        ae = [keep.tile([P, NT, B], F32, name="ae%d" % h) for h in range(H)]
-        t1u = [keep.tile([P, k, HD], F32, name="t1_%d" % j) for j, (h, a0, k) in enumerate(UNITS)]
+        gxp = [keep.tile([P, 2 * NT, B], F32, name="gxp%d" % q) for q in range(H // 2)]
+        aep = [keep.tile([P, 2 * NT, B], F32, name="aep%d" % q) for q in range(H // 2)]
+        gx = [gxp[h // 2][:, (h % 2) * NT:(h % 2 + 1) * NT, :] for h in range(H)]
+        ae = [aep[h // 2][:, (h % 2) * NT:(h % 2 + 1) * NT, :] for h in range(H)]
+        t1u = [keep.tile([P, k, HD], F32, name="t1_%d" % j) for j, (a, h0, k) in enumerate(UNITS)]
         unit_of = {}
-        for j, (h, a0, k) in enumerate(UNITS):
+        for j, (a, h0, k) in enumerate(UNITS):
             for i in range(k):
-                unit_of[h * NA + a0 + i] = (j, i)
+                unit_of[(h0 + i) * NA + a] = (j, i)
+
+        def unit_view(pairs, j, i0, n):
+            a, h0, k = UNITS[j]
+            r0 = (h0 % 2 + i0) * NT
+            return pairs[h0 // 2][:, r0:r0 + n * NT, a * P:(a + 1) * P]
 
         xts = {}
         wgs = {}
@@ -297,38 +304,43 @@ def tile_rglru_kernel(tc, x, state, w_in, b_in, w_a, b_a, a_param, out_0, out_1)
                 op=ALU.mult,
             )
 
-        def sqr(j):
-            h, a0, k = UNITS[j]
-            sq = win.tile([P, NT, k * P], F32, tag="raw", name="sq%d" % j)
-            sqs[j] = sq[:]
-            a = ae[h][:, :, a0 * P:(a0 + k) * P]
-            if j in SQ_ON_POOL:
-                nc.gpsimd.tensor_tensor(out=sqs[j], in0=a, in1=a, op=ALU.mult)
+        def sqr(j, i0, n, on_pool):
+            a, h0, k = UNITS[j]
+            if j not in sqs:
+                if j < 8:
+                    sq = win.tile([P, k * NT, P], F32, tag="raw", name="sq%d" % j)
+                else:
+                    sq = wgp.tile([P, k * NT, P], F32, tag="wg", name="sq%d" % j, align_bytes=64)
+                sqs[j] = sq[:]
+            src = unit_view(aep, j, i0, n)
+            dst = sqs[j][:, i0 * NT:(i0 + n) * NT, :]
+            if on_pool:
+                nc.gpsimd.tensor_tensor(out=dst, in0=src, in1=src, op=ALU.mult)
             else:
-                nc.scalar.activation(out=sqs[j], in_=a, func=ACT.Square)
+                nc.scalar.activation(out=dst, in_=src, func=ACT.Square)
 
         def sqrt(j):
             nc.scalar.activation(out=sqs[j], in_=sqs[j], func=ACT.Sqrt, bias=quarter[:, 0:1], scale=-0.25)
 
         def t3c(j):
-            h, a0, k = UNITS[j]
+            a, h0, k = UNITS[j]
             eng = nc.gpsimd if j in T3C_ON_POOL else nc.vector
-            eng.tensor_tensor(out=sqs[j], in0=gx[h][:, :, a0 * P:(a0 + k) * P], in1=sqs[j], op=ALU.mult)
+            eng.tensor_tensor(out=sqs[j], in0=unit_view(gxp, j, 0, k), in1=sqs[j], op=ALU.mult)
 
         gps = {}
 
         def g_copy(j, u):
-            h, a0, k = UNITS[j]
-            gp = ptr.tile([P, 2, k * P], F32, tag="tr", name="gp%d_%d" % (j, u))
+            gp = ptr.tile([P, NT, P], F32, tag="tr", name="gp%d_%d" % (j, u))
             gps[(j, u)] = gp
+            src = unit_view(gxp, j, u, 1)
             for e in range(2):
                 nc.tensor.matmul(
-                    gp[:, e, :], lhsT=ident[:], rhs=gx[h][:, 2 * u + e, a0 * P:(a0 + k) * P], start=True, stop=True
+                    gp[:, 2 * e:2 * e + 2, :], lhsT=ident[:], rhs=src[:, 2 * e:2 * e + 2, :], start=True, stop=True
                 )
 
         def t3c_psum(j):
             for u in range(2):
-                r = sqs[j][:, 2 * u:2 * u + 2, :]
+                r = sqs[j][:, u * NT:(u + 1) * NT, :]
                 nc.vector.tensor_tensor(out=r, in0=gps[(j, u)][:], in1=r, op=ALU.mult)
 
         def o_t(v):
@@ -336,7 +348,7 @@ def tile_rglru_kernel(tc, x, state, w_in, b_in, w_a, b_a, a_param, out_0, out_1)
             tr = pmx.tile([P, NT, P], F32, tag="ps%d" % (v % 2), name="ot%d" % v)
             ots[v] = tr
             for t in range(NT):
-                nc.tensor.transpose(tr[:, t, :], sqs[j][:, t, i * P:(i + 1) * P], ident[:])
+                nc.tensor.transpose(tr[:, t, :], sqs[j][:, i * NT + t, :], ident[:])
 
         def keep_warm(k, n_cols, early):
             for i in range(k):
@@ -356,25 +368,25 @@ def tile_rglru_kernel(tc, x, state, w_in, b_in, w_a, b_a, a_param, out_0, out_1)
             )
 
         def dram_view(out, j):
-            h, a0, k = UNITS[j]
-            return out[a0 * P:(a0 + k) * P, h * HD:(h + 1) * HD].rearrange("(i p) c -> p i c", p=P)
+            a, h0, k = UNITS[j]
+            return out[a * P:(a + 1) * P, h0 * HD:(h0 + k) * HD]
 
         def st0(j):
-            nc.sync.dma_start(out=dram_view(out_0, j), in_=t1u[j][:])
+            nc.sync.dma_start(out=dram_view(out_0, j), in_=t1u[j][:].rearrange("p i c -> p (i c)"))
 
         def cast(j):
-            h, a0, k = UNITS[j]
+            a, h0, k = UNITS[j]
             f8 = f8p.tile([P, k * HD], FP8, tag="f8%d" % k, name="f8_%d" % j)
             src = t1u[j][:].rearrange("p i c -> p (i c)")
             if j in CAST_ON_ACT:
                 nc.scalar.activation(out=f8[:], in_=src, func=ACT.Copy, scale=Y_SCALE, saturate=False)
             else:
                 nc.vector.tensor_scalar(out=f8[:], in0=src, scalar1=Y_SCALE, scalar2=None, op0=ALU.mult, saturate=False)
-            nc.sync.dma_start(out=dram_view(out_1, j), in_=f8[:].bitcast(U8).rearrange("p (i c) -> p i c", i=k))
+            nc.sync.dma_start(out=dram_view(out_1, j), in_=f8[:].bitcast(U8))
 
         def tiles(j):
-            h, a0, k = UNITS[j]
-            return [h * NA + a0 + i for i in range(k)]
+            a, h0, k = UNITS[j]
+            return [(h0 + i) * NA + a for i in range(k)]
 
         keep_warm(WARM_HEAD, 2 * P, True)
         x_t(0, 0)
@@ -478,11 +490,10 @@ def tile_rglru_kernel(tc, x, state, w_in, b_in, w_a, b_a, a_param, out_0, out_1)
                 wq(hp, 1)
                 wq(hp, 0)
                 xq(hp)
-            for hh in range(H):
-                if c == max(2 * (H - 1), NT * hh + NT):
-                    for j in SQ_ON_POOL:
-                        if UNITS[j][0] == hh:
-                            sqr(j)
+            for j, (a, h0, k) in enumerate(UNITS):
+                n_pool = min(h0 + k, POOL_HEADS) - h0
+                if n_pool > 0 and c == max(2 * (H - 1), NT * (h0 + n_pool)):
+                    sqr(j, 0, n_pool, True)
             if c >= R2_FROM:
                 regime2(R2_RATE)
             if c + 2 < H * NT:
@@ -498,12 +509,9 @@ def tile_rglru_kernel(tc, x, state, w_in, b_in, w_a, b_a, a_param, out_0, out_1)
                 work.extend([("g", h, 0), ("g", h, 1)] + [("t", h * NA + a) for a in range(NA)])
 
         n = len(UNITS)
-        act_sq = [j for j in range(n) if j not in SQ_ON_POOL]
         for s in range(n + LAG_CA + 1):
-            if s == 0 and 0 in act_sq:
-                sqr(0)
-            if s + 1 in act_sq:
-                sqr(s + 1)
+            if s + 1 < n and UNITS[s + 1][1] + UNITS[s + 1][2] > POOL_HEADS:
+                sqr(s + 1, POOL_HEADS - UNITS[s + 1][1], 1, False)
             if s < n:
                 sqrt(s)
             regime2(R2_RATE)

@@ -466,30 +466,29 @@ def tile_rglru_kernel(tc, x, state, w_in, b_in, w_a, b_a, a_param, out_0, out_1)
                 small["pa"]()
                 winth(1, 1, 0)
                 small["y1"]()
-                winth(1, 0, 0)
+                winth(1, 1, 1)
                 small["qa"]()
             if c == 1:
                 wqh(1, 1, 0)
                 small["qb"]()
-                wqh(1, 0, 0)
+                winth(1, 0, 0)
                 small["pb"]()
-                winth(1, 1, 1)
-                small["ch"]()
-                xq(1)
-                winth(1, 0, 1)
-            if c == 2:
                 wqh(1, 1, 1)
+                small["ch"]()
+                winth(1, 0, 1)
+                wqh(1, 0, 0)
+                xq(1)
+            if c == 2:
                 wqh(1, 0, 1)
             if 1 < hp < H and c % 2 == 0:
                 wint(hp, 1)
-                wint(hp, 0)
-                if XEVAC[hp] == "V":
-                    xev(hp, 0)
-                    xev(hp, 1)
-            if 1 < hp < H and c % 2 == 1:
+                xev(hp, 0)
+                xev(hp, 1)
                 wq(hp, 1)
-                wq(hp, 0)
+            if 1 < hp < H and c % 2 == 1:
+                wint(hp, 0)
                 xq(hp)
+                wq(hp, 0)
             for j, (a, h0, k) in enumerate(UNITS):
                 n_pool = min(h0 + k, POOL_HEADS) - h0
                 if n_pool > 0 and c == max(2 * (H - 1), NT * (h0 + n_pool)):

@@ -36,8 +36,8 @@ LAG_T3V = 2
 LAG_OT = 2
 LAG_ADD = 3
 LAG_CAST = 4
-WARM_HEAD = 1
-WARM_MID = 3
+WARM_HEAD = 2
+WARM_MID = 1
 WARM_GAP = 2
 GA, GB = 1.36, 0.71
 
@@ -57,10 +57,10 @@ def tile_rglru_kernel(tc, x, state, w_in, b_in, w_a, b_a, a_param, out_0, out_1)
         ptr = ctx.enter_context(tc.psum_pool(name="ptr", bufs=4))
         ctx.enter_context(tc.manual_schedule())
 
+        zeros = const.tile([P, 2 * P], F32, name="zeros")
+        nc.gpsimd.memset(zeros[:], 0.0)
         vrow = const.tile([P, P], BF16, name="vrow")
         nc.gpsimd.memset(vrow[:], 0.0)
-        zeros = const.tile([P, 2 * P], F32, name="zeros")
-        nc.vector.memset(zeros[:], 0.0)
         warm = const.tile([P, 1], F32, name="warm")
         nc.vector.memset(warm[:], 0.0)
         quarter = const.tile([P, 1], F32, name="quarter")

@@ -150,7 +150,9 @@ def tile_rglru_kernel(tc, x, state, w_in, b_in, w_a, b_a, a_param, out_0, out_1)
         aep = [keep.tile([P, 2 * NT, B], F32, name="aep%d" % q) for q in range(H // 2)]
         gx = [gxp[h // 2][:, (h % 2) * NT:(h % 2 + 1) * NT, :] for h in range(H)]
         ae = [aep[h // 2][:, (h % 2) * NT:(h % 2 + 1) * NT, :] for h in range(H)]
-        t1u = [keep.tile([P, k, HD], F32, name="t1_%d" % j) for j, (a, h0, k) in enumerate(UNITS)]
+        t1u = [keep.tile([P, k, HD], F32, name="t1_%d" % j)[:] for j, (a, h0, k) in enumerate(UNITS[:-2])]
+        t1_last = keep.tile([P, 2, HD], F32, name="t1_last")
+        t1u.extend([t1_last[:, 0:1, :], t1_last[:, 1:2, :]])
         unit_of = {}
         for j, (a, h0, k) in enumerate(UNITS):
             for i in range(k):
@@ -372,17 +374,31 @@ def tile_rglru_kernel(tc, x, state, w_in, b_in, w_a, b_a, a_param, out_0, out_1)
             return out[a * P:(a + 1) * P, h0 * HD:(h0 + k) * HD]
 
         def st0(j):
-            nc.sync.dma_start(out=dram_view(out_0, j), in_=t1u[j][:].rearrange("p i c -> p (i c)"))
+            if j < len(UNITS) - 2:
+                nc.sync.dma_start(out=dram_view(out_0, j), in_=t1u[j].rearrange("p i c -> p (i c)"))
+            elif j == len(UNITS) - 1:
+                nc.sync.dma_start(out=out_0[(NA - 1) * P:NA * P, 2 * HD:4 * HD], in_=t1_last[:].rearrange("p i c -> p (i c)"))
+
+        f8l = []
 
         def cast(j):
             a, h0, k = UNITS[j]
-            f8 = f8p.tile([P, k * HD], FP8, tag="f8%d" % k, name="f8_%d" % j)
-            src = t1u[j][:].rearrange("p i c -> p (i c)")
-            if j in CAST_ON_ACT:
-                nc.scalar.activation(out=f8[:], in_=src, func=ACT.Copy, scale=Y_SCALE, saturate=False)
+            src = t1u[j].rearrange("p i c -> p (i c)")
+            if j < len(UNITS) - 2:
+                f8t = f8p.tile([P, k * HD], FP8, tag="f8%d" % k, name="f8_%d" % j)
+                f8 = f8t[:]
             else:
-                nc.vector.tensor_scalar(out=f8[:], in0=src, scalar1=Y_SCALE, scalar2=None, op0=ALU.mult, saturate=False)
-            nc.sync.dma_start(out=dram_view(out_1, j), in_=f8[:].bitcast(U8))
+                if j == len(UNITS) - 2:
+                    f8l.append(f8p.tile([P, 2 * HD], FP8, tag="f82", name="f8_last"))
+                f8 = f8l[0][:, (j - len(UNITS) + 2) * HD:(j - len(UNITS) + 3) * HD]
+            if j in CAST_ON_ACT:
+                nc.scalar.activation(out=f8, in_=src, func=ACT.Copy, scale=Y_SCALE, saturate=False)
+            else:
+                nc.vector.tensor_scalar(out=f8, in0=src, scalar1=Y_SCALE, scalar2=None, op0=ALU.mult, saturate=False)
+            if j < len(UNITS) - 2:
+                nc.sync.dma_start(out=dram_view(out_1, j), in_=f8.bitcast(U8))
+            elif j == len(UNITS) - 1:
+                nc.sync.dma_start(out=out_1[(NA - 1) * P:NA * P, 2 * HD:4 * HD], in_=f8l[0][:].bitcast(U8))
 
         def tiles(j):
             a, h0, k = UNITS[j]
@@ -525,8 +541,9 @@ def tile_rglru_kernel(tc, x, state, w_in, b_in, w_a, b_a, a_param, out_0, out_1)
                 for v in tiles(s - LAG_ADD):
                     add(v)
                 st0(s - LAG_ADD)
-            if 0 <= s - LAG_CAST < n and (s - LAG_CAST) not in CAST_ON_ACT:
-                cast(s - LAG_CAST)
+            if s - LAG_ADD == n - 1:
+                cast(n - 2)
+                cast(n - 1)
             if 0 <= s - LAG_CA < n and (s - LAG_CA) in CAST_ON_ACT:
                 cast(s - LAG_CA)
             if 0 <= s - LAG_OT < n:

@@ -23,7 +23,8 @@ Y_SCALE = 280.0
 
 XEVAC = ("V", "S", "V", "V")
 UNITS = ((0, 0, 1), (0, 1, 1), (1, 0, 2), (2, 0, 2), (3, 0, 2), (0, 2, 2), (1, 2, 2), (2, 2, 2), (3, 2, 1), (3, 3, 1))
-CAST_ON_ACT = (0, 1, 2, 3, 4, 5, 6, 7)
+CAST_ON_ACT = (0, 1, 2, 3, 4, 5, 6)
+SHARED_CAST = 7
 T3C_ON_POOL = (0, 1, 2, 4, 5, 7, 8)
 WINT_ON_POOL = ()
 T3C_FROM_PSUM = (3, 6)
@@ -400,6 +401,19 @@ def tile_rglru_kernel(tc, x, state, w_in, b_in, w_a, b_a, a_param, out_0, out_1)
             elif j == len(UNITS) - 1:
                 nc.sync.dma_start(out=out_1[(NA - 1) * P:NA * P, 2 * HD:4 * HD], in_=f8l[0][:].bitcast(U8))
 
+        f8h = []
+
+        def cast_half(j, i):
+            if not f8h:
+                f8h.append(f8p.tile([P, 2 * HD], FP8, tag="f82", name="f8_%d" % j))
+            f8 = f8h[0][:, i * HD:(i + 1) * HD]
+            src = t1u[j][:, i, :]
+            if i == 0:
+                nc.scalar.activation(out=f8, in_=src, func=ACT.Copy, scale=Y_SCALE, saturate=False)
+                nc.sync.dma_start(out=dram_view(out_1, j), in_=f8h[0][:].bitcast(U8))
+            else:
+                nc.vector.tensor_scalar(out=f8, in0=src, scalar1=Y_SCALE, scalar2=None, op0=ALU.mult, saturate=False)
+
         def tiles(j):
             a, h0, k = UNITS[j]
             return [(h0 + i) * NA + a for i in range(k)]
@@ -541,11 +555,15 @@ def tile_rglru_kernel(tc, x, state, w_in, b_in, w_a, b_a, a_param, out_0, out_1)
                 for v in tiles(s - LAG_ADD):
                     add(v)
                 st0(s - LAG_ADD)
+            if s - LAG_CAST == SHARED_CAST:
+                cast_half(SHARED_CAST, 1)
             if s - LAG_ADD == n - 1:
                 cast(n - 2)
                 cast(n - 1)
             if 0 <= s - LAG_CA < n and (s - LAG_CA) in CAST_ON_ACT:
                 cast(s - LAG_CA)
+            if s - LAG_CA == SHARED_CAST:
+                cast_half(SHARED_CAST, 0)
             if 0 <= s - LAG_OT < n:
                 for v in tiles(s - LAG_OT):
                     o_t(v)

@@ -426,8 +426,9 @@ def tile_rglru_kernel(tc, x, state, w_in, b_in, w_a, b_a, a_param, out_0, out_1)
         keep_warm(WARM_MID, 2 * P, True)
         xev(0, 0, "V")
         xev(0, 1, "S")
-        nc.scalar.copy(out=vecs[:].rearrange("p i c -> p (i c)"), in_=vt[:, 0:3 * NC])
-        small["av"]()
+        nc.scalar.activation(out=sm["av"][:], in_=vt[:, 2 * NC:3 * NC], func=ACT.Abs)
+        nc.scalar.activation(out=hb[:].rearrange("p i c -> p (i c)"), in_=vt[:, 0:2 * NC], func=ACT.Copy, scale=0.5)
+        nc.scalar.copy(out=vecs[:, 2, :], in_=vt[:, 2 * NC:3 * NC])
         wintq(0, 1, 0)
         xqh(0, 0)
         xqh(0, 1)
@@ -437,9 +438,6 @@ def tile_rglru_kernel(tc, x, state, w_in, b_in, w_a, b_a, a_param, out_0, out_1)
         wintq(0, 0, 0)
         wintq(0, 0, 1, True)
         small["t"]()
-        half_biases()
-        small["y0"]()
-        small["e1"]()
         wqq(0, 1, 1)
         wqq(0, 0, 0)
         wqq(0, 0, 1)
@@ -477,7 +475,11 @@ def tile_rglru_kernel(tc, x, state, w_in, b_in, w_a, b_a, a_param, out_0, out_1)
         for c in range(H * NT):
             h, t = c // NT, c % NT
             tha(c)
+            if c == 0:
+                small["y0"]()
             thx(c)
+            if c == 0:
+                small["e1"]()
             if c == 3:
                 ex(0)
                 ex(1)

@@ -521,9 +521,10 @@ def tile_rglru_kernel(tc, x, state, w_in, b_in, w_a, b_a, a_param, out_0, out_1)
                 wint(hp, 0)
                 xq(hp)
                 wq(hp, 0)
-            for j, (a, h0, k) in enumerate(UNITS):
+            for j in (1, 0) + tuple(range(2, len(UNITS))):
+                a, h0, k = UNITS[j]
                 n_pool = min(h0 + k, POOL_HEADS) - h0
-                if n_pool > 0 and c == max(2 * (H - 1), NT * (h0 + n_pool)):
+                if n_pool > 0 and c == max(2 * NT, NT * (h0 + n_pool)):
                     sqr(j, 0, n_pool, True)
             if c >= R2_FROM:
                 regime2(R2_RATE)

@@ -4,7 +4,6 @@ import concourse.mybir as mybir
 from concourse.masks import make_identity
 
 B, H, HD = 512, 4, 512
-W = H * HD
 FLOPS = 2 * 2 * B * H * HD * HD
 
 F32 = mybir.dt.float32
@@ -17,29 +16,27 @@ ACT = mybir.ActivationFunctionType
 ALU = mybir.AluOpType
 
 P = 128
-NT = 4
-NA = 4
+PACK = 4
+NT = HD // P
+NA = B // P
+NC = H * NT
 Y_SCALE = 280.0
 
-XEVAC = ("V", "S", "V", "V")
 UNITS = ((0, 0, 1), (0, 1, 1), (1, 0, 2), (2, 0, 2), (3, 0, 2), (0, 2, 2), (1, 2, 2), (2, 2, 2), (3, 2, 1), (3, 3, 1))
+NU = len(UNITS)
+POOL_HEADS = 3
+ROOT_PRODUCT_ON_POOL = (0, 1, 2, 4, 5, 7, 8)
+ROOT_PRODUCT_FROM_PSUM = (3, 6)
 CAST_ON_ACT = (0, 1, 2, 3, 4, 5, 6)
 SHARED_CAST = 7
-T3C_ON_POOL = (0, 1, 2, 4, 5, 7, 8)
-WINT_ON_POOL = ()
-T3C_FROM_PSUM = (3, 6)
-POOL_HEADS = 3
-R2_FROM = 8
-R2_RATE = 2
-LAG_CA = 5
-LAG_T3C = 1
-LAG_T3V = 2
-LAG_OT = 2
-LAG_ADD = 3
-LAG_CAST = 4
-WARM_HEAD = 2
-WARM_MID = 1
-WARM_GAP = 2
+PASSES_FROM = 8
+PASSES_A_STEP = 2
+LAG_PRODUCT_POOL = 1
+LAG_PRODUCT_DVE = 2
+LAG_BACK = 2
+LAG_SUM = 3
+LAG_CAST_DVE = 4
+LAG_CAST_ACT = 5
 GA, GB = 1.36, 0.71
 
 
@@ -49,8 +46,8 @@ def tile_rglru_kernel(tc, x, state, w_in, b_in, w_a, b_a, a_param, out_0, out_1)
 
     with ExitStack() as ctx:
         const = ctx.enter_context(tc.tile_pool(name="const", bufs=1))
-        xin = ctx.enter_context(tc.tile_pool(name="xin", bufs=4))
-        win = ctx.enter_context(tc.tile_pool(name="win", bufs=8))
+        xin = ctx.enter_context(tc.tile_pool(name="xin", bufs=H))
+        win = ctx.enter_context(tc.tile_pool(name="win", bufs=2 * H))
         wgp = ctx.enter_context(tc.tile_pool(name="wgp", bufs=4))
         keep = ctx.enter_context(tc.tile_pool(name="keep", bufs=1))
         f8p = ctx.enter_context(tc.tile_pool(name="f8p", bufs=6))
@@ -66,15 +63,11 @@ def tile_rglru_kernel(tc, x, state, w_in, b_in, w_a, b_a, a_param, out_0, out_1)
         nc.vector.memset(warm[:], 0.0)
         quarter = const.tile([P, 1], F32, name="quarter")
         nc.vector.memset(quarter[:], 0.25)
-        vecs = const.tile([P, 3, H * NT], BF16, name="vecs")
-        NC = H * NT
         nc.scalar.dma_start(out=vrow[2 * NC:3 * NC, :], in_=a_param.rearrange("(c m) -> c m", m=P))
         nc.scalar.dma_start(out=vrow[0:NC, :], in_=b_in.rearrange("h (t m) -> (h t) m", m=P))
         nc.scalar.dma_start(out=vrow[NC:2 * NC, :], in_=b_a.rearrange("h (t m) -> (h t) m", m=P))
-
-        warm2 = const.tile([P, 1], F32, name="warm2")
-        nc.scalar.activation(out=warm2[:], in_=warm[:], func=ACT.Exp)
-
+        warm_out = const.tile([P, 1], F32, name="warm_out")
+        nc.scalar.activation(out=warm_out[:], in_=warm[:], func=ACT.Exp)
         ident = const.tile([P, P], F32, name="ident")
         make_identity(nc, ident[:])
         ident_bf = const.tile([P, P], BF16, name="ident_bf")
@@ -86,7 +79,7 @@ def tile_rglru_kernel(tc, x, state, w_in, b_in, w_a, b_a, a_param, out_0, out_1)
 
         def load_x(h):
             xn[h] = xin.tile([P, NA, HD], BF16, tag="xn", name="xn%d" % h)
-            src = x[:, h * HD:(h + 1) * HD].rearrange("(a p) c -> p a c", p=P)
+            src = x[:, h * HD:(h + 1) * HD].rearrange("(a p) k -> p a k", p=P)
             if h == 0:
                 for a in range(NA):
                     nc.sync.dma_start(out=xn[h][:, a, :], in_=src[:, a, :])
@@ -94,162 +87,131 @@ def tile_rglru_kernel(tc, x, state, w_in, b_in, w_a, b_a, a_param, out_0, out_1)
                 nc.sync.dma_start(out=xn[h][:], in_=src)
 
         def load_w(h, g):
-            raw[h][g] = win.tile([P, 4, HD], BF16, tag="raw", name="raw%d_%d" % (h, g))
-            nc.sync.dma_start(out=raw[h][g][:], in_=w_dram[g][h].rearrange("(p j) n -> p j n", j=4))
+            raw[h][g] = win.tile([P, PACK, HD], BF16, tag="raw", name="raw%d_%d" % (h, g))
+            nc.sync.dma_start(out=raw[h][g][:], in_=w_dram[g][h].rearrange("(p j) n -> p j n", j=PACK))
 
-        def load_st(h):
+        def load_state(h):
             st[h] = keep.tile([P, NA, HD], BF16, name="st%d" % h)
-            nc.sync.dma_start(
-                out=st[h][:], in_=state[:, h * HD:(h + 1) * HD].rearrange("(a p) c -> p a c", p=P)
-            )
+            nc.sync.dma_start(out=st[h][:], in_=state[:, h * HD:(h + 1) * HD].rearrange("(a p) k -> p a k", p=P))
 
         for h in range(H):
             load_x(h)
             load_w(h, 1)
             load_w(h, 0)
         for h in range(H):
-            load_st(h)
+            load_state(h)
 
-        v = vecs[:, 2, :]
-        hb = const.tile([P, 2, H * NT], F32, name="hb")
-        ch = const.tile([P, H * NT], F32, name="ch")
+        a_param_bf = const.tile([P, NC], BF16, name="a_param_bf")
+        hb = const.tile([P, 2, NC], F32, name="hb")
+        ch = const.tile([P, NC], F32, name="ch")
         sm = {}
         for nm in ("av", "w", "t", "y0", "e1", "pa", "y1", "e2", "pb", "qa", "qb"):
-            sm[nm] = const.tile([P, H * NT], F32, name="sm_" + nm)
+            sm[nm] = const.tile([P, NC], F32, name="sm_" + nm)
 
         def stt(out, in0, scalar, in1, op0, op1):
             nc.vector.scalar_tensor_tensor(out=out, in0=in0, scalar=scalar, in1=in1, op0=op0, op1=op1)
 
-        def small_act(out, in_, func, scale):
-            nc.scalar.activation(out=sm[out][:], in_=in_, func=func, scale=scale)
+        def small_exp(out, in_, scale):
+            nc.scalar.activation(out=sm[out][:], in_=sm[in_][:], func=ACT.Exp, scale=scale)
 
         small = {
-            "av": lambda: small_act("av", v, ACT.Abs, 1.0),
-            "w": lambda: small_act("w", sm["av"][:], ACT.Exp, -1.0),
-            "t": lambda: small_act("t", sm["w"][:], ACT.Exp, -GB),
+            "w": lambda: small_exp("w", "av", -1.0),
+            "t": lambda: small_exp("t", "w", -GB),
             "y0": lambda: nc.scalar.activation(out=sm["y0"][:], in_=sm["t"][:], func=ACT.Copy, scale=-GA, bias=GA),
-            "e1": lambda: small_act("e1", sm["y0"][:], ACT.Exp, -1.0),
+            "e1": lambda: small_exp("e1", "y0", -1.0),
             "pa": lambda: stt(sm["pa"][:], sm["w"][:], 1.0, sm["e1"][:], ALU.add, ALU.mult),
             "y1": lambda: stt(sm["y1"][:], sm["pa"][:], -1.0, sm["y0"][:], ALU.add, ALU.add),
-            "e2": lambda: small_act("e2", sm["y1"][:], ACT.Exp, -1.0),
-            "qa": lambda: stt(sm["qa"][:], v, 0.0, sm["y1"][:], ALU.max, ALU.add),
+            "e2": lambda: small_exp("e2", "y1", -1.0),
+            "qa": lambda: stt(sm["qa"][:], a_param_bf[:], 0.0, sm["y1"][:], ALU.max, ALU.add),
             "qb": lambda: nc.vector.tensor_scalar(
                 out=sm["qb"][:], in0=sm["qa"][:], scalar1=-1.0, scalar2=-4.0, op0=ALU.add, op1=ALU.mult),
             "pb": lambda: stt(sm["pb"][:], sm["w"][:], 1.0, sm["e2"][:], ALU.add, ALU.mult),
             "ch": lambda: stt(ch[:], sm["pb"][:], -4.0, sm["qb"][:], ALU.mult, ALU.add),
         }
 
-        def half_biases():
-            nc.scalar.activation(out=hb[:], in_=vecs[:, 0:2, :], func=ACT.Copy, scale=0.5)
-
-        xg = [keep.tile([P, 4 * B], BF16, name="xg%d" % h, align_bytes=64) for h in range(H)]
+        xg = [keep.tile([P, PACK * B], BF16, name="xg%d" % h, align_bytes=64) for h in range(H)]
         xc = [keep.tile([P, B], U32, name="xc%d" % h, align_bytes=64) for h in range(H)]
         xs = [keep.tile([P, B], U8, name="xs%d" % h, align_bytes=64) for h in range(H)]
         wc = [[keep.tile([P, HD], U32, name="wc%d_%d" % (h, g), align_bytes=64) for g in range(2)] for h in range(H)]
         ws = [[keep.tile([P, HD], U8, name="ws%d_%d" % (h, g), align_bytes=64) for g in range(2)] for h in range(H)]
-        gxp = [keep.tile([P, 2 * NT, B], F32, name="gxp%d" % q) for q in range(H // 2)]
-        aep = [keep.tile([P, 2 * NT, B], F32, name="aep%d" % q) for q in range(H // 2)]
-        gx = [gxp[h // 2][:, (h % 2) * NT:(h % 2 + 1) * NT, :] for h in range(H)]
-        ae = [aep[h // 2][:, (h % 2) * NT:(h % 2 + 1) * NT, :] for h in range(H)]
-        t1u = [keep.tile([P, k, HD], F32, name="t1_%d" % j)[:] for j, (a, h0, k) in enumerate(UNITS[:-2])]
-        t1_last = keep.tile([P, 2, HD], F32, name="t1_last")
-        t1u.extend([t1_last[:, 0:1, :], t1_last[:, 1:2, :]])
+        gx_pair = [keep.tile([P, 2 * NT, B], F32, name="gx_pair%d" % q) for q in range(H // 2)]
+        decay_pair = [keep.tile([P, 2 * NT, B], F32, name="decay_pair%d" % q) for q in range(H // 2)]
+        gx = [gx_pair[h // 2][:, (h % 2) * NT:(h % 2 + 1) * NT, :] for h in range(H)]
+        decay = [decay_pair[h // 2][:, (h % 2) * NT:(h % 2 + 1) * NT, :] for h in range(H)]
+        res = [keep.tile([P, k, HD], F32, name="res%d" % j)[:] for j, (a, h0, k) in enumerate(UNITS[:-2])]
+        res_last = keep.tile([P, 2, HD], F32, name="res_last")
+        res.extend([res_last[:, 0:1, :], res_last[:, 1:2, :]])
         unit_of = {}
         for j, (a, h0, k) in enumerate(UNITS):
             for i in range(k):
                 unit_of[(h0 + i) * NA + a] = (j, i)
+
+        def tiles_of(j):
+            a, h0, k = UNITS[j]
+            return [(h0 + i) * NA + a for i in range(k)]
 
         def unit_view(pairs, j, i0, n):
             a, h0, k = UNITS[j]
             r0 = (h0 % 2 + i0) * NT
             return pairs[h0 // 2][:, r0:r0 + n * NT, a * P:(a + 1) * P]
 
-        xts = {}
-        wgs = {}
-        acc = {}
-        ats = {}
-        sqs = {}
-        ots = {}
+        def hbm_view(out, j):
+            a, h0, k = UNITS[j]
+            return out[a * P:(a + 1) * P, h0 * HD:(h0 + k) * HD]
 
-        def x_t(h, half):
+        x_words = {}
+        wg = {}
+        sums = {}
+        x_cols = {}
+        decay_back = {}
+        sq = {}
+        gx_psum = {}
+        prod_back = {}
+
+        def turn_x_words(h, half):
             xt = ptr.tile([P, 2, 2, P], F32, tag="tr", name="xt%d_%d" % (h, half))
-            xts[(h, half)] = xt
+            x_words[(h, half)] = xt
             for a in range(2):
                 words = xn[h][:, 2 * half + a, :].bitcast(F32)
                 for u in range(2):
                     nc.tensor.transpose(xt[:, a, u, :], words[:, u:HD // 2:2], ident[:])
 
-        def xev(h, half, eng=None):
-            xgw = xg[h][:].bitcast(F32).rearrange("p (a r u) -> p a r u", a=NA, u=2)
-            dst = xgw[:, 2 * half:2 * half + 2, :, :]
-            src = xts[(h, half)][:].rearrange("p a u r -> p a r u")
-            if (eng or XEVAC[h]) == "V":
+        def copy_x_words(h, half, engine):
+            dst = xg[h][:].bitcast(F32).rearrange("p (a r u) -> p a r u", a=NA, u=2)[:, 2 * half:2 * half + 2, :, :]
+            src = x_words[(h, half)][:].rearrange("p a u r -> p a r u")
+            if engine == "V":
                 nc.vector.tensor_copy(out=dst, in_=src)
             else:
                 nc.scalar.copy(out=dst, in_=src)
 
-        def xqh(h, half):
+        def quantize_x(h, first=0, halves=2):
+            tok = slice(first * (B // 2), (first + halves) * (B // 2))
             nc.vector.quantize_mx(
-                out=xc[h][:, half * (B // 2):(half + 1) * (B // 2)].bitcast(FP8X4),
-                scales=xs[h][:, half * (B // 2):(half + 1) * (B // 2)],
-                in_=xg[h][:, half * 2 * B:(half + 1) * 2 * B],
+                out=xc[h][:, tok].bitcast(FP8X4), scales=xs[h][:, tok],
+                in_=xg[h][:, first * (B // 2) * PACK:(first + halves) * (B // 2) * PACK],
             )
 
-        def xq(h):
-            nc.vector.quantize_mx(out=xc[h][:].bitcast(FP8X4), scales=xs[h][:], in_=xg[h][:])
-
-        def new_wg(h, g):
-            wgs[(h, g)] = wgp.tile([P, 4 * HD], BF16, tag="wg", name="wg%d_%d" % (h, g), align_bytes=64)
-
-        def wint(h, g):
-            new_wg(h, g)
-            if (h, g) in WINT_ON_POOL:
-                dst = wgs[(h, g)][:].rearrange("p (t m j) -> p t m j", t=NT, j=4)
-                src = raw[h][g][:].rearrange("p j (m t) -> p t m j", t=NT)
-                nc.gpsimd.tensor_scalar(out=dst, in0=src, scalar1=1.0, scalar2=0.0, op0=ALU.mult, op1=ALU.add)
-            else:
-                dst = wgs[(h, g)][:].rearrange("p (c i j) -> p c j i", i=4, j=4)
-                src = raw[h][g][:].rearrange("p j (c i) -> p c j i", i=4)
+        def interleave_w(h, g, first=0, quarters=NT, engine="V"):
+            if (h, g) not in wg:
+                wg[(h, g)] = wgp.tile([P, PACK * HD], BF16, tag="wg", name="wg%d_%d" % (h, g), align_bytes=64)
+            dst = wg[(h, g)][:, first * HD:(first + quarters) * HD].rearrange("p (q i j) -> p q j i", i=4, j=PACK)
+            src = raw[h][g][:, :, first * P:(first + quarters) * P].rearrange("p j (q i) -> p q j i", i=4)
+            if engine == "V":
                 nc.vector.tensor_copy(out=dst, in_=src)
-
-        def wq(h, g):
-            nc.vector.quantize_mx(out=wc[h][g][:].bitcast(FP8X4), scales=ws[h][g][:], in_=wgs[(h, g)][:])
-
-        def wintq(h, g, t, on_act=False):
-            if t == 0:
-                new_wg(h, g)
-            dst = wgs[(h, g)][:, t * HD:(t + 1) * HD].rearrange("p (c i j) -> p c j i", i=4, j=4)
-            src = raw[h][g][:, :, t * P:(t + 1) * P].rearrange("p j (c i) -> p c j i", i=4)
-            if on_act:
+            else:
                 nc.scalar.copy(out=dst, in_=src)
-            else:
-                nc.vector.tensor_copy(out=dst, in_=src)
 
-        def winth(h, g, half):
-            if (h, g) not in wgs:
-                new_wg(h, g)
-            dst = wgs[(h, g)][:, half * 2 * HD:(half + 1) * 2 * HD].rearrange("p (c i j) -> p c j i", i=4, j=4)
-            src = raw[h][g][:, :, half * 2 * P:(half + 1) * 2 * P].rearrange("p j (c i) -> p c j i", i=4)
-            nc.vector.tensor_copy(out=dst, in_=src)
-
-        def wqh(h, g, half):
-            cols = slice(half * 2 * P, (half + 1) * 2 * P)
+        def quantize_w(h, g, first=0, quarters=NT):
+            cols = slice(first * P, (first + quarters) * P)
             nc.vector.quantize_mx(
                 out=wc[h][g][:, cols].bitcast(FP8X4), scales=ws[h][g][:, cols],
-                in_=wgs[(h, g)][:, half * 2 * HD:(half + 1) * 2 * HD],
+                in_=wg[(h, g)][:, first * HD:(first + quarters) * HD],
             )
 
-        def wqq(h, g, t):
-            cols = slice(t * P, (t + 1) * P)
-            nc.vector.quantize_mx(
-                out=wc[h][g][:, cols].bitcast(FP8X4), scales=ws[h][g][:, cols],
-                in_=wgs[(h, g)][:, t * HD:(t + 1) * HD],
-            )
-
-        def mx(c):
+        def matmuls(c):
             h, t = c // NT, c % NT
             cols = slice(t * P, (t + 1) * P)
-            pair = [None, None]
+            banks = [None, None]
             for g in (1, 0):
                 ps = pmx.tile([P, B], F32, tag="ps%d" % g, name="ps%d_%d" % (g, c))
                 nc.tensor.matmul_mx(
@@ -261,318 +223,287 @@ def tile_rglru_kernel(tc, x, state, w_in, b_in, w_a, b_a, a_param, out_0, out_1)
                     start=True,
                     stop=True,
                 )
-                pair[g] = ps
-            acc[c] = pair
+                banks[g] = ps
+            sums[c] = banks
 
-        def thx(c):
+        def tanh_x(c):
             h, t = c // NT, c % NT
-            nc.scalar.activation(out=gx[h][:, t, :], in_=acc[c][0][:], func=ACT.Tanh, bias=hb[:, 0, c:c + 1], scale=0.5)
+            nc.scalar.activation(out=gx[h][:, t, :], in_=sums[c][0][:], func=ACT.Tanh, bias=hb[:, 0, c:c + 1], scale=0.5)
 
-        def tha(c):
+        def tanh_decay(c):
             h, t = c // NT, c % NT
-            nc.scalar.activation(out=ae[h][:, t, :], in_=acc[c][1][:], func=ACT.Tanh, bias=hb[:, 1, c:c + 1], scale=0.5)
+            nc.scalar.activation(out=decay[h][:, t, :], in_=sums[c][1][:], func=ACT.Tanh, bias=hb[:, 1, c:c + 1], scale=0.5)
 
-        def ex(c):
+        def exp_decay(c):
             h, t = c // NT, c % NT
-            nc.scalar.activation(out=ae[h][:, t, :], in_=ae[h][:, t, :], func=ACT.Exp, bias=ch[:, c:c + 1], scale=ch[:, c:c + 1])
+            nc.scalar.activation(out=decay[h][:, t, :], in_=decay[h][:, t, :], func=ACT.Exp, bias=ch[:, c:c + 1], scale=ch[:, c:c + 1])
 
-        xus = {}
-
-        def x_t2(h, u):
-            xu = ptr.tile([P, 2, B], BF16, tag="tr", name="xu%d_%d" % (h, u))
-            xus[(h, u)] = xu
+        def turn_x_cols(h, two):
+            xu = ptr.tile([P, 2, B], BF16, tag="tr", name="xu%d_%d" % (h, two))
+            x_cols[(h, two)] = xu
             for e in range(2):
-                t = 2 * u + e
+                t = 2 * two + e
                 for a in range(NA):
                     nc.tensor.transpose(xu[:, e, a * P:(a + 1) * P], xn[h][:, a, t * P:(t + 1) * P], ident_bf[:])
 
-        def gxx2(h, u):
-            g = gx[h][:, 2 * u:2 * u + 2, :]
-            nc.vector.scalar_tensor_tensor(out=g, in0=g, scalar=1.0, in1=xus[(h, u)][:], op0=ALU.add, op1=ALU.mult)
+        def times_x(h, two):
+            th = gx[h][:, 2 * two:2 * two + 2, :]
+            nc.vector.scalar_tensor_tensor(out=th, in0=th, scalar=1.0, in1=x_cols[(h, two)][:], op0=ALU.add, op1=ALU.mult)
 
-        def a_t(u):
-            h, a = u // NA, u % NA
-            tr = ptr.tile([P, NT, P], F32, tag="tr", name="at%d" % u)
-            ats[u] = tr
+        def turn_decay_back(v):
+            h, a = v // NA, v % NA
+            tr = ptr.tile([P, NT, P], F32, tag="tr", name="at%d" % v)
+            decay_back[v] = tr
             for t in range(NT):
-                nc.tensor.transpose(tr[:, t, :], ae[h][:, t, a * P:(a + 1) * P], ident[:])
+                nc.tensor.transpose(tr[:, t, :], decay[h][:, t, a * P:(a + 1) * P], ident[:])
 
-        def t1(v):
+        def times_state(v):
             h, a = v // NA, v % NA
             j, i = unit_of[v]
             nc.vector.tensor_tensor(
-                out=t1u[j][:, i, :],
-                in0=ats[v][:].rearrange("p t m -> p (t m)"),
-                in1=st[h][:, a, :],
-                op=ALU.mult,
+                out=res[j][:, i, :], in0=decay_back[v][:].rearrange("p t m -> p (t m)"), in1=st[h][:, a, :], op=ALU.mult
             )
 
-        def sqr(j, i0, n, on_pool):
-            a, h0, k = UNITS[j]
-            if j not in sqs:
-                if j < 8:
-                    sq = win.tile([P, k * NT, P], F32, tag="raw", name="sq%d" % j)
+        waiting = []
+        turned = []
+
+        def passes():
+            for task in turned:
+                if task[0] == "x":
+                    times_x(task[1], task[2])
                 else:
-                    sq = wgp.tile([P, k * NT, P], F32, tag="wg", name="sq%d" % j, align_bytes=64)
-                sqs[j] = sq[:]
-            src = unit_view(aep, j, i0, n)
-            dst = sqs[j][:, i0 * NT:(i0 + n) * NT, :]
+                    times_state(task[1])
+            turned.clear()
+            for i in range(PASSES_A_STEP):
+                if waiting:
+                    task = waiting.pop(0)
+                    if task[0] == "x":
+                        turn_x_cols(task[1], task[2])
+                    else:
+                        turn_decay_back(task[1])
+                    turned.append(task)
+
+        def square(j, i0, n, on_pool):
+            a, h0, k = UNITS[j]
+            if j not in sq:
+                if j < 2 * H:
+                    sq[j] = win.tile([P, k * NT, P], F32, tag="raw", name="sq%d" % j)[:]
+                else:
+                    sq[j] = wgp.tile([P, k * NT, P], F32, tag="wg", name="sq%d" % j, align_bytes=64)[:]
+            src = unit_view(decay_pair, j, i0, n)
+            dst = sq[j][:, i0 * NT:(i0 + n) * NT, :]
             if on_pool:
                 nc.gpsimd.tensor_tensor(out=dst, in0=src, in1=src, op=ALU.mult)
             else:
                 nc.scalar.activation(out=dst, in_=src, func=ACT.Square)
 
-        def sqrt(j):
-            nc.scalar.activation(out=sqs[j], in_=sqs[j], func=ACT.Sqrt, bias=quarter[:, 0:1], scale=-0.25)
+        def root(j):
+            nc.scalar.activation(out=sq[j], in_=sq[j], func=ACT.Sqrt, bias=quarter[:, 0:1], scale=-0.25)
 
-        def t3c(j):
+        def root_product(j):
             a, h0, k = UNITS[j]
-            eng = nc.gpsimd if j in T3C_ON_POOL else nc.vector
-            eng.tensor_tensor(out=sqs[j], in0=unit_view(gxp, j, 0, k), in1=sqs[j], op=ALU.mult)
+            eng = nc.gpsimd if j in ROOT_PRODUCT_ON_POOL else nc.vector
+            eng.tensor_tensor(out=sq[j], in0=unit_view(gx_pair, j, 0, k), in1=sq[j], op=ALU.mult)
 
-        gps = {}
-
-        def g_copy(j, u):
-            gp = ptr.tile([P, NT, P], F32, tag="tr", name="gp%d_%d" % (j, u))
-            gps[(j, u)] = gp
-            src = unit_view(gxp, j, u, 1)
+        def lay_gx_into_psum(j, i):
+            gp = ptr.tile([P, NT, P], F32, tag="tr", name="gp%d_%d" % (j, i))
+            gx_psum[(j, i)] = gp
+            src = unit_view(gx_pair, j, i, 1)
             for e in range(2):
                 nc.tensor.matmul(
                     gp[:, 2 * e:2 * e + 2, :], lhsT=ident[:], rhs=src[:, 2 * e:2 * e + 2, :], start=True, stop=True
                 )
 
-        def t3c_psum(j):
-            for u in range(2):
-                r = sqs[j][:, u * NT:(u + 1) * NT, :]
-                nc.vector.tensor_tensor(out=r, in0=gps[(j, u)][:], in1=r, op=ALU.mult)
+        def root_product_from_psum(j):
+            for i in range(2):
+                r = sq[j][:, i * NT:(i + 1) * NT, :]
+                nc.vector.tensor_tensor(out=r, in0=gx_psum[(j, i)][:], in1=r, op=ALU.mult)
 
-        def o_t(v):
+        def turn_product_back(v):
             j, i = unit_of[v]
             tr = pmx.tile([P, NT, P], F32, tag="ps%d" % (v % 2), name="ot%d" % v)
-            ots[v] = tr
+            prod_back[v] = tr
             for t in range(NT):
-                nc.tensor.transpose(tr[:, t, :], sqs[j][:, i * NT + t, :], ident[:])
+                nc.tensor.transpose(tr[:, t, :], sq[j][:, i * NT + t, :], ident[:])
 
-        def keep_warm(k, n_cols, early):
-            for i in range(k):
-                if early:
-                    dummy = pmx.tile([P, n_cols], F32, tag="ps%d" % (i % 2), name="dummy")
-                else:
-                    dummy = ptr.tile([P, n_cols], F32, tag="tr", name="dummy")
-                nc.tensor.matmul(dummy[:], lhsT=zeros[:, 0:P], rhs=zeros[:, 0:n_cols], start=True, stop=True)
-
-        def add(v):
+        def final_sum(v):
             j, i = unit_of[v]
             nc.vector.tensor_tensor(
-                out=t1u[j][:, i, :],
-                in0=ots[v][:].rearrange("p t m -> p (t m)"),
-                in1=t1u[j][:, i, :],
-                op=ALU.add,
+                out=res[j][:, i, :], in0=prod_back[v][:].rearrange("p t m -> p (t m)"), in1=res[j][:, i, :], op=ALU.add
             )
 
-        def dram_view(out, j):
-            a, h0, k = UNITS[j]
-            return out[a * P:(a + 1) * P, h0 * HD:(h0 + k) * HD]
+        def store_out_0(j):
+            if j < NU - 2:
+                nc.sync.dma_start(out=hbm_view(out_0, j), in_=res[j].rearrange("p i n -> p (i n)"))
+            elif j == NU - 1:
+                nc.sync.dma_start(out=out_0[(NA - 1) * P:NA * P, (H - 2) * HD:H * HD], in_=res_last[:].rearrange("p i n -> p (i n)"))
 
-        def st0(j):
-            if j < len(UNITS) - 2:
-                nc.sync.dma_start(out=dram_view(out_0, j), in_=t1u[j].rearrange("p i c -> p (i c)"))
-            elif j == len(UNITS) - 1:
-                nc.sync.dma_start(out=out_0[(NA - 1) * P:NA * P, 2 * HD:4 * HD], in_=t1_last[:].rearrange("p i c -> p (i c)"))
+        def cast_to(f8, src, on_act):
+            if on_act:
+                nc.scalar.activation(out=f8, in_=src, func=ACT.Copy, scale=Y_SCALE, saturate=False)
+            else:
+                nc.vector.tensor_scalar(out=f8, in0=src, scalar1=Y_SCALE, scalar2=None, op0=ALU.mult, saturate=False)
 
-        f8l = []
+        f8_joint = {}
 
         def cast(j):
             a, h0, k = UNITS[j]
-            src = t1u[j].rearrange("p i c -> p (i c)")
-            if j < len(UNITS) - 2:
-                f8t = f8p.tile([P, k * HD], FP8, tag="f8%d" % k, name="f8_%d" % j)
-                f8 = f8t[:]
+            src = res[j].rearrange("p i n -> p (i n)")
+            if j < NU - 2:
+                f8 = f8p.tile([P, k * HD], FP8, tag="f8%d" % k, name="f8_%d" % j)
+                cast_to(f8[:], src, j in CAST_ON_ACT)
+                nc.sync.dma_start(out=hbm_view(out_1, j), in_=f8[:].bitcast(U8))
             else:
-                if j == len(UNITS) - 2:
-                    f8l.append(f8p.tile([P, 2 * HD], FP8, tag="f82", name="f8_last"))
-                f8 = f8l[0][:, (j - len(UNITS) + 2) * HD:(j - len(UNITS) + 3) * HD]
-            if j in CAST_ON_ACT:
-                nc.scalar.activation(out=f8, in_=src, func=ACT.Copy, scale=Y_SCALE, saturate=False)
-            else:
-                nc.vector.tensor_scalar(out=f8, in0=src, scalar1=Y_SCALE, scalar2=None, op0=ALU.mult, saturate=False)
-            if j < len(UNITS) - 2:
-                nc.sync.dma_start(out=dram_view(out_1, j), in_=f8.bitcast(U8))
-            elif j == len(UNITS) - 1:
-                nc.sync.dma_start(out=out_1[(NA - 1) * P:NA * P, 2 * HD:4 * HD], in_=f8l[0][:].bitcast(U8))
+                if j == NU - 2:
+                    f8_joint["last"] = f8p.tile([P, 2 * HD], FP8, tag="f82", name="f8_last")
+                i = j - (NU - 2)
+                cast_to(f8_joint["last"][:, i * HD:(i + 1) * HD], src, False)
+                if j == NU - 1:
+                    nc.sync.dma_start(out=out_1[(NA - 1) * P:NA * P, (H - 2) * HD:H * HD], in_=f8_joint["last"][:].bitcast(U8))
 
-        f8h = []
-
-        def cast_half(j, i):
-            if not f8h:
-                f8h.append(f8p.tile([P, 2 * HD], FP8, tag="f82", name="f8_%d" % j))
-            f8 = f8h[0][:, i * HD:(i + 1) * HD]
-            src = t1u[j][:, i, :]
+        def cast_half(i):
+            if i == 1:
+                f8_joint["shared"] = f8p.tile([P, 2 * HD], FP8, tag="f82", name="f8_%d" % SHARED_CAST)
+            cast_to(f8_joint["shared"][:, i * HD:(i + 1) * HD], res[SHARED_CAST][:, i, :], i == 0)
             if i == 0:
-                nc.scalar.activation(out=f8, in_=src, func=ACT.Copy, scale=Y_SCALE, saturate=False)
-                nc.sync.dma_start(out=dram_view(out_1, j), in_=f8h[0][:].bitcast(U8))
-            else:
-                nc.vector.tensor_scalar(out=f8, in0=src, scalar1=Y_SCALE, scalar2=None, op0=ALU.mult, saturate=False)
+                nc.sync.dma_start(out=hbm_view(out_1, SHARED_CAST), in_=f8_joint["shared"][:].bitcast(U8))
 
-        def tiles(j):
-            a, h0, k = UNITS[j]
-            return [(h0 + i) * NA + a for i in range(k)]
+        def idle_matmuls(count, early):
+            for i in range(count):
+                if early:
+                    dummy = pmx.tile([P, 2 * P], F32, tag="ps%d" % (i % 2), name="dummy")
+                else:
+                    dummy = ptr.tile([P, 2 * P], F32, tag="tr", name="dummy")
+                nc.tensor.matmul(dummy[:], lhsT=zeros[:, 0:P], rhs=zeros[:], start=True, stop=True)
 
-        keep_warm(WARM_HEAD, 2 * P, True)
-        x_t(0, 0)
-        x_t(0, 1)
+        idle_matmuls(2, True)
+        turn_x_words(0, 0)
+        turn_x_words(0, 1)
         vt = ptr.tile([P, P], BF16, tag="tr", name="vt")
         nc.tensor.transpose(vt[:], vrow[:], ident_bf[:])
-        keep_warm(WARM_MID, 2 * P, True)
-        xev(0, 0, "V")
-        xev(0, 1, "S")
+        idle_matmuls(1, True)
+        copy_x_words(0, 0, "V")
+        copy_x_words(0, 1, "S")
         nc.scalar.activation(out=sm["av"][:], in_=vt[:, 2 * NC:3 * NC], func=ACT.Abs)
-        nc.scalar.activation(out=hb[:].rearrange("p i c -> p (i c)"), in_=vt[:, 0:2 * NC], func=ACT.Copy, scale=0.5)
-        nc.scalar.copy(out=vecs[:, 2, :], in_=vt[:, 2 * NC:3 * NC])
-        wintq(0, 1, 0)
-        xqh(0, 0)
-        xqh(0, 1)
-        wintq(0, 1, 1, True)
+        nc.scalar.activation(out=hb[:].rearrange("p i n -> p (i n)"), in_=vt[:, 0:2 * NC], func=ACT.Copy, scale=0.5)
+        nc.scalar.copy(out=a_param_bf[:], in_=vt[:, 2 * NC:3 * NC])
+        interleave_w(0, 1, 0, 1)
+        quantize_x(0, 0, 1)
+        quantize_x(0, 1, 1)
+        interleave_w(0, 1, 1, 1, "S")
         small["w"]()
-        wqq(0, 1, 0)
-        wintq(0, 0, 0)
-        wintq(0, 0, 1, True)
+        quantize_w(0, 1, 0, 1)
+        interleave_w(0, 0, 0, 1)
+        interleave_w(0, 0, 1, 1, "S")
         small["t"]()
-        wqq(0, 1, 1)
-        wqq(0, 0, 0)
-        wqq(0, 0, 1)
-        winth(0, 1, 1)
-        mx(0)
-        mx(1)
-        x_t(1, 0)
-        x_t(1, 1)
+        quantize_w(0, 1, 1, 1)
+        quantize_w(0, 0, 0, 1)
+        quantize_w(0, 0, 1, 1)
+        interleave_w(0, 1, 2, 2)
+        matmuls(0)
+        matmuls(1)
+        turn_x_words(1, 0)
+        turn_x_words(1, 1)
 
-        work = []
-        pend = []
-
-        def pe_part(task):
-            if task[0] == "g":
-                x_t2(task[1], task[2])
-            else:
-                a_t(task[1])
-
-        def dve_part(task):
-            if task[0] == "g":
-                gxx2(task[1], task[2])
-            else:
-                t1(task[1])
-
-        def regime2(rate):
-            for task in pend:
-                dve_part(task)
-            pend.clear()
-            for i in range(rate):
-                if work:
-                    task = work.pop(0)
-                    pe_part(task)
-                    pend.append(task)
-
-        for c in range(H * NT):
+        for c in range(NC):
             h, t = c // NT, c % NT
-            tha(c)
+            tanh_decay(c)
             if c == 0:
                 small["y0"]()
-            thx(c)
+            tanh_x(c)
             if c == 0:
                 small["e1"]()
-            if c == 3:
-                ex(0)
-                ex(1)
-                ex(2)
-            if c > 2:
-                ex(c)
-            hp = c // 2 + 1
+            if c == NT - 1:
+                for earlier in range(c):
+                    exp_decay(earlier)
+            if c >= NT - 1:
+                exp_decay(c)
             if c == 1:
-                xev(1, 0)
-                xev(1, 1)
+                copy_x_words(1, 0, "S")
+                copy_x_words(1, 1, "S")
                 small["e2"]()
             if c == 0:
-                winth(0, 0, 1)
-                wqh(0, 1, 1)
-                wqh(0, 0, 1)
+                interleave_w(0, 0, 2, 2)
+                quantize_w(0, 1, 2, 2)
+                quantize_w(0, 0, 2, 2)
                 small["pa"]()
-                winth(1, 1, 0)
+                interleave_w(1, 1, 0, 2)
                 small["y1"]()
-                winth(1, 1, 1)
+                interleave_w(1, 1, 2, 2)
                 small["qa"]()
             if c == 1:
-                wqh(1, 1, 0)
+                quantize_w(1, 1, 0, 2)
                 small["qb"]()
-                winth(1, 0, 0)
+                interleave_w(1, 0, 0, 2)
                 small["pb"]()
-                wqh(1, 1, 1)
+                quantize_w(1, 1, 2, 2)
                 small["ch"]()
-                winth(1, 0, 1)
-                wqh(1, 0, 0)
-                xq(1)
+                interleave_w(1, 0, 2, 2)
+                quantize_w(1, 0, 0, 2)
+                quantize_x(1)
             if c == 2:
-                wqh(1, 0, 1)
-            if 1 < hp < H and c % 2 == 0:
-                wint(hp, 1)
-                xev(hp, 0)
-                xev(hp, 1)
-                wq(hp, 1)
-            if 1 < hp < H and c % 2 == 1:
-                wint(hp, 0)
-                xq(hp)
-                wq(hp, 0)
-            for j in (1, 0) + tuple(range(2, len(UNITS))):
+                quantize_w(1, 0, 2, 2)
+            prepared = c // 2 + 1
+            if 1 < prepared < H and c % 2 == 0:
+                interleave_w(prepared, 1)
+                copy_x_words(prepared, 0, "V")
+                copy_x_words(prepared, 1, "V")
+                quantize_w(prepared, 1)
+            if 1 < prepared < H and c % 2 == 1:
+                interleave_w(prepared, 0)
+                quantize_x(prepared)
+                quantize_w(prepared, 0)
+            for j in (1, 0) + tuple(range(2, NU)):
                 a, h0, k = UNITS[j]
                 n_pool = min(h0 + k, POOL_HEADS) - h0
                 if n_pool > 0 and c == max(2 * NT, NT * (h0 + n_pool)):
-                    sqr(j, 0, n_pool, True)
-            if c >= R2_FROM:
-                regime2(R2_RATE)
-            if c + 2 < H * NT:
-                mx(c + 2)
-            if hp + 1 < H and c % 2 == 1:
-                x_t(hp + 1, 0)
-                x_t(hp + 1, 1)
+                    square(j, 0, n_pool, True)
+            if c >= PASSES_FROM:
+                passes()
+            if c + 2 < NC:
+                matmuls(c + 2)
+            if prepared + 1 < H and c % 2 == 1:
+                turn_x_words(prepared + 1, 0)
+                turn_x_words(prepared + 1, 1)
             if c == 1:
-                keep_warm(WARM_GAP, 2 * P, False)
-            if c + 2 >= H * NT:
-                keep_warm(1, 2 * P, False)
+                idle_matmuls(2, False)
+            if c + 2 >= NC:
+                idle_matmuls(1, False)
             if t == NT - 1:
-                work.extend([("g", h, 0), ("g", h, 1)] + [("t", h * NA + a) for a in range(NA)])
+                waiting.extend([("x", h, 0), ("x", h, 1)] + [("state", h * NA + a) for a in range(NA)])
 
-        n = len(UNITS)
-        for s in range(n + LAG_CA + 1):
-            if s + 1 < n and UNITS[s + 1][1] + UNITS[s + 1][2] > POOL_HEADS:
-                sqr(s + 1, POOL_HEADS - UNITS[s + 1][1], 1, False)
-            if s < n:
-                sqrt(s)
-            regime2(R2_RATE)
-            if 0 <= s - LAG_T3C < n and (s - LAG_T3C) in T3C_ON_POOL:
-                t3c(s - LAG_T3C)
-            if 0 <= s - LAG_T3V < n and (s - LAG_T3V) not in T3C_ON_POOL:
-                if s - LAG_T3V in T3C_FROM_PSUM:
-                    t3c_psum(s - LAG_T3V)
+        for s in range(NU + LAG_CAST_ACT + 1):
+            if s + 1 < NU and UNITS[s + 1][1] + UNITS[s + 1][2] > POOL_HEADS:
+                square(s + 1, POOL_HEADS - UNITS[s + 1][1], 1, False)
+            if s < NU:
+                root(s)
+            passes()
+            if 0 <= s - LAG_PRODUCT_POOL < NU and (s - LAG_PRODUCT_POOL) in ROOT_PRODUCT_ON_POOL:
+                root_product(s - LAG_PRODUCT_POOL)
+            if 0 <= s - LAG_PRODUCT_DVE < NU and (s - LAG_PRODUCT_DVE) not in ROOT_PRODUCT_ON_POOL:
+                if s - LAG_PRODUCT_DVE in ROOT_PRODUCT_FROM_PSUM:
+                    root_product_from_psum(s - LAG_PRODUCT_DVE)
                 else:
-                    t3c(s - LAG_T3V)
-            if 0 <= s - LAG_ADD < n:
-                for v in tiles(s - LAG_ADD):
-                    add(v)
-                st0(s - LAG_ADD)
-            if s - LAG_CAST == SHARED_CAST:
-                cast_half(SHARED_CAST, 1)
-            if s - LAG_ADD == n - 1:
-                cast(n - 2)
-                cast(n - 1)
-            if 0 <= s - LAG_CA < n and (s - LAG_CA) in CAST_ON_ACT:
-                cast(s - LAG_CA)
-            if s - LAG_CA == SHARED_CAST:
-                cast_half(SHARED_CAST, 0)
-            if 0 <= s - LAG_OT < n:
-                for v in tiles(s - LAG_OT):
-                    o_t(v)
-            if s + 3 - LAG_T3V in T3C_FROM_PSUM:
-                g_copy(s + 3 - LAG_T3V, 0)
-            elif s + 2 - LAG_T3V in T3C_FROM_PSUM:
-                g_copy(s + 2 - LAG_T3V, 1)
-            elif s < n + LAG_OT:
-                keep_warm(1, 2 * P, False)
+                    root_product(s - LAG_PRODUCT_DVE)
+            if 0 <= s - LAG_SUM < NU:
+                for v in tiles_of(s - LAG_SUM):
+                    final_sum(v)
+                store_out_0(s - LAG_SUM)
+            if s - LAG_CAST_DVE == SHARED_CAST:
+                cast_half(1)
+            if s - LAG_SUM == NU - 1:
+                cast(NU - 2)
+                cast(NU - 1)
+            if 0 <= s - LAG_CAST_ACT < NU and (s - LAG_CAST_ACT) in CAST_ON_ACT:
+                cast(s - LAG_CAST_ACT)
+            if s - LAG_CAST_ACT == SHARED_CAST:
+                cast_half(0)
+            if 0 <= s - LAG_BACK < NU:
+                for v in tiles_of(s - LAG_BACK):
+                    turn_product_back(v)
+            if s + 3 - LAG_PRODUCT_DVE in ROOT_PRODUCT_FROM_PSUM:
+                lay_gx_into_psum(s + 3 - LAG_PRODUCT_DVE, 0)
+            elif s + 2 - LAG_PRODUCT_DVE in ROOT_PRODUCT_FROM_PSUM:
+                lay_gx_into_psum(s + 2 - LAG_PRODUCT_DVE, 1)
+            elif s < NU + LAG_BACK:
+                idle_matmuls(1, False)

@@ -47,7 +47,7 @@ def tile_rglru_kernel(tc, x, state, w_in, b_in, w_a, b_a, a_param, out_0, out_1)
     with ExitStack() as ctx:
         const = ctx.enter_context(tc.tile_pool(name="const", bufs=1))
         xin = ctx.enter_context(tc.tile_pool(name="xin", bufs=H))
-        win = ctx.enter_context(tc.tile_pool(name="win", bufs=2 * H))
+        win = ctx.enter_context(tc.tile_pool(name="win", bufs=H // 2))
         wgp = ctx.enter_context(tc.tile_pool(name="wgp", bufs=4))
         keep = ctx.enter_context(tc.tile_pool(name="keep", bufs=1))
         f8p = ctx.enter_context(tc.tile_pool(name="f8p", bufs=6))
@@ -61,6 +61,7 @@ def tile_rglru_kernel(tc, x, state, w_in, b_in, w_a, b_a, a_param, out_0, out_1)
         nc.gpsimd.memset(vrow[:], 0.0)
         warm = const.tile([P, 1], F32, name="warm")
         nc.vector.memset(warm[:], 0.0)
+        hold = const.tile([P, 1], U32, name="hold")
         quarter = const.tile([P, 1], F32, name="quarter")
         nc.vector.memset(quarter[:], 0.25)
         nc.scalar.dma_start(out=vrow[2 * NC:3 * NC, :], in_=a_param.rearrange("(c m) -> c m", m=P))
@@ -86,9 +87,13 @@ def tile_rglru_kernel(tc, x, state, w_in, b_in, w_a, b_a, a_param, out_0, out_1)
             else:
                 nc.sync.dma_start(out=xn[h][:], in_=src)
 
+        raw_pair = [None] * (H // 2)
+
         def load_w(h, g):
-            raw[h][g] = win.tile([P, PACK, HD], BF16, tag="raw", name="raw%d_%d" % (h, g))
-            nc.sync.dma_start(out=raw[h][g][:], in_=w_dram[g][h].rearrange("(p j) n -> p j n", j=PACK))
+            if raw_pair[h // 2] is None:
+                raw_pair[h // 2] = win.tile([P, 4, PACK, HD], BF16, tag="raw", name="raw_pair%d" % (h // 2))
+            raw[h][g] = raw_pair[h // 2][:, 2 * (h % 2) + g, :, :]
+            nc.sync.dma_start(out=raw[h][g], in_=w_dram[g][h].rearrange("(p j) n -> p j n", j=PACK))
 
         def load_state(h):
             st[h] = keep.tile([P, NA, HD], BF16, name="st%d" % h)
@@ -283,19 +288,16 @@ def tile_rglru_kernel(tc, x, state, w_in, b_in, w_a, b_a, a_param, out_0, out_1)
                         turn_decay_back(task[1])
                     turned.append(task)
 
-        def square(j, i0, n, on_pool):
-            a, h0, k = UNITS[j]
-            if j not in sq:
-                if j < 2 * H:
-                    sq[j] = win.tile([P, k * NT, P], F32, tag="raw", name="sq%d" % j)[:]
-                else:
-                    sq[j] = wgp.tile([P, k * NT, P], F32, tag="wg", name="sq%d" % j, align_bytes=64)[:]
-            src = unit_view(decay_pair, j, i0, n)
-            dst = sq[j][:, i0 * NT:(i0 + n) * NT, :]
-            if on_pool:
-                nc.gpsimd.tensor_tensor(out=dst, in0=src, in1=src, op=ALU.mult)
-            else:
-                nc.scalar.activation(out=dst, in_=src, func=ACT.Square)
+        def squares_on_pool(q, heads):
+            sq_pair = win.tile([P, NA, 2 * NT, P], F32, tag="raw", name="sq_pair%d" % q)
+            for j, (a, h0, k) in enumerate(UNITS):
+                if h0 // 2 == q:
+                    sq[j] = sq_pair[:, a, (h0 % 2) * NT:(h0 % 2 + k) * NT, :]
+            src = decay_pair[q][:, 0:heads * NT, :].rearrange("p c (a r) -> p a c r", a=NA)
+            nc.gpsimd.tensor_tensor(out=sq_pair[:, :, 0:heads * NT, :], in0=src, in1=src, op=ALU.mult)
+
+        def square(j, i0, n):
+            nc.scalar.activation(out=sq[j][:, i0 * NT:(i0 + n) * NT, :], in_=unit_view(decay_pair, j, i0, n), func=ACT.Square)
 
         def root(j):
             nc.scalar.activation(out=sq[j], in_=sq[j], func=ACT.Sqrt, bias=quarter[:, 0:1], scale=-0.25)
@@ -453,11 +455,11 @@ def tile_rglru_kernel(tc, x, state, w_in, b_in, w_a, b_a, a_param, out_0, out_1)
                 interleave_w(prepared, 0)
                 quantize_x(prepared)
                 quantize_w(prepared, 0)
-            for j in (1, 0) + tuple(range(2, NU)):
-                a, h0, k = UNITS[j]
-                n_pool = min(h0 + k, POOL_HEADS) - h0
-                if n_pool > 0 and c == max(2 * NT, NT * (h0 + n_pool)):
-                    square(j, 0, n_pool, True)
+            if c == 2 * NT:
+                nc.gpsimd.tensor_copy(out=hold[:], in_=wc[H - 1][0][:, HD - 1:HD])
+                squares_on_pool(0, 2)
+            if c == 3 * NT:
+                squares_on_pool(1, POOL_HEADS - 2)
             if c >= PASSES_FROM:
                 passes()
             if c + 2 < NC:
@@ -474,7 +476,7 @@ def tile_rglru_kernel(tc, x, state, w_in, b_in, w_a, b_a, a_param, out_0, out_1)
 
         for s in range(NU + LAG_CAST_ACT + 1):
             if s + 1 < NU and UNITS[s + 1][1] + UNITS[s + 1][2] > POOL_HEADS:
-                square(s + 1, POOL_HEADS - UNITS[s + 1][1], 1, False)
+                square(s + 1, POOL_HEADS - UNITS[s + 1][1], 1)
             if s < NU:
                 root(s)
             passes()

from contextlib import ExitStack

import concourse.mybir as mybir
from concourse.masks import make_identity

B, H, HD = 512, 4, 512
FLOPS = 2 * 2 * B * H * HD * HD

F32 = mybir.dt.float32
BF16 = mybir.dt.bfloat16
U32 = mybir.dt.uint32
U8 = mybir.dt.uint8
FP8X4 = mybir.dt.float8_e4m3fn_x4
FP8 = mybir.dt.float8_e4m3fn
ACT = mybir.ActivationFunctionType
ALU = mybir.AluOpType

P = 128
PACK = 4
NT = HD // P
NA = B // P
NC = H * NT
Y_SCALE = 280.0

UNITS = ((0, 0, 1), (0, 1, 1), (1, 0, 2), (2, 0, 2), (3, 0, 2), (0, 2, 2), (1, 2, 2), (2, 2, 2), (3, 2, 1), (3, 3, 1))
NU = len(UNITS)
POOL_HEADS = 3
ROOT_PRODUCT_ON_POOL = (0, 1, 2, 4, 5, 7, 8)
ROOT_PRODUCT_FROM_PSUM = (3, 6)
CAST_ON_ACT = (0, 1, 2, 3, 4, 5, 6)
SHARED_CAST = 7
PASSES_FROM = 8
PASSES_A_STEP = 2
LAG_PRODUCT_POOL = 1
LAG_PRODUCT_DVE = 2
LAG_BACK = 2
LAG_SUM = 3
LAG_CAST_DVE = 4
LAG_CAST_ACT = 5
GA, GB = 1.36, 0.71


def tile_rglru_kernel(tc, x, state, w_in, b_in, w_a, b_a, a_param, out_0, out_1):
    nc = tc.nc
    w_dram = (w_in, w_a)

    with ExitStack() as ctx:
        const = ctx.enter_context(tc.tile_pool(name="const", bufs=1))
        xin = ctx.enter_context(tc.tile_pool(name="xin", bufs=H))
        win = ctx.enter_context(tc.tile_pool(name="win", bufs=H // 2))
        wgp = ctx.enter_context(tc.tile_pool(name="wgp", bufs=4))
        keep = ctx.enter_context(tc.tile_pool(name="keep", bufs=1))
        f8p = ctx.enter_context(tc.tile_pool(name="f8p", bufs=6))
        pmx = ctx.enter_context(tc.psum_pool(name="pmx", bufs=2))
        ptr = ctx.enter_context(tc.psum_pool(name="ptr", bufs=4))
        ctx.enter_context(tc.manual_schedule())

        zeros = const.tile([P, 2 * P], F32, name="zeros")
        nc.gpsimd.memset(zeros[:], 0.0)
        vrow = const.tile([P, P], BF16, name="vrow")
        nc.gpsimd.memset(vrow[:], 0.0)
        warm = const.tile([P, 1], F32, name="warm")
        nc.vector.memset(warm[:], 0.0)
        hold = const.tile([P, 1], U32, name="hold")
        quarter = const.tile([P, 1], F32, name="quarter")
        nc.vector.memset(quarter[:], 0.25)
        nc.scalar.dma_start(out=vrow[2 * NC:3 * NC, :], in_=a_param.rearrange("(c m) -> c m", m=P))
        nc.scalar.dma_start(out=vrow[0:NC, :], in_=b_in.rearrange("h (t m) -> (h t) m", m=P))
        nc.scalar.dma_start(out=vrow[NC:2 * NC, :], in_=b_a.rearrange("h (t m) -> (h t) m", m=P))
        warm_out = const.tile([P, 1], F32, name="warm_out")
        nc.scalar.activation(out=warm_out[:], in_=warm[:], func=ACT.Exp)
        ident = const.tile([P, P], F32, name="ident")
        make_identity(nc, ident[:])
        ident_bf = const.tile([P, P], BF16, name="ident_bf")
        make_identity(nc, ident_bf[:])

        xn = [None] * H
        raw = [[None, None] for h in range(H)]
        st = [None] * H

        def load_x(h):
            xn[h] = xin.tile([P, NA, HD], BF16, tag="xn", name="xn%d" % h)
            src = x[:, h * HD:(h + 1) * HD].rearrange("(a p) k -> p a k", p=P)
            if h == 0:
                for a in range(NA):
                    nc.sync.dma_start(out=xn[h][:, a, :], in_=src[:, a, :])
            else:
                nc.sync.dma_start(out=xn[h][:], in_=src)

        raw_pair = [None] * (H // 2)

        def load_w(h, g):
            if raw_pair[h // 2] is None:
                raw_pair[h // 2] = win.tile([P, 4, PACK, HD], BF16, tag="raw", name="raw_pair%d" % (h // 2))
            raw[h][g] = raw_pair[h // 2][:, 2 * (h % 2) + g, :, :]
            nc.sync.dma_start(out=raw[h][g], in_=w_dram[g][h].rearrange("(p j) n -> p j n", j=PACK))

        def load_state(h):
            st[h] = keep.tile([P, NA, HD], BF16, name="st%d" % h)
            nc.sync.dma_start(out=st[h][:], in_=state[:, h * HD:(h + 1) * HD].rearrange("(a p) k -> p a k", p=P))

        for h in range(H):
            load_x(h)
            load_w(h, 1)
            load_w(h, 0)
        for h in range(H):
            load_state(h)

        a_param_bf = const.tile([P, NC], BF16, name="a_param_bf")
        hb = const.tile([P, 2, NC], F32, name="hb")
        ch = const.tile([P, NC], F32, name="ch")
        sm = {}
        for nm in ("av", "w", "t", "y0", "e1", "pa", "y1", "e2", "pb", "qa", "qb"):
            sm[nm] = const.tile([P, NC], F32, name="sm_" + nm)

        def stt(out, in0, scalar, in1, op0, op1):
            nc.vector.scalar_tensor_tensor(out=out, in0=in0, scalar=scalar, in1=in1, op0=op0, op1=op1)

        def small_exp(out, in_, scale):
            nc.scalar.activation(out=sm[out][:], in_=sm[in_][:], func=ACT.Exp, scale=scale)

        small = {
            "w": lambda: small_exp("w", "av", -1.0),
            "t": lambda: small_exp("t", "w", -GB),
            "y0": lambda: nc.scalar.activation(out=sm["y0"][:], in_=sm["t"][:], func=ACT.Copy, scale=-GA, bias=GA),
            "e1": lambda: small_exp("e1", "y0", -1.0),
            "pa": lambda: stt(sm["pa"][:], sm["w"][:], 1.0, sm["e1"][:], ALU.add, ALU.mult),
            "y1": lambda: stt(sm["y1"][:], sm["pa"][:], -1.0, sm["y0"][:], ALU.add, ALU.add),
            "e2": lambda: small_exp("e2", "y1", -1.0),
            "qa": lambda: stt(sm["qa"][:], a_param_bf[:], 0.0, sm["y1"][:], ALU.max, ALU.add),
            "qb": lambda: nc.vector.tensor_scalar(
                out=sm["qb"][:], in0=sm["qa"][:], scalar1=-1.0, scalar2=-4.0, op0=ALU.add, op1=ALU.mult),
            "pb": lambda: stt(sm["pb"][:], sm["w"][:], 1.0, sm["e2"][:], ALU.add, ALU.mult),
            "ch": lambda: stt(ch[:], sm["pb"][:], -4.0, sm["qb"][:], ALU.mult, ALU.add),
        }

        xg = [keep.tile([P, PACK * B], BF16, name="xg%d" % h, align_bytes=64) for h in range(H)]
        xc = [keep.tile([P, B], U32, name="xc%d" % h, align_bytes=64) for h in range(H)]
        xs = [keep.tile([P, B], U8, name="xs%d" % h, align_bytes=64) for h in range(H)]
        wc = [[keep.tile([P, HD], U32, name="wc%d_%d" % (h, g), align_bytes=64) for g in range(2)] for h in range(H)]
        ws = [[keep.tile([P, HD], U8, name="ws%d_%d" % (h, g), align_bytes=64) for g in range(2)] for h in range(H)]
        gx_pair = [keep.tile([P, 2 * NT, B], F32, name="gx_pair%d" % q) for q in range(H // 2)]
        decay_pair = [keep.tile([P, 2 * NT, B], F32, name="decay_pair%d" % q) for q in range(H // 2)]
        gx = [gx_pair[h // 2][:, (h % 2) * NT:(h % 2 + 1) * NT, :] for h in range(H)]
        decay = [decay_pair[h // 2][:, (h % 2) * NT:(h % 2 + 1) * NT, :] for h in range(H)]
        res = [keep.tile([P, k, HD], F32, name="res%d" % j)[:] for j, (a, h0, k) in enumerate(UNITS[:-2])]
        res_last = keep.tile([P, 2, HD], F32, name="res_last")
        res.extend([res_last[:, 0:1, :], res_last[:, 1:2, :]])
        unit_of = {}
        for j, (a, h0, k) in enumerate(UNITS):
            for i in range(k):
                unit_of[(h0 + i) * NA + a] = (j, i)

        def tiles_of(j):
            a, h0, k = UNITS[j]
            return [(h0 + i) * NA + a for i in range(k)]

        def unit_view(pairs, j, i0, n):
            a, h0, k = UNITS[j]
            r0 = (h0 % 2 + i0) * NT
            return pairs[h0 // 2][:, r0:r0 + n * NT, a * P:(a + 1) * P]

        def hbm_view(out, j):
            a, h0, k = UNITS[j]
            return out[a * P:(a + 1) * P, h0 * HD:(h0 + k) * HD]

        x_words = {}
        wg = {}
        sums = {}
        x_cols = {}
        decay_back = {}
        sq = {}
        gx_psum = {}
        prod_back = {}

        def turn_x_words(h, half):
            xt = ptr.tile([P, 2, 2, P], F32, tag="tr", name="xt%d_%d" % (h, half))
            x_words[(h, half)] = xt
            for a in range(2):
                words = xn[h][:, 2 * half + a, :].bitcast(F32)
                for u in range(2):
                    nc.tensor.transpose(xt[:, a, u, :], words[:, u:HD // 2:2], ident[:])

        def copy_x_words(h, half, engine):
            dst = xg[h][:].bitcast(F32).rearrange("p (a r u) -> p a r u", a=NA, u=2)[:, 2 * half:2 * half + 2, :, :]
            src = x_words[(h, half)][:].rearrange("p a u r -> p a r u")
            if engine == "V":
                nc.vector.tensor_copy(out=dst, in_=src)
            else:
                nc.scalar.copy(out=dst, in_=src)

        def quantize_x(h, first=0, halves=2):
            tok = slice(first * (B // 2), (first + halves) * (B // 2))
            nc.vector.quantize_mx(
                out=xc[h][:, tok].bitcast(FP8X4), scales=xs[h][:, tok],
                in_=xg[h][:, first * (B // 2) * PACK:(first + halves) * (B // 2) * PACK],
            )

        def interleave_w(h, g, first=0, quarters=NT, engine="V"):
            if (h, g) not in wg:
                wg[(h, g)] = wgp.tile([P, PACK * HD], BF16, tag="wg", name="wg%d_%d" % (h, g), align_bytes=64)
            dst = wg[(h, g)][:, first * HD:(first + quarters) * HD].rearrange("p (q i j) -> p q j i", i=4, j=PACK)
            src = raw[h][g][:, :, first * P:(first + quarters) * P].rearrange("p j (q i) -> p q j i", i=4)
            if engine == "V":
                nc.vector.tensor_copy(out=dst, in_=src)
            else:
                nc.scalar.copy(out=dst, in_=src)

        def quantize_w(h, g, first=0, quarters=NT):
            cols = slice(first * P, (first + quarters) * P)
            nc.vector.quantize_mx(
                out=wc[h][g][:, cols].bitcast(FP8X4), scales=ws[h][g][:, cols],
                in_=wg[(h, g)][:, first * HD:(first + quarters) * HD],
            )

        def matmuls(c):
            h, t = c // NT, c % NT
            cols = slice(t * P, (t + 1) * P)
            banks = [None, None]
            for g in (1, 0):
                ps = pmx.tile([P, B], F32, tag="ps%d" % g, name="ps%d_%d" % (g, c))
                nc.tensor.matmul_mx(
                    out=ps[:],
                    lhsT=wc[h][g][:, cols].bitcast(FP8X4),
                    lhsT_scale=ws[h][g][:, cols],
                    rhs=xc[h][:].bitcast(FP8X4),
                    rhs_scale=xs[h][:],
                    start=True,
                    stop=True,
                )
                banks[g] = ps
            sums[c] = banks

        def tanh_x(c):
            h, t = c // NT, c % NT
            nc.scalar.activation(out=gx[h][:, t, :], in_=sums[c][0][:], func=ACT.Tanh, bias=hb[:, 0, c:c + 1], scale=0.5)

        def tanh_decay(c):
            h, t = c // NT, c % NT
            nc.scalar.activation(out=decay[h][:, t, :], in_=sums[c][1][:], func=ACT.Tanh, bias=hb[:, 1, c:c + 1], scale=0.5)

        def exp_decay(c):
            h, t = c // NT, c % NT
            nc.scalar.activation(out=decay[h][:, t, :], in_=decay[h][:, t, :], func=ACT.Exp, bias=ch[:, c:c + 1], scale=ch[:, c:c + 1])

        def turn_x_cols(h, two):
            xu = ptr.tile([P, 2, B], BF16, tag="tr", name="xu%d_%d" % (h, two))
            x_cols[(h, two)] = xu
            for e in range(2):
                t = 2 * two + e
                for a in range(NA):
                    nc.tensor.transpose(xu[:, e, a * P:(a + 1) * P], xn[h][:, a, t * P:(t + 1) * P], ident_bf[:])

        def times_x(h, two):
            th = gx[h][:, 2 * two:2 * two + 2, :]
            nc.vector.scalar_tensor_tensor(out=th, in0=th, scalar=1.0, in1=x_cols[(h, two)][:], op0=ALU.add, op1=ALU.mult)

        def turn_decay_back(v):
            h, a = v // NA, v % NA
            tr = ptr.tile([P, NT, P], F32, tag="tr", name="at%d" % v)
            decay_back[v] = tr
            for t in range(NT):
                nc.tensor.transpose(tr[:, t, :], decay[h][:, t, a * P:(a + 1) * P], ident[:])

        def times_state(v):
            h, a = v // NA, v % NA
            j, i = unit_of[v]
            nc.vector.tensor_tensor(
                out=res[j][:, i, :], in0=decay_back[v][:].rearrange("p t m -> p (t m)"), in1=st[h][:, a, :], op=ALU.mult
            )

        waiting = []
        turned = []

        def passes():
            for task in turned:
                if task[0] == "x":
                    times_x(task[1], task[2])
                else:
                    times_state(task[1])
            turned.clear()
            for i in range(PASSES_A_STEP):
                if waiting:
                    task = waiting.pop(0)
                    if task[0] == "x":
                        turn_x_cols(task[1], task[2])
                    else:
                        turn_decay_back(task[1])
                    turned.append(task)

        def squares_on_pool(q, heads):
            sq_pair = win.tile([P, NA, 2 * NT, P], F32, tag="raw", name="sq_pair%d" % q)
            for j, (a, h0, k) in enumerate(UNITS):
                if h0 // 2 == q:
                    sq[j] = sq_pair[:, a, (h0 % 2) * NT:(h0 % 2 + k) * NT, :]
            src = decay_pair[q][:, 0:heads * NT, :].rearrange("p c (a r) -> p a c r", a=NA)
            nc.gpsimd.tensor_tensor(out=sq_pair[:, :, 0:heads * NT, :], in0=src, in1=src, op=ALU.mult)

        def square(j, i0, n):
            nc.scalar.activation(out=sq[j][:, i0 * NT:(i0 + n) * NT, :], in_=unit_view(decay_pair, j, i0, n), func=ACT.Square)

        def root(j):
            nc.scalar.activation(out=sq[j], in_=sq[j], func=ACT.Sqrt, bias=quarter[:, 0:1], scale=-0.25)

        def root_product(j):
            a, h0, k = UNITS[j]
            eng = nc.gpsimd if j in ROOT_PRODUCT_ON_POOL else nc.vector
            eng.tensor_tensor(out=sq[j], in0=unit_view(gx_pair, j, 0, k), in1=sq[j], op=ALU.mult)

        def lay_gx_into_psum(j, i):
            gp = ptr.tile([P, NT, P], F32, tag="tr", name="gp%d_%d" % (j, i))
            gx_psum[(j, i)] = gp
            src = unit_view(gx_pair, j, i, 1)
            for e in range(2):
                nc.tensor.matmul(
                    gp[:, 2 * e:2 * e + 2, :], lhsT=ident[:], rhs=src[:, 2 * e:2 * e + 2, :], start=True, stop=True
                )

        def root_product_from_psum(j):
            for i in range(2):
                r = sq[j][:, i * NT:(i + 1) * NT, :]
                nc.vector.tensor_tensor(out=r, in0=gx_psum[(j, i)][:], in1=r, op=ALU.mult)

        def turn_product_back(v):
            j, i = unit_of[v]
            tr = pmx.tile([P, NT, P], F32, tag="ps%d" % (v % 2), name="ot%d" % v)
            prod_back[v] = tr
            for t in range(NT):
                nc.tensor.transpose(tr[:, t, :], sq[j][:, i * NT + t, :], ident[:])

        def final_sum(v):
            j, i = unit_of[v]
            nc.vector.tensor_tensor(
                out=res[j][:, i, :], in0=prod_back[v][:].rearrange("p t m -> p (t m)"), in1=res[j][:, i, :], op=ALU.add
            )

        def store_out_0(j):
            if j < NU - 2:
                nc.sync.dma_start(out=hbm_view(out_0, j), in_=res[j].rearrange("p i n -> p (i n)"))
            elif j == NU - 1:
                nc.sync.dma_start(out=out_0[(NA - 1) * P:NA * P, (H - 2) * HD:H * HD], in_=res_last[:].rearrange("p i n -> p (i n)"))

        def cast_to(f8, src, on_act):
            if on_act:
                nc.scalar.activation(out=f8, in_=src, func=ACT.Copy, scale=Y_SCALE, saturate=False)
            else:
                nc.vector.tensor_scalar(out=f8, in0=src, scalar1=Y_SCALE, scalar2=None, op0=ALU.mult, saturate=False)

        f8_joint = {}

        def cast(j):
            a, h0, k = UNITS[j]
            src = res[j].rearrange("p i n -> p (i n)")
            if j < NU - 2:
                f8 = f8p.tile([P, k * HD], FP8, tag="f8%d" % k, name="f8_%d" % j)
                cast_to(f8[:], src, j in CAST_ON_ACT)
                nc.sync.dma_start(out=hbm_view(out_1, j), in_=f8[:].bitcast(U8))
            else:
                if j == NU - 2:
                    f8_joint["last"] = f8p.tile([P, 2 * HD], FP8, tag="f82", name="f8_last")
                i = j - (NU - 2)
                cast_to(f8_joint["last"][:, i * HD:(i + 1) * HD], src, False)
                if j == NU - 1:
                    nc.sync.dma_start(out=out_1[(NA - 1) * P:NA * P, (H - 2) * HD:H * HD], in_=f8_joint["last"][:].bitcast(U8))

        def cast_half(i):
            if i == 1:
                f8_joint["shared"] = f8p.tile([P, 2 * HD], FP8, tag="f82", name="f8_%d" % SHARED_CAST)
            cast_to(f8_joint["shared"][:, i * HD:(i + 1) * HD], res[SHARED_CAST][:, i, :], i == 0)
            if i == 0:
                nc.sync.dma_start(out=hbm_view(out_1, SHARED_CAST), in_=f8_joint["shared"][:].bitcast(U8))

        def idle_matmuls(count, early):
            for i in range(count):
                if early:
                    dummy = pmx.tile([P, 2 * P], F32, tag="ps%d" % (i % 2), name="dummy")
                else:
                    dummy = ptr.tile([P, 2 * P], F32, tag="tr", name="dummy")
                nc.tensor.matmul(dummy[:], lhsT=zeros[:, 0:P], rhs=zeros[:], start=True, stop=True)

        idle_matmuls(2, True)
        turn_x_words(0, 0)
        turn_x_words(0, 1)
        vt = ptr.tile([P, P], BF16, tag="tr", name="vt")
        nc.tensor.transpose(vt[:], vrow[:], ident_bf[:])
        idle_matmuls(1, True)
        copy_x_words(0, 0, "V")
        copy_x_words(0, 1, "S")
        nc.scalar.activation(out=sm["av"][:], in_=vt[:, 2 * NC:3 * NC], func=ACT.Abs)
        nc.scalar.activation(out=hb[:].rearrange("p i n -> p (i n)"), in_=vt[:, 0:2 * NC], func=ACT.Copy, scale=0.5)
        nc.scalar.copy(out=a_param_bf[:], in_=vt[:, 2 * NC:3 * NC])
        interleave_w(0, 1, 0, 1)
        quantize_x(0, 0, 1)
        quantize_x(0, 1, 1)
        interleave_w(0, 1, 1, 1, "S")
        small["w"]()
        quantize_w(0, 1, 0, 1)
        interleave_w(0, 0, 0, 1)
        interleave_w(0, 0, 1, 1, "S")
        small["t"]()
        quantize_w(0, 1, 1, 1)
        quantize_w(0, 0, 0, 1)
        quantize_w(0, 0, 1, 1)
        interleave_w(0, 1, 2, 2)
        matmuls(0)
        matmuls(1)
        turn_x_words(1, 0)
        turn_x_words(1, 1)

        for c in range(NC):
            h, t = c // NT, c % NT
            tanh_decay(c)
            if c == 0:
                small["y0"]()
            tanh_x(c)
            if c == 0:
                small["e1"]()
            if c == NT - 1:
                for earlier in range(c):
                    exp_decay(earlier)
            if c >= NT - 1:
                exp_decay(c)
            if c == 1:
                copy_x_words(1, 0, "S")
                copy_x_words(1, 1, "S")
                small["e2"]()
            if c == 0:
                interleave_w(0, 0, 2, 2)
                quantize_w(0, 1, 2, 2)
                quantize_w(0, 0, 2, 2)
                small["pa"]()
                interleave_w(1, 1, 0, 2)
                small["y1"]()
                interleave_w(1, 1, 2, 2)
                small["qa"]()
            if c == 1:
                quantize_w(1, 1, 0, 2)
                small["qb"]()
                interleave_w(1, 0, 0, 2)
                small["pb"]()
                quantize_w(1, 1, 2, 2)
                small["ch"]()
                interleave_w(1, 0, 2, 2)
                quantize_w(1, 0, 0, 2)
                quantize_x(1)
            if c == 2:
                quantize_w(1, 0, 2, 2)
            prepared = c // 2 + 1
            if 1 < prepared < H and c % 2 == 0:
                interleave_w(prepared, 1)
                copy_x_words(prepared, 0, "V")
                copy_x_words(prepared, 1, "V")
                quantize_w(prepared, 1)
            if 1 < prepared < H and c % 2 == 1:
                interleave_w(prepared, 0)
                quantize_x(prepared)
                quantize_w(prepared, 0)
            if c == 2 * NT:
                nc.gpsimd.tensor_copy(out=hold[:], in_=wc[H - 1][0][:, HD - 1:HD])
                squares_on_pool(0, 2)
            if c == 3 * NT:
                squares_on_pool(1, POOL_HEADS - 2)
            if c >= PASSES_FROM:
                passes()
            if c + 2 < NC:
                matmuls(c + 2)
            if prepared + 1 < H and c % 2 == 1:
                turn_x_words(prepared + 1, 0)
                turn_x_words(prepared + 1, 1)
            if c == 1:
                idle_matmuls(2, False)
            if c + 2 >= NC:
                idle_matmuls(1, False)
            if t == NT - 1:
                waiting.extend([("x", h, 0), ("x", h, 1)] + [("state", h * NA + a) for a in range(NA)])

        for s in range(NU + LAG_CAST_ACT + 1):
            if s + 1 < NU and UNITS[s + 1][1] + UNITS[s + 1][2] > POOL_HEADS:
                square(s + 1, POOL_HEADS - UNITS[s + 1][1], 1)
            if s < NU:
                root(s)
            passes()
            if 0 <= s - LAG_PRODUCT_POOL < NU and (s - LAG_PRODUCT_POOL) in ROOT_PRODUCT_ON_POOL:
                root_product(s - LAG_PRODUCT_POOL)
            if 0 <= s - LAG_PRODUCT_DVE < NU and (s - LAG_PRODUCT_DVE) not in ROOT_PRODUCT_ON_POOL:
                if s - LAG_PRODUCT_DVE in ROOT_PRODUCT_FROM_PSUM:
                    root_product_from_psum(s - LAG_PRODUCT_DVE)
                else:
                    root_product(s - LAG_PRODUCT_DVE)
            if 0 <= s - LAG_SUM < NU:
                for v in tiles_of(s - LAG_SUM):
                    final_sum(v)
                store_out_0(s - LAG_SUM)
            if s - LAG_CAST_DVE == SHARED_CAST:
                cast_half(1)
            if s - LAG_SUM == NU - 1:
                cast(NU - 2)
                cast(NU - 1)
            if 0 <= s - LAG_CAST_ACT < NU and (s - LAG_CAST_ACT) in CAST_ON_ACT:
                cast(s - LAG_CAST_ACT)
            if s - LAG_CAST_ACT == SHARED_CAST:
                cast_half(0)
            if 0 <= s - LAG_BACK < NU:
                for v in tiles_of(s - LAG_BACK):
                    turn_product_back(v)
            if s + 3 - LAG_PRODUCT_DVE in ROOT_PRODUCT_FROM_PSUM:
                lay_gx_into_psum(s + 3 - LAG_PRODUCT_DVE, 0)
            elif s + 2 - LAG_PRODUCT_DVE in ROOT_PRODUCT_FROM_PSUM:
                lay_gx_into_psum(s + 2 - LAG_PRODUCT_DVE, 1)
            elif s < NU + LAG_BACK:
                idle_matmuls(1, False)
